import numpy as np
import ml_dtypes


def mxq(x, axis, fmt="e4m3"):
    dtype, down = {"e4m3": (ml_dtypes.float8_e4m3fn, 7), "e5m2": (ml_dtypes.float8_e5m2, 14)}[fmt]
    v = np.moveaxis(np.asarray(x, np.float32).astype(ml_dtypes.bfloat16).astype(np.float64), axis, -1)
    blocks = v.reshape(v.shape[:-1] + (-1, 32))
    amax = np.abs(blocks).max(-1, keepdims=True)
    byte = np.maximum(np.where(amax > 0, np.frexp(amax)[1] - 1 + 127, 0) - down, 1)
    scale = np.exp2(byte - 127.0)
    codes = (blocks / scale).astype(np.float32).astype(dtype).astype(np.float64)
    return np.moveaxis((codes * scale).reshape(v.shape), -1, axis)


WIDE = False


def mx_kscale(k):
    if not WIDE:
        return np.ones(k)
    levels = np.array([10, -10, 5, -5, 0])
    a = np.random.permutation(np.resize(levels, k // 512 * 4)).reshape(k // 512, 4)
    idx = np.arange(k)
    return np.exp2(a[idx // 512, idx % 128 // 32])


BF16 = ml_dtypes.bfloat16


def bf(x):
    return np.asarray(x, np.float32).astype(BF16)


def f64(x):
    return np.asarray(x).astype(np.float64)


T, IN, OUT, BLOCK, R, C = 1024, 1024, 1024, 60, 8, 2
EPS = 1e-12
SIG = 2.5


def row_entropy(logits):
    sh = logits - logits.max(-1, keepdims=True)
    e = np.exp(sh)
    z = e.sum(-1, keepdims=True)
    return -((e / z) * (sh - np.log(z))).sum(-1) / np.log(logits.shape[0])


def block_keep():
    ids = np.arange(T) // BLOCK
    return np.where(ids[:, None] == ids[None, :], 1.0, 0.0)


def setup_inputs():
    s = mx_kscale(OUT)
    g = np.random.standard_normal((T, R)) / np.sqrt(R)
    p = np.random.standard_normal((R, IN))
    x = g @ p + np.random.standard_normal((T, IN))
    a = np.sqrt(SIG / np.sqrt(OUT))
    return {"x": bf(x),
            "q": bf(np.random.standard_normal((T, OUT)) * a * s),
            "k": bf(np.random.standard_normal((T, OUT)) * a / s)}


def reference(x, q, k):
    x, q, k = f64(x), f64(q), f64(k)
    x_unit = x / np.maximum(np.sqrt((x * x).sum(1, keepdims=True)), EPS)
    xq = mxq(x_unit, 1, "e4m3")
    diversity = 1.0 - (xq @ xq.T)
    energies = mxq(q, 1, "e4m3") @ mxq(k, 1, "e4m3").T
    e = np.exp(energies - energies.max(-1, keepdims=True))
    att = e / e.sum(-1, keepdims=True)
    entropy = row_entropy(energies)
    entropy = entropy / np.maximum(np.abs(entropy).sum(), EPS)
    keep = block_keep()
    zero = 1.0 - keep
    entropy_win = row_entropy(energies * keep)
    attn_rem = att * zero
    div_rem = diversity * zero
    dep_factor = (div_rem * attn_rem).sum(-1) / div_rem.sum(-1)
    att_win = att * keep + dep_factor[None, :] * keep
    div_h = np.prod(1.0 - att, axis=1)
    div = div_h / np.abs(div_h).sum()
    return att_win, entropy_win, div, entropy, dep_factor

@@ -1,0 +1,402 @@
+from contextlib import ExitStack
+
+import concourse.mybir as mybir
+from concourse.masks import make_identity
+
+F32 = mybir.dt.float32
+BF16 = mybir.dt.bfloat16
+U32 = mybir.dt.uint32
+U8 = mybir.dt.uint8
+FP8X4 = mybir.dt.float8_e4m3fn_x4
+ACT = mybir.ActivationFunctionType
+ALU = mybir.AluOpType
+AX = mybir.AxisListType
+
+P = 128
+T = 1024
+FEAT = 1024
+NT = T // P
+K_PASS = 4 * P
+PASSES = FEAT // K_PASS
+BANK = 512
+HALVES = T // BANK
+BLOCK = 60
+EPS = 1e-12
+LN_T = 10 * 0.6931471805599453
+
+WIN_STEP = 2 * BLOCK
+WIN = T - WIN_STEP * (NT - 1)
+WIN_BLOCKS = 4
+ROW_SHIFT = P - WIN_STEP
+
+LOAD_TILES = 2
+
+FLOPS = 2 * 2 * T * T * FEAT
+
+COL_ENT_WIN, COL_DIV, COL_ENT, COL_DEP = 0, NT, 2 * NT, 3 * NT
+
+
+def window_pieces(r):
+    lo = WIN_STEP * r
+    pieces = []
+    for h in range(HALVES):
+        first = max(lo, BANK * h)
+        last = min(lo + WIN, BANK * (h + 1))
+        if first < last:
+            pieces.append((h, first - BANK * h, last - BANK * h, first - lo, last - lo))
+    return pieces
+
+
+def tile_selfattention_pa_kernel(tc, x, q, k, out_0, out_1, out_2, out_3, out_4):
+    nc = tc.nc
+    with ExitStack() as ctx:
+        const = ctx.enter_context(tc.tile_pool(name="const", bufs=1))
+        resident = ctx.enter_context(tc.tile_pool(name="resident", bufs=1))
+        stats = ctx.enter_context(tc.tile_pool(name="stats", bufs=1))
+        stage = ctx.enter_context(tc.tile_pool(name="stage", bufs=3))
+        junk = ctx.enter_context(tc.tile_pool(name="junk", bufs=3))
+        psum_t = ctx.enter_context(tc.psum_pool(name="psum_t", bufs=2))
+        psum_mm = ctx.enter_context(tc.psum_pool(name="psum_mm", bufs=3))
+
+        k_sb = resident.tile([P, NT, FEAT], BF16)
+        q_sb = resident.tile([P, NT, FEAT], BF16)
+        x_sb = resident.tile([P, NT, FEAT], BF16)
+        for dst, src in ((k_sb, k), (q_sb, q), (x_sb, x)):
+            view = src.rearrange("(r p) f -> p r f", p=P)
+            for first in range(0, NT, LOAD_TILES):
+                tiles = slice(first, first + LOAD_TILES)
+                nc.sync.dma_start(out=dst[:, tiles, :], in_=view[:, tiles, :])
+
+        ident_f32 = const.tile([P, P], F32)
+        make_identity(nc, ident_f32[:])
+        ident_bf16 = const.tile([P, P], BF16)
+        make_identity(nc, ident_bf16[:])
+        ones = const.tile([P, P], F32)
+        nc.vector.memset(ones[:], 1.0)
+        zeros = const.tile([P, T - WIN], F32)
+        nc.vector.memset(zeros[:], 0.0)
+
+        keep4 = const.tile([P, NT, WIN_BLOCKS, BLOCK], F32)
+        nc.gpsimd.memset(keep4[:], 1.0)
+        nc.gpsimd.affine_select(
+            out=keep4[:], in_=keep4[:], compare_op=ALU.is_ge, fill=0.0,
+            base=0, channel_multiplier=1,
+            pattern=[[ROW_SHIFT, NT], [-BLOCK, WIN_BLOCKS], [0, BLOCK]],
+        )
+        nc.gpsimd.affine_select(
+            out=keep4[:], in_=keep4[:], compare_op=ALU.is_ge, fill=0.0,
+            base=BLOCK - 1, channel_multiplier=-1,
+            pattern=[[-ROW_SHIFT, NT], [BLOCK, WIN_BLOCKS], [0, BLOCK]],
+        )
+        keep = keep4[:].rearrange("p r b c -> p r (b c)")
+
+        for r in range(NT):
+            rows = slice(P * r, P * (r + 1))
+            lo = WIN_STEP * r
+            if lo > 0:
+                nc.sync.dma_start(out=out_0[rows, 0:lo], in_=zeros[:, 0:lo])
+            if lo + WIN < T:
+                nc.sync.dma_start(out=out_0[rows, lo + WIN : T], in_=zeros[:, 0 : T - WIN - lo])
+
+        k_codes = resident.tile([P, PASSES, T], U32, align_bytes=64)
+        k_scales = resident.tile([P, PASSES, T], U8, align_bytes=64)
+        q_codes = resident.tile([P, PASSES, T], U32, align_bytes=64)
+        q_scales = resident.tile([P, PASSES, T], U8, align_bytes=64)
+        u_codes = resident.tile([P, PASSES, T], U32, align_bytes=64)
+        u_scales = resident.tile([P, PASSES, T], U8, align_bytes=64)
+
+        def quantise_tile(grouped, codes, scales, r):
+            cols = slice(P * r, P * (r + 1))
+            for g in range(PASSES):
+                nc.vector.quantize_mx(
+                    out=codes[:, g, cols].bitcast(FP8X4),
+                    scales=scales[:, g, cols],
+                    in_=grouped[:, g, :],
+                )
+
+        def prepare_input_tile(src_sb, codes, scales, r, copy):
+            words = src_sb[:].bitcast(F32)
+            planes = psum_t.tile([P, 2 * PASSES, P], F32, tag="t")
+            for w in range(2 * PASSES):
+                nc.tensor.transpose(planes[:, w, :], words[:, r, P * w : P * (w + 1)], ident_f32[:])
+            grouped = stage.tile([P, PASSES, K_PASS], BF16, align_bytes=64, tag="grouped")
+            copy(
+                out=grouped[:].bitcast(F32).rearrange("p g (c v) -> p g c v", v=2),
+                in_=planes[:].rearrange("p (g v) c -> p g c v", v=2),
+            )
+            quantise_tile(grouped, codes, scales, r)
+
+        for r in range(NT):
+            copy = nc.vector.tensor_copy if r % 2 == 0 else nc.scalar.copy
+            prepare_input_tile(k_sb, k_codes, k_scales, r, copy)
+
+        sum_sq = stats.tile([P, NT], F32)
+        norm = stats.tile([P, NT], F32)
+        inv_norm = stats.tile([P, NT], F32)
+        u_sb = resident.tile([P, NT, FEAT], BF16)
+
+        def sum_squares(r):
+            squares = junk.tile([P, FEAT], BF16, tag="squares")
+            nc.scalar.activation(
+                out=squares[:], in_=x_sb[:, r, :], func=ACT.Square, accum_out=sum_sq[:, r : r + 1]
+            )
+
+        def inverse_norms():
+            nc.scalar.activation(out=norm[:], in_=sum_sq[:], func=ACT.Sqrt)
+            nc.vector.tensor_scalar_max(out=inv_norm[:], in0=norm[:], scalar1=EPS)
+            nc.vector.reciprocal(out=inv_norm[:], in_=inv_norm[:])
+
+        def prepare_u_tile(r):
+            nc.vector.tensor_scalar_mul(
+                out=u_sb[:, r, :], in0=x_sb[:, r, :], scalar1=inv_norm[:, r : r + 1]
+            )
+            planes = psum_t.tile([P, 4 * PASSES, P], BF16, tag="t")
+            for j in range(4 * PASSES):
+                nc.tensor.transpose(planes[:, j, :], u_sb[:, r, P * j : P * (j + 1)], ident_bf16[:])
+            grouped = stage.tile([P, PASSES, K_PASS], BF16, align_bytes=64, tag="grouped")
+            nc.scalar.copy(
+                out=grouped[:].rearrange("p g (c t) -> p g c t", t=4),
+                in_=planes[:].rearrange("p (g t) c -> p g c t", t=4),
+            )
+            quantise_tile(grouped, u_codes, u_scales, r)
+
+        def product_tile(a_codes, a_scales, b_codes, b_scales, r):
+            rows = slice(P * r, P * (r + 1))
+            banks = []
+            for h in range(HALVES):
+                cols = slice(BANK * h, BANK * (h + 1))
+                bank = psum_mm.tile([P, BANK], F32, name="bank%d" % h, tag="bank%d" % h)
+                for g in range(PASSES):
+                    nc.tensor.matmul_mx(
+                        out=bank[:],
+                        lhsT=a_codes[:, g, rows].bitcast(FP8X4),
+                        lhsT_scale=a_scales[:, g, rows],
+                        rhs=b_codes[:, g, cols].bitcast(FP8X4),
+                        rhs_scale=b_scales[:, g, cols],
+                        start=(g == 0),
+                        stop=(g == PASSES - 1),
+                    )
+                banks.append(bank)
+            return banks
+
+        e_all = resident.tile([P, NT, T], F32)
+        e_keep = resident.tile([P, NT, WIN], F32)
+        max_halves = stats.tile([P, NT * HALVES], F32)
+        neg_max = stats.tile([P, NT], F32)
+        z_halves = stats.tile([P, NT * HALVES], F32)
+        s_halves = stats.tile([P, NT * HALVES], F32)
+        neg_max_win = stats.tile([P, NT], F32)
+        z_win = stats.tile([P, NT], F32)
+        s_win = stats.tile([P, NT], F32)
+
+        def softmax_sums(r, banks):
+            for h in range(HALVES):
+                nc.vector.tensor_reduce(
+                    out=max_halves[:, HALVES * r + h : HALVES * r + h + 1], in_=banks[h][:],
+                    axis=AX.X, op=ALU.max,
+                )
+            nc.vector.tensor_reduce(
+                out=neg_max[:, r : r + 1], in_=max_halves[:, HALVES * r : HALVES * (r + 1)],
+                axis=AX.X, op=ALU.max, negate=True,
+            )
+            for h in range(HALVES):
+                col = HALVES * r + h
+                e_half = e_all[:, r, BANK * h : BANK * (h + 1)]
+                nc.scalar.activation(
+                    out=e_half, in_=banks[h][:], func=ACT.Exp, bias=neg_max[:, r : r + 1],
+                    accum_out=z_halves[:, col : col + 1],
+                )
+                products = junk.tile([P, BANK], F32, tag="products")
+                nc.vector.scalar_tensor_tensor(
+                    out=products[:], in0=banks[h][:], scalar=neg_max[:, r : r + 1], in1=e_half,
+                    op0=ALU.add, op1=ALU.mult, accum_out=s_halves[:, col : col + 1],
+                )
+
+        def window_softmax_sums(r, banks):
+            logits = stage.tile([P, WIN], F32, tag="logits")
+            for h, first, last, w_first, w_last in window_pieces(r):
+                nc.vector.tensor_tensor(
+                    out=logits[:, w_first:w_last], in0=banks[h][:, first:last],
+                    in1=keep[:, r, w_first:w_last], op=ALU.mult,
+                )
+            nc.vector.tensor_reduce(
+                out=neg_max_win[:, r : r + 1], in_=logits[:], axis=AX.X, op=ALU.max, negate=True
+            )
+            e_win = stage.tile([P, WIN], F32, tag="e_win")
+            nc.scalar.activation(
+                out=e_win[:], in_=logits[:], func=ACT.Exp, bias=neg_max_win[:, r : r + 1],
+                accum_out=z_win[:, r : r + 1],
+            )
+            products = junk.tile([P, WIN], F32, tag="win_products")
+            nc.vector.scalar_tensor_tensor(
+                out=products[:], in0=logits[:], scalar=neg_max_win[:, r : r + 1], in1=e_win[:],
+                op0=ALU.add, op1=ALU.mult, accum_out=s_win[:, r : r + 1],
+            )
+            lo = WIN_STEP * r
+            nc.gpsimd.tensor_tensor(
+                out=e_keep[:, r, :], in0=e_all[:, r, lo : lo + WIN], in1=keep[:, r, 0:WIN],
+                op=ALU.mult,
+            )
+
+        X_TILES = 2
+        NORM_STEP = NT // X_TILES
+        for r in range(NT):
+            prepare_input_tile(q_sb, q_codes, q_scales, r, nc.scalar.copy)
+            banks = product_tile(q_codes, q_scales, k_codes, k_scales, r)
+            softmax_sums(r, banks)
+            window_softmax_sums(r, banks)
+            for i in range(X_TILES):
+                if r < NORM_STEP:
+                    sum_squares(X_TILES * r + i)
+                else:
+                    prepare_u_tile(X_TILES * (r - NORM_STEP) + i)
+            if r == NORM_STEP - 1:
+                inverse_norms()
+
+        z_both = stats.tile([P, 2 * NT], F32)
+        s_both = stats.tile([P, 2 * NT], F32)
+        inv_z_both = stats.tile([P, 2 * NT], F32)
+        neg_inv_z = stats.tile([P, NT], F32)
+        e_of_zero = stats.tile([P, NT], F32)
+        s_of_zero = stats.tile([P, NT], F32)
+        nc.vector.tensor_reduce(
+            out=z_both[:, 0:NT], in_=z_halves[:].rearrange("p (r h) -> p r h", h=HALVES),
+            axis=AX.X, op=ALU.add,
+        )
+        nc.vector.tensor_reduce(
+            out=s_both[:, 0:NT], in_=s_halves[:].rearrange("p (r h) -> p r h", h=HALVES),
+            axis=AX.X, op=ALU.add,
+        )
+        nc.scalar.activation(out=e_of_zero[:], in_=neg_max_win[:], func=ACT.Exp)
+        nc.vector.scalar_tensor_tensor(
+            out=z_both[:, NT : 2 * NT], in0=e_of_zero[:], scalar=float(T - WIN), in1=z_win[:],
+            op0=ALU.mult, op1=ALU.add,
+        )
+        nc.vector.tensor_mul(out=s_of_zero[:], in0=e_of_zero[:], in1=neg_max_win[:])
+        nc.vector.scalar_tensor_tensor(
+            out=s_both[:, NT : 2 * NT], in0=s_of_zero[:], scalar=float(T - WIN), in1=s_win[:],
+            op0=ALU.mult, op1=ALU.add,
+        )
+        nc.vector.reciprocal(out=inv_z_both[:], in_=z_both[:])
+        nc.vector.tensor_scalar_mul(out=neg_inv_z[:], in0=inv_z_both[:, 0:NT], scalar1=-1.0)
+
+        minus_d_sums = stats.tile([P, 3, NT, HALVES], F32)
+        nc.vector.memset(minus_d_sums[:], 0.0)
+        gram_halves = stats.tile([P, NT * HALVES], F32)
+        ln_sums = stats.tile([P, NT], F32)
+        ln_z_both = stats.tile([P, 2 * NT], F32)
+        nc.scalar.activation(out=ln_z_both[:], in_=z_both[:], func=ACT.Ln)
+
+        for r in range(NT):
+            banks = product_tile(u_codes, u_scales, u_codes, u_scales, r)
+            for h in range(HALVES):
+                col = HALVES * r + h
+                products = junk.tile([P, BANK], F32, tag="products")
+                nc.vector.scalar_tensor_tensor(
+                    out=products[:], in0=banks[h][:], scalar=-1.0,
+                    in1=e_all[:, r, BANK * h : BANK * (h + 1)],
+                    op0=ALU.add, op1=ALU.mult, accum_out=minus_d_sums[:, 0, r, h : h + 1],
+                )
+                gram_copy = junk.tile([P, BANK], F32, tag="gram_copy")
+                nc.scalar.activation(
+                    out=gram_copy[:], in_=banks[h][:], func=ACT.Copy,
+                    accum_out=gram_halves[:, col : col + 1],
+                )
+            for i, (h, first, last, w_first, w_last) in enumerate(window_pieces(r)):
+                for plane, weights in ((1, e_keep[:, r, w_first:w_last]), (2, keep[:, r, w_first:w_last])):
+                    products = junk.tile([P, WIN], F32, tag="win_products")
+                    nc.vector.scalar_tensor_tensor(
+                        out=products[:, w_first:w_last], in0=banks[h][:, first:last], scalar=-1.0,
+                        in1=weights, op0=ALU.add, op1=ALU.mult,
+                        accum_out=minus_d_sums[:, plane, r, i : i + 1],
+                    )
+            logs = junk.tile([P, T], F32, tag="logs", bufs=2)
+            nc.scalar.activation(
+                out=logs[:], in_=e_all[:, r, :], func=ACT.Ln, scale=neg_inv_z[:, r : r + 1], bias=1.0,
+                accum_out=ln_sums[:, r : r + 1],
+            )
+
+        vectors = stats.tile([P, P], F32)
+        nc.vector.memset(vectors[:], 0.0)
+
+        entropy_both = stats.tile([P, 2 * NT], F32)
+        entropy = stats.tile([P, NT], F32)
+        nc.vector.tensor_mul(out=entropy_both[:], in0=s_both[:], in1=inv_z_both[:])
+        nc.vector.tensor_sub(out=entropy_both[:], in0=ln_z_both[:], in1=entropy_both[:])
+        nc.vector.tensor_scalar_mul(
+            out=vectors[:, COL_ENT_WIN : COL_ENT_WIN + NT], in0=entropy_both[:, NT : 2 * NT],
+            scalar1=1.0 / LN_T,
+        )
+        nc.vector.tensor_scalar_mul(out=entropy[:], in0=entropy_both[:, 0:NT], scalar1=1.0 / LN_T)
+
+        sums = stats.tile([P, 3, NT], F32)
+        gram_sums = stats.tile([P, NT], F32)
+        numer = stats.tile([P, NT], F32)
+        denom = stats.tile([P, NT], F32)
+        nc.vector.tensor_reduce(
+            out=sums[:].rearrange("p a r -> p (a r)"),
+            in_=minus_d_sums[:].rearrange("p a r h -> p (a r) h"), axis=AX.X, op=ALU.add,
+        )
+        nc.vector.tensor_reduce(
+            out=gram_sums[:], in_=gram_halves[:].rearrange("p (r h) -> p r h", h=HALVES),
+            axis=AX.X, op=ALU.add,
+        )
+        nc.vector.tensor_sub(out=numer[:], in0=sums[:, 1, :], in1=sums[:, 0, :])
+        nc.vector.tensor_mul(out=numer[:], in0=numer[:], in1=inv_z_both[:, 0:NT])
+        nc.vector.tensor_sub(out=denom[:], in0=sums[:, 2, :], in1=gram_sums[:])
+        nc.vector.tensor_scalar_add(out=denom[:], in0=denom[:], scalar1=float(T))
+        nc.vector.reciprocal(out=denom[:], in_=denom[:])
+        nc.vector.tensor_mul(out=vectors[:, COL_DEP : COL_DEP + NT], in0=numer[:], in1=denom[:])
+
+        div_h = stats.tile([P, NT], F32)
+        abs_entropy = stats.tile([P, NT], F32)
+        partial = stats.tile([P, 2], F32)
+        nc.scalar.activation(out=abs_entropy[:], in_=entropy[:], func=ACT.Abs, accum_out=partial[:, 0:1])
+        nc.scalar.activation(out=div_h[:], in_=ln_sums[:], func=ACT.Exp, accum_out=partial[:, 1:2])
+        totals_ps = psum_t.tile([P, 2], F32, tag="t")
+        nc.tensor.matmul(out=totals_ps[:], lhsT=ones[:], rhs=partial[:], start=True, stop=True)
+        totals = stats.tile([P, 2], F32)
+        nc.vector.tensor_scalar_max(out=totals[:, 0:1], in0=totals_ps[:, 0:1], scalar1=EPS)
+        nc.vector.tensor_copy(out=totals[:, 1:2], in_=totals_ps[:, 1:2])
+        nc.vector.reciprocal(out=totals[:], in_=totals[:])
+        nc.vector.tensor_scalar_mul(
+            out=vectors[:, COL_ENT : COL_ENT + NT], in0=entropy[:], scalar1=totals[:, 0:1]
+        )
+        nc.vector.tensor_scalar_mul(
+            out=vectors[:, COL_DIV : COL_DIV + NT], in0=div_h[:], scalar1=totals[:, 1:2]
+        )
+
+        dep_rows = []
+        for h in range(HALVES):
+            bank = psum_mm.tile([P, BANK], F32, name="bank%d" % h, tag="bank%d" % h)
+            for i in range(BANK // P):
+                col = COL_DEP + h * (BANK // P) + i
+                nc.tensor.matmul(
+                    out=bank[:, P * i : P * (i + 1)],
+                    lhsT=vectors[:, col : col + 1].to_broadcast([P, P]), rhs=ident_f32[:],
+                    start=True, stop=True,
+                )
+            dep_rows.append(bank)
+        for r in range(NT):
+            dep_keep = stage.tile([P, WIN], F32, tag="dep_keep")
+            for h, first, last, w_first, w_last in window_pieces(r):
+                nc.vector.tensor_tensor(
+                    out=dep_keep[:, w_first:w_last], in0=dep_rows[h][:, first:last],
+                    in1=keep[:, r, w_first:w_last], op=ALU.mult,
+                )
+            att_win = stage.tile([P, WIN], F32, tag="att_win")
+            nc.vector.scalar_tensor_tensor(
+                out=att_win[:], in0=e_keep[:, r, :], scalar=inv_z_both[:, r : r + 1], in1=dep_keep[:],
+                op0=ALU.mult, op1=ALU.add,
+            )
+            lo = WIN_STEP * r
+            nc.sync.dma_start(out=out_0[P * r : P * (r + 1), lo : lo + WIN], in_=att_win[:])
+
+        vectors_t_ps = psum_t.tile([P, P], F32, tag="t")
+        nc.tensor.transpose(vectors_t_ps[:], vectors[:], ident_f32[:])
+        vectors_t = stats.tile([P, P], F32)
+        nc.scalar.copy(out=vectors_t[:], in_=vectors_t_ps[:])
+        for out_vec, col in ((out_1, COL_ENT_WIN), (out_2, COL_DIV), (out_3, COL_ENT), (out_4, COL_DEP)):
+            nc.sync.dma_start(
+                out=out_vec.rearrange("(r p) -> r p", p=P), in_=vectors_t[col : col + NT, :]
+            )

@@ -50,34 +50,43 @@ def window_pieces(r):
 def tile_selfattention_pa_kernel(tc, x, q, k, out_0, out_1, out_2, out_3, out_4):
     nc = tc.nc
     with ExitStack() as ctx:
+        ctx.enter_context(tc.manual_schedule())
         const = ctx.enter_context(tc.tile_pool(name="const", bufs=1))
         resident = ctx.enter_context(tc.tile_pool(name="resident", bufs=1))
         stats = ctx.enter_context(tc.tile_pool(name="stats", bufs=1))
         stage = ctx.enter_context(tc.tile_pool(name="stage", bufs=3))
         junk = ctx.enter_context(tc.tile_pool(name="junk", bufs=3))
         psum_t = ctx.enter_context(tc.psum_pool(name="psum_t", bufs=2))
-        psum_mm = ctx.enter_context(tc.psum_pool(name="psum_mm", bufs=3))
+        psum_mm = ctx.enter_context(tc.psum_pool(name="psum_mm", bufs=2))
+        psum_sum = ctx.enter_context(tc.psum_pool(name="psum_sum", bufs=2))
 
         k_sb = resident.tile([P, NT, FEAT], BF16)
         q_sb = resident.tile([P, NT, FEAT], BF16)
         x_sb = resident.tile([P, NT, FEAT], BF16)
-        for dst, src in ((k_sb, k), (q_sb, q), (x_sb, x)):
-            view = src.rearrange("(r p) f -> p r f", p=P)
-            for first in range(0, NT, LOAD_TILES):
-                tiles = slice(first, first + LOAD_TILES)
-                nc.sync.dma_start(out=dst[:, tiles, :], in_=view[:, tiles, :])
+
+        def load(dst, src, first):
+            tiles = slice(first, first + LOAD_TILES)
+            nc.sync.dma_start(
+                out=dst[:, tiles, :], in_=src.rearrange("(r p) f -> p r f", p=P)[:, tiles, :]
+            )
+
+        for first in range(0, NT, LOAD_TILES):
+            load(k_sb, k, first)
+        for first in range(0, NT, LOAD_TILES):
+            load(q_sb, q, first)
+            load(x_sb, x, first)
 
         ident_f32 = const.tile([P, P], F32)
         make_identity(nc, ident_f32[:])
-        ident_bf16 = const.tile([P, P], BF16)
-        make_identity(nc, ident_bf16[:])
         ones = const.tile([P, P], F32)
         nc.vector.memset(ones[:], 1.0)
         zeros = const.tile([P, T - WIN], F32)
         nc.vector.memset(zeros[:], 0.0)
+        minus_half = const.tile([P, NT], F32)
+        nc.vector.memset(minus_half[:], -0.5)
 
         keep4 = const.tile([P, NT, WIN_BLOCKS, BLOCK], F32)
-        nc.gpsimd.memset(keep4[:], 1.0)
+        nc.vector.memset(keep4[:], 1.0)
         nc.gpsimd.affine_select(
             out=keep4[:], in_=keep4[:], compare_op=ALU.is_ge, fill=0.0,
             base=0, channel_multiplier=1,
@@ -89,6 +98,8 @@ def tile_selfattention_pa_kernel(tc, x, q, k, out_0, out_1, out_2, out_3, out_4)
             pattern=[[-ROW_SHIFT, NT], [BLOCK, WIN_BLOCKS], [0, BLOCK]],
         )
         keep = keep4[:].rearrange("p r b c -> p r (b c)")
+        ident_bf16 = const.tile([P, P], BF16)
+        make_identity(nc, ident_bf16[:])
 
         for r in range(NT):
             rows = slice(P * r, P * (r + 1))
@@ -114,24 +125,27 @@ def tile_selfattention_pa_kernel(tc, x, q, k, out_0, out_1, out_2, out_3, out_4)
                     in_=grouped[:, g, :],
                 )
 
-        def prepare_input_tile(src_sb, codes, scales, r, copy):
+        def regroup_input_tile(src_sb, r, copy):
             words = src_sb[:].bitcast(F32)
             planes = psum_t.tile([P, 2 * PASSES, P], F32, tag="t")
             for w in range(2 * PASSES):
                 nc.tensor.transpose(planes[:, w, :], words[:, r, P * w : P * (w + 1)], ident_f32[:])
-            grouped = stage.tile([P, PASSES, K_PASS], BF16, align_bytes=64, tag="grouped")
+            grouped = stage.tile([P, PASSES, K_PASS], BF16, align_bytes=64, tag="grouped", bufs=5)
             copy(
                 out=grouped[:].bitcast(F32).rearrange("p g (c v) -> p g c v", v=2),
                 in_=planes[:].rearrange("p (g v) c -> p g c v", v=2),
             )
-            quantise_tile(grouped, codes, scales, r)
+            return grouped
 
+        k_grouped = []
         for r in range(NT):
             copy = nc.vector.tensor_copy if r % 2 == 0 else nc.scalar.copy
-            prepare_input_tile(k_sb, k_codes, k_scales, r, copy)
+            k_grouped.append(regroup_input_tile(k_sb, r, copy))
+            if r >= 1:
+                quantise_tile(k_grouped[r - 1], k_codes, k_scales, r - 1)
+        quantise_tile(k_grouped[NT - 1], k_codes, k_scales, NT - 1)
 
         sum_sq = stats.tile([P, NT], F32)
-        norm = stats.tile([P, NT], F32)
         inv_norm = stats.tile([P, NT], F32)
         u_sb = resident.tile([P, NT, FEAT], BF16)
 
@@ -142,23 +156,24 @@ def tile_selfattention_pa_kernel(tc, x, q, k, out_0, out_1, out_2, out_3, out_4)
             )
 
         def inverse_norms():
-            nc.scalar.activation(out=norm[:], in_=sum_sq[:], func=ACT.Sqrt)
-            nc.vector.tensor_scalar_max(out=inv_norm[:], in0=norm[:], scalar1=EPS)
-            nc.vector.reciprocal(out=inv_norm[:], in_=inv_norm[:])
+            nc.gpsimd.tensor_scalar_max(out=inv_norm[:], in0=sum_sq[:], scalar1=EPS * EPS)
+            nc.gpsimd.tensor_tensor(out=inv_norm[:], in0=inv_norm[:], in1=minus_half[:], op=ALU.pow)
 
-        def prepare_u_tile(r):
+        def scale_x_tile(r):
             nc.vector.tensor_scalar_mul(
                 out=u_sb[:, r, :], in0=x_sb[:, r, :], scalar1=inv_norm[:, r : r + 1]
             )
+
+        def regroup_u_tile(r):
             planes = psum_t.tile([P, 4 * PASSES, P], BF16, tag="t")
             for j in range(4 * PASSES):
                 nc.tensor.transpose(planes[:, j, :], u_sb[:, r, P * j : P * (j + 1)], ident_bf16[:])
-            grouped = stage.tile([P, PASSES, K_PASS], BF16, align_bytes=64, tag="grouped")
+            grouped = stage.tile([P, PASSES, K_PASS], BF16, align_bytes=64, tag="grouped", bufs=5)
             nc.scalar.copy(
                 out=grouped[:].rearrange("p g (c t) -> p g c t", t=4),
                 in_=planes[:].rearrange("p (g t) c -> p g c t", t=4),
             )
-            quantise_tile(grouped, u_codes, u_scales, r)
+            return grouped
 
         def product_tile(a_codes, a_scales, b_codes, b_scales, r):
             rows = slice(P * r, P * (r + 1))
@@ -189,7 +204,7 @@ def tile_selfattention_pa_kernel(tc, x, q, k, out_0, out_1, out_2, out_3, out_4)
         z_win = stats.tile([P, NT], F32)
         s_win = stats.tile([P, NT], F32)
 
-        def softmax_sums(r, banks):
+        def maxima(r, banks):
             for h in range(HALVES):
                 nc.vector.tensor_reduce(
                     out=max_halves[:, HALVES * r + h : HALVES * r + h + 1], in_=banks[h][:],
@@ -199,20 +214,6 @@ def tile_selfattention_pa_kernel(tc, x, q, k, out_0, out_1, out_2, out_3, out_4)
                 out=neg_max[:, r : r + 1], in_=max_halves[:, HALVES * r : HALVES * (r + 1)],
                 axis=AX.X, op=ALU.max, negate=True,
             )
-            for h in range(HALVES):
-                col = HALVES * r + h
-                e_half = e_all[:, r, BANK * h : BANK * (h + 1)]
-                nc.scalar.activation(
-                    out=e_half, in_=banks[h][:], func=ACT.Exp, bias=neg_max[:, r : r + 1],
-                    accum_out=z_halves[:, col : col + 1],
-                )
-                products = junk.tile([P, BANK], F32, tag="products")
-                nc.vector.scalar_tensor_tensor(
-                    out=products[:], in0=banks[h][:], scalar=neg_max[:, r : r + 1], in1=e_half,
-                    op0=ALU.add, op1=ALU.mult, accum_out=s_halves[:, col : col + 1],
-                )
-
-        def window_softmax_sums(r, banks):
             logits = stage.tile([P, WIN], F32, tag="logits")
             for h, first, last, w_first, w_last in window_pieces(r):
                 nc.vector.tensor_tensor(
@@ -222,36 +223,94 @@ def tile_selfattention_pa_kernel(tc, x, q, k, out_0, out_1, out_2, out_3, out_4)
             nc.vector.tensor_reduce(
                 out=neg_max_win[:, r : r + 1], in_=logits[:], axis=AX.X, op=ALU.max, negate=True
             )
+            return logits
+
+        def exponentials(r, banks, logits):
+            for h in range(HALVES):
+                col = HALVES * r + h
+                nc.scalar.activation(
+                    out=e_all[:, r, BANK * h : BANK * (h + 1)], in_=banks[h][:], func=ACT.Exp,
+                    bias=neg_max[:, r : r + 1], accum_out=z_halves[:, col : col + 1],
+                )
             e_win = stage.tile([P, WIN], F32, tag="e_win")
             nc.scalar.activation(
                 out=e_win[:], in_=logits[:], func=ACT.Exp, bias=neg_max_win[:, r : r + 1],
                 accum_out=z_win[:, r : r + 1],
             )
+            return e_win
+
+        def entropy_sums(r, banks, logits, e_win):
+            for h in range(HALVES):
+                col = HALVES * r + h
+                products = junk.tile([P, BANK], F32, tag="products")
+                nc.vector.scalar_tensor_tensor(
+                    out=products[:], in0=banks[h][:], scalar=neg_max[:, r : r + 1],
+                    in1=e_all[:, r, BANK * h : BANK * (h + 1)],
+                    op0=ALU.add, op1=ALU.mult, accum_out=s_halves[:, col : col + 1],
+                )
             products = junk.tile([P, WIN], F32, tag="win_products")
             nc.vector.scalar_tensor_tensor(
                 out=products[:], in0=logits[:], scalar=neg_max_win[:, r : r + 1], in1=e_win[:],
                 op0=ALU.add, op1=ALU.mult, accum_out=s_win[:, r : r + 1],
             )
-            lo = WIN_STEP * r
-            nc.gpsimd.tensor_tensor(
-                out=e_keep[:, r, :], in0=e_all[:, r, lo : lo + WIN], in1=keep[:, r, 0:WIN],
-                op=ALU.mult,
-            )
+
+        def split_by_keep(r):
+            window = e_all[:, r, WIN_STEP * r : WIN_STEP * r + WIN]
+            nc.gpsimd.tensor_tensor(out=e_keep[:, r, :], in0=window, in1=keep[:, r, 0:WIN], op=ALU.mult)
+            nc.gpsimd.tensor_tensor(out=window, in0=window, in1=e_keep[:, r, :], op=ALU.subtract)
 
         X_TILES = 2
         NORM_STEP = NT // X_TILES
+        quantise_tile(regroup_input_tile(q_sb, 0, nc.scalar.copy), q_codes, q_scales, 0)
+        next_banks = product_tile(q_codes, q_scales, k_codes, k_scales, 0)
+        u_pending = []
         for r in range(NT):
-            prepare_input_tile(q_sb, q_codes, q_scales, r, nc.scalar.copy)
-            banks = product_tile(q_codes, q_scales, k_codes, k_scales, r)
-            softmax_sums(r, banks)
-            window_softmax_sums(r, banks)
+            banks = next_banks
+            if r + 1 < NT:
+                q_grouped = regroup_input_tile(q_sb, r + 1, nc.scalar.copy)
+            logits = maxima(r, banks)
+            e_win = exponentials(r, banks, logits)
+            if r + 1 < NT:
+                quantise_tile(q_grouped, q_codes, q_scales, r + 1)
+                next_banks = product_tile(q_codes, q_scales, k_codes, k_scales, r + 1)
+            for tile_index, grouped in u_pending:
+                quantise_tile(grouped, u_codes, u_scales, tile_index)
+            u_pending = []
+            if r == NORM_STEP:
+                for tile_index in range(NT):
+                    scale_x_tile(tile_index)
+            entropy_sums(r, banks, logits, e_win)
+            split_by_keep(r)
             for i in range(X_TILES):
                 if r < NORM_STEP:
                     sum_squares(X_TILES * r + i)
                 else:
-                    prepare_u_tile(X_TILES * (r - NORM_STEP) + i)
+                    tile_index = X_TILES * (r - NORM_STEP) + i
+                    u_pending.append((tile_index, regroup_u_tile(tile_index)))
             if r == NORM_STEP - 1:
                 inverse_norms()
+        for tile_index, grouped in u_pending:
+            quantise_tile(grouped, u_codes, u_scales, tile_index)
+
+        def gram_row_sums(r):
+            rows = slice(P * r, P * (r + 1))
+            acc = psum_sum.tile([P, P], F32, tag="acc")
+            for g in range(PASSES):
+                for c in range(NT):
+                    cols = slice(P * c, P * (c + 1))
+                    nc.tensor.matmul_mx(
+                        out=acc[:],
+                        lhsT=u_codes[:, g, rows].bitcast(FP8X4),
+                        lhsT_scale=u_scales[:, g, rows],
+                        rhs=u_codes[:, g, cols].bitcast(FP8X4),
+                        rhs_scale=u_scales[:, g, cols],
+                        start=(g == 0 and c == 0),
+                        stop=(g == PASSES - 1 and c == NT - 1),
+                    )
+            return acc
+
+        next_banks = product_tile(u_codes, u_scales, u_codes, u_scales, 0)
+        next_acc = gram_row_sums(0)
 
         z_both = stats.tile([P, 2 * NT], F32)
         s_both = stats.tile([P, 2 * NT], F32)
@@ -259,112 +318,83 @@ def tile_selfattention_pa_kernel(tc, x, q, k, out_0, out_1, out_2, out_3, out_4)
         neg_inv_z = stats.tile([P, NT], F32)
         e_of_zero = stats.tile([P, NT], F32)
         s_of_zero = stats.tile([P, NT], F32)
+        nc.scalar.activation(out=e_of_zero[:], in_=neg_max_win[:], func=ACT.Exp)
         nc.vector.tensor_reduce(
             out=z_both[:, 0:NT], in_=z_halves[:].rearrange("p (r h) -> p r h", h=HALVES),
             axis=AX.X, op=ALU.add,
         )
-        nc.vector.tensor_reduce(
-            out=s_both[:, 0:NT], in_=s_halves[:].rearrange("p (r h) -> p r h", h=HALVES),
-            axis=AX.X, op=ALU.add,
-        )
-        nc.scalar.activation(out=e_of_zero[:], in_=neg_max_win[:], func=ACT.Exp)
         nc.vector.scalar_tensor_tensor(
             out=z_both[:, NT : 2 * NT], in0=e_of_zero[:], scalar=float(T - WIN), in1=z_win[:],
             op0=ALU.mult, op1=ALU.add,
+        )
+        nc.vector.reciprocal(out=inv_z_both[:], in_=z_both[:])
+        nc.vector.tensor_scalar_mul(out=neg_inv_z[:], in0=inv_z_both[:, 0:NT], scalar1=-1.0)
+        nc.vector.tensor_reduce(
+            out=s_both[:, 0:NT], in_=s_halves[:].rearrange("p (r h) -> p r h", h=HALVES),
+            axis=AX.X, op=ALU.add,
         )
         nc.vector.tensor_mul(out=s_of_zero[:], in0=e_of_zero[:], in1=neg_max_win[:])
         nc.vector.scalar_tensor_tensor(
             out=s_both[:, NT : 2 * NT], in0=s_of_zero[:], scalar=float(T - WIN), in1=s_win[:],
             op0=ALU.mult, op1=ALU.add,
         )
-        nc.vector.reciprocal(out=inv_z_both[:], in_=z_both[:])
-        nc.vector.tensor_scalar_mul(out=neg_inv_z[:], in0=inv_z_both[:, 0:NT], scalar1=-1.0)
 
-        minus_d_sums = stats.tile([P, 3, NT, HALVES], F32)
+        minus_d_sums = stats.tile([P, 2, NT, HALVES], F32)
         nc.vector.memset(minus_d_sums[:], 0.0)
-        gram_halves = stats.tile([P, NT * HALVES], F32)
-        ln_sums = stats.tile([P, NT], F32)
+        gram_sums = stats.tile([P, NT], F32)
+        ln_parts = stats.tile([P, NT, 2], F32)
         ln_z_both = stats.tile([P, 2 * NT], F32)
         nc.scalar.activation(out=ln_z_both[:], in_=z_both[:], func=ACT.Ln)
 
         for r in range(NT):
-            banks = product_tile(u_codes, u_scales, u_codes, u_scales, r)
+            banks, acc = next_banks, next_acc
+            if r + 1 < NT:
+                next_banks = product_tile(u_codes, u_scales, u_codes, u_scales, r + 1)
+                next_acc = gram_row_sums(r + 1)
             for h in range(HALVES):
-                col = HALVES * r + h
                 products = junk.tile([P, BANK], F32, tag="products")
                 nc.vector.scalar_tensor_tensor(
                     out=products[:], in0=banks[h][:], scalar=-1.0,
                     in1=e_all[:, r, BANK * h : BANK * (h + 1)],
                     op0=ALU.add, op1=ALU.mult, accum_out=minus_d_sums[:, 0, r, h : h + 1],
                 )
-                gram_copy = junk.tile([P, BANK], F32, tag="gram_copy")
-                nc.scalar.activation(
-                    out=gram_copy[:], in_=banks[h][:], func=ACT.Copy,
-                    accum_out=gram_halves[:, col : col + 1],
-                )
             for i, (h, first, last, w_first, w_last) in enumerate(window_pieces(r)):
-                for plane, weights in ((1, e_keep[:, r, w_first:w_last]), (2, keep[:, r, w_first:w_last])):
-                    products = junk.tile([P, WIN], F32, tag="win_products")
-                    nc.vector.scalar_tensor_tensor(
-                        out=products[:, w_first:w_last], in0=banks[h][:, first:last], scalar=-1.0,
-                        in1=weights, op0=ALU.add, op1=ALU.mult,
-                        accum_out=minus_d_sums[:, plane, r, i : i + 1],
-                    )
+                products = junk.tile([P, WIN], F32, tag="win_products")
+                nc.vector.scalar_tensor_tensor(
+                    out=products[:, w_first:w_last], in0=banks[h][:, first:last], scalar=-1.0,
+                    in1=keep[:, r, w_first:w_last], op0=ALU.add, op1=ALU.mult,
+                    accum_out=minus_d_sums[:, 1, r, i : i + 1],
+                )
             logs = junk.tile([P, T], F32, tag="logs", bufs=2)
             nc.scalar.activation(
                 out=logs[:], in_=e_all[:, r, :], func=ACT.Ln, scale=neg_inv_z[:, r : r + 1], bias=1.0,
-                accum_out=ln_sums[:, r : r + 1],
+                accum_out=ln_parts[:, r, 0:1],
+            )
+            win_logs = junk.tile([P, WIN], F32, tag="win_logs")
+            nc.scalar.activation(
+                out=win_logs[:], in_=e_keep[:, r, :], func=ACT.Ln, scale=neg_inv_z[:, r : r + 1], bias=1.0,
+                accum_out=ln_parts[:, r, 1:2],
+            )
+            acc_copy = junk.tile([P, P], F32, tag="acc_copy")
+            nc.scalar.activation(
+                out=acc_copy[:], in_=acc[:], func=ACT.Copy, accum_out=gram_sums[:, r : r + 1]
             )
 
         vectors = stats.tile([P, P], F32)
         nc.vector.memset(vectors[:], 0.0)
 
-        entropy_both = stats.tile([P, 2 * NT], F32)
-        entropy = stats.tile([P, NT], F32)
-        nc.vector.tensor_mul(out=entropy_both[:], in0=s_both[:], in1=inv_z_both[:])
-        nc.vector.tensor_sub(out=entropy_both[:], in0=ln_z_both[:], in1=entropy_both[:])
-        nc.vector.tensor_scalar_mul(
-            out=vectors[:, COL_ENT_WIN : COL_ENT_WIN + NT], in0=entropy_both[:, NT : 2 * NT],
-            scalar1=1.0 / LN_T,
-        )
-        nc.vector.tensor_scalar_mul(out=entropy[:], in0=entropy_both[:, 0:NT], scalar1=1.0 / LN_T)
-
-        sums = stats.tile([P, 3, NT], F32)
-        gram_sums = stats.tile([P, NT], F32)
+        sums = stats.tile([P, 2, NT], F32)
         numer = stats.tile([P, NT], F32)
         denom = stats.tile([P, NT], F32)
         nc.vector.tensor_reduce(
             out=sums[:].rearrange("p a r -> p (a r)"),
             in_=minus_d_sums[:].rearrange("p a r h -> p (a r) h"), axis=AX.X, op=ALU.add,
         )
-        nc.vector.tensor_reduce(
-            out=gram_sums[:], in_=gram_halves[:].rearrange("p (r h) -> p r h", h=HALVES),
-            axis=AX.X, op=ALU.add,
-        )
-        nc.vector.tensor_sub(out=numer[:], in0=sums[:, 1, :], in1=sums[:, 0, :])
-        nc.vector.tensor_mul(out=numer[:], in0=numer[:], in1=inv_z_both[:, 0:NT])
-        nc.vector.tensor_sub(out=denom[:], in0=sums[:, 2, :], in1=gram_sums[:])
+        nc.vector.tensor_mul(out=numer[:], in0=sums[:, 0, :], in1=neg_inv_z[:])
+        nc.vector.tensor_sub(out=denom[:], in0=sums[:, 1, :], in1=gram_sums[:])
         nc.vector.tensor_scalar_add(out=denom[:], in0=denom[:], scalar1=float(T))
         nc.vector.reciprocal(out=denom[:], in_=denom[:])
         nc.vector.tensor_mul(out=vectors[:, COL_DEP : COL_DEP + NT], in0=numer[:], in1=denom[:])
-
-        div_h = stats.tile([P, NT], F32)
-        abs_entropy = stats.tile([P, NT], F32)
-        partial = stats.tile([P, 2], F32)
-        nc.scalar.activation(out=abs_entropy[:], in_=entropy[:], func=ACT.Abs, accum_out=partial[:, 0:1])
-        nc.scalar.activation(out=div_h[:], in_=ln_sums[:], func=ACT.Exp, accum_out=partial[:, 1:2])
-        totals_ps = psum_t.tile([P, 2], F32, tag="t")
-        nc.tensor.matmul(out=totals_ps[:], lhsT=ones[:], rhs=partial[:], start=True, stop=True)
-        totals = stats.tile([P, 2], F32)
-        nc.vector.tensor_scalar_max(out=totals[:, 0:1], in0=totals_ps[:, 0:1], scalar1=EPS)
-        nc.vector.tensor_copy(out=totals[:, 1:2], in_=totals_ps[:, 1:2])
-        nc.vector.reciprocal(out=totals[:], in_=totals[:])
-        nc.vector.tensor_scalar_mul(
-            out=vectors[:, COL_ENT : COL_ENT + NT], in0=entropy[:], scalar1=totals[:, 0:1]
-        )
-        nc.vector.tensor_scalar_mul(
-            out=vectors[:, COL_DIV : COL_DIV + NT], in0=div_h[:], scalar1=totals[:, 1:2]
-        )
 
         dep_rows = []
         for h in range(HALVES):
@@ -377,6 +407,27 @@ def tile_selfattention_pa_kernel(tc, x, q, k, out_0, out_1, out_2, out_3, out_4)
                     start=True, stop=True,
                 )
             dep_rows.append(bank)
+
+        entropy_both = stats.tile([P, 2 * NT], F32)
+        entropy = stats.tile([P, NT], F32)
+        ln_sums = stats.tile([P, NT], F32)
+        nc.vector.tensor_mul(out=entropy_both[:], in0=s_both[:], in1=inv_z_both[:])
+        nc.vector.tensor_sub(out=entropy_both[:], in0=ln_z_both[:], in1=entropy_both[:])
+        nc.vector.tensor_scalar_mul(out=entropy[:], in0=entropy_both[:, 0:NT], scalar1=1.0 / LN_T)
+        nc.vector.tensor_scalar_mul(
+            out=vectors[:, COL_ENT_WIN : COL_ENT_WIN + NT], in0=entropy_both[:, NT : 2 * NT],
+            scalar1=1.0 / LN_T,
+        )
+        nc.vector.tensor_reduce(out=ln_sums[:], in_=ln_parts[:], axis=AX.X, op=ALU.add)
+
+        div_h = stats.tile([P, NT], F32)
+        abs_entropy = stats.tile([P, NT], F32)
+        partial = stats.tile([P, 2], F32)
+        nc.scalar.activation(out=abs_entropy[:], in_=entropy[:], func=ACT.Abs, accum_out=partial[:, 0:1])
+        nc.scalar.activation(out=div_h[:], in_=ln_sums[:], func=ACT.Exp, accum_out=partial[:, 1:2])
+        totals_ps = psum_t.tile([P, 2], F32, tag="t")
+        nc.tensor.matmul(out=totals_ps[:], lhsT=ones[:], rhs=partial[:], start=True, stop=True)
+
         for r in range(NT):
             dep_keep = stage.tile([P, WIN], F32, tag="dep_keep")
             for h, first, last, w_first, w_last in window_pieces(r):
@@ -391,6 +442,17 @@ def tile_selfattention_pa_kernel(tc, x, q, k, out_0, out_1, out_2, out_3, out_4)
             )
             lo = WIN_STEP * r
             nc.sync.dma_start(out=out_0[P * r : P * (r + 1), lo : lo + WIN], in_=att_win[:])
+
+        totals = stats.tile([P, 2], F32)
+        nc.vector.tensor_scalar_max(out=totals[:, 0:1], in0=totals_ps[:, 0:1], scalar1=EPS)
+        nc.vector.tensor_copy(out=totals[:, 1:2], in_=totals_ps[:, 1:2])
+        nc.vector.reciprocal(out=totals[:], in_=totals[:])
+        nc.vector.tensor_scalar_mul(
+            out=vectors[:, COL_ENT : COL_ENT + NT], in0=entropy[:], scalar1=totals[:, 0:1]
+        )
+        nc.vector.tensor_scalar_mul(
+            out=vectors[:, COL_DIV : COL_DIV + NT], in0=div_h[:], scalar1=totals[:, 1:2]
+        )
 
         vectors_t_ps = psum_t.tile([P, P], F32, tag="t")
         nc.tensor.transpose(vectors_t_ps[:], vectors[:], ident_f32[:])

@@ -56,9 +56,8 @@ def tile_selfattention_pa_kernel(tc, x, q, k, out_0, out_1, out_2, out_3, out_4)
         stats = ctx.enter_context(tc.tile_pool(name="stats", bufs=1))
         stage = ctx.enter_context(tc.tile_pool(name="stage", bufs=3))
         junk = ctx.enter_context(tc.tile_pool(name="junk", bufs=3))
-        psum_t = ctx.enter_context(tc.psum_pool(name="psum_t", bufs=2))
+        psum_t = ctx.enter_context(tc.psum_pool(name="psum_t", bufs=4))
         psum_mm = ctx.enter_context(tc.psum_pool(name="psum_mm", bufs=2))
-        psum_sum = ctx.enter_context(tc.psum_pool(name="psum_sum", bufs=2))
 
         k_sb = resident.tile([P, NT, FEAT], BF16)
         q_sb = resident.tile([P, NT, FEAT], BF16)
@@ -84,6 +83,10 @@ def tile_selfattention_pa_kernel(tc, x, q, k, out_0, out_1, out_2, out_3, out_4)
         nc.vector.memset(zeros[:], 0.0)
         minus_half = const.tile([P, NT], F32)
         nc.vector.memset(minus_half[:], -0.5)
+        vectors = stats.tile([P, P], F32)
+        nc.vector.memset(vectors[:], 0.0)
+        minus_d_sums = stats.tile([P, 2, NT, HALVES], F32)
+        nc.vector.memset(minus_d_sums[:], 0.0)
 
         keep4 = const.tile([P, NT, WIN_BLOCKS, BLOCK], F32)
         nc.vector.memset(keep4[:], 1.0)
@@ -130,7 +133,7 @@ def tile_selfattention_pa_kernel(tc, x, q, k, out_0, out_1, out_2, out_3, out_4)
             planes = psum_t.tile([P, 2 * PASSES, P], F32, tag="t")
             for w in range(2 * PASSES):
                 nc.tensor.transpose(planes[:, w, :], words[:, r, P * w : P * (w + 1)], ident_f32[:])
-            grouped = stage.tile([P, PASSES, K_PASS], BF16, align_bytes=64, tag="grouped", bufs=5)
+            grouped = stage.tile([P, PASSES, K_PASS], BF16, align_bytes=64, tag="grouped", bufs=6)
             copy(
                 out=grouped[:].bitcast(F32).rearrange("p g (c v) -> p g c v", v=2),
                 in_=planes[:].rearrange("p (g v) c -> p g c v", v=2),
@@ -168,7 +171,7 @@ def tile_selfattention_pa_kernel(tc, x, q, k, out_0, out_1, out_2, out_3, out_4)
             planes = psum_t.tile([P, 4 * PASSES, P], BF16, tag="t")
             for j in range(4 * PASSES):
                 nc.tensor.transpose(planes[:, j, :], u_sb[:, r, P * j : P * (j + 1)], ident_bf16[:])
-            grouped = stage.tile([P, PASSES, K_PASS], BF16, align_bytes=64, tag="grouped", bufs=5)
+            grouped = stage.tile([P, PASSES, K_PASS], BF16, align_bytes=64, tag="grouped", bufs=6)
             nc.scalar.copy(
                 out=grouped[:].rearrange("p g (c t) -> p g c t", t=4),
                 in_=planes[:].rearrange("p (g t) c -> p g c t", t=4),
@@ -259,42 +262,9 @@ def tile_selfattention_pa_kernel(tc, x, q, k, out_0, out_1, out_2, out_3, out_4)
             nc.gpsimd.tensor_tensor(out=e_keep[:, r, :], in0=window, in1=keep[:, r, 0:WIN], op=ALU.mult)
             nc.gpsimd.tensor_tensor(out=window, in0=window, in1=e_keep[:, r, :], op=ALU.subtract)
 
-        X_TILES = 2
-        NORM_STEP = NT // X_TILES
-        quantise_tile(regroup_input_tile(q_sb, 0, nc.scalar.copy), q_codes, q_scales, 0)
-        next_banks = product_tile(q_codes, q_scales, k_codes, k_scales, 0)
-        u_pending = []
-        for r in range(NT):
-            banks = next_banks
-            if r + 1 < NT:
-                q_grouped = regroup_input_tile(q_sb, r + 1, nc.scalar.copy)
-            logits = maxima(r, banks)
-            e_win = exponentials(r, banks, logits)
-            if r + 1 < NT:
-                quantise_tile(q_grouped, q_codes, q_scales, r + 1)
-                next_banks = product_tile(q_codes, q_scales, k_codes, k_scales, r + 1)
-            for tile_index, grouped in u_pending:
-                quantise_tile(grouped, u_codes, u_scales, tile_index)
-            u_pending = []
-            if r == NORM_STEP:
-                for tile_index in range(NT):
-                    scale_x_tile(tile_index)
-            entropy_sums(r, banks, logits, e_win)
-            split_by_keep(r)
-            for i in range(X_TILES):
-                if r < NORM_STEP:
-                    sum_squares(X_TILES * r + i)
-                else:
-                    tile_index = X_TILES * (r - NORM_STEP) + i
-                    u_pending.append((tile_index, regroup_u_tile(tile_index)))
-            if r == NORM_STEP - 1:
-                inverse_norms()
-        for tile_index, grouped in u_pending:
-            quantise_tile(grouped, u_codes, u_scales, tile_index)
-
         def gram_row_sums(r):
             rows = slice(P * r, P * (r + 1))
-            acc = psum_sum.tile([P, P], F32, tag="acc")
+            acc = psum_t.tile([P, P], F32, tag="t")
             for g in range(PASSES):
                 for c in range(NT):
                     cols = slice(P * c, P * (c + 1))
@@ -309,8 +279,43 @@ def tile_selfattention_pa_kernel(tc, x, q, k, out_0, out_1, out_2, out_3, out_4)
                     )
             return acc
 
-        next_banks = product_tile(u_codes, u_scales, u_codes, u_scales, 0)
-        next_acc = gram_row_sums(0)
+        X_TILES = 2
+        NORM_STEP = NT // X_TILES
+
+        def x_step(s):
+            regrouped = []
+            for tile_index in range(X_TILES * (s % NORM_STEP), X_TILES * (s % NORM_STEP + 1)):
+                if s < NORM_STEP:
+                    sum_squares(tile_index)
+                else:
+                    regrouped.append((tile_index, regroup_u_tile(tile_index)))
+            if s == NORM_STEP - 1:
+                inverse_norms()
+            return regrouped
+
+        quantise_tile(regroup_input_tile(q_sb, 0, nc.scalar.copy), q_codes, q_scales, 0)
+        next_banks = product_tile(q_codes, q_scales, k_codes, k_scales, 0)
+        u_pending = x_step(0)
+        for r in range(NT):
+            banks = next_banks
+            if r + 1 < NT:
+                q_grouped = regroup_input_tile(q_sb, r + 1, nc.scalar.copy)
+            logits = maxima(r, banks)
+            e_win = exponentials(r, banks, logits)
+            if r + 1 < NT:
+                quantise_tile(q_grouped, q_codes, q_scales, r + 1)
+                next_banks = product_tile(q_codes, q_scales, k_codes, k_scales, r + 1)
+            for tile_index, grouped in u_pending:
+                quantise_tile(grouped, u_codes, u_scales, tile_index)
+            if r + 1 == NORM_STEP:
+                for tile_index in range(NT):
+                    scale_x_tile(tile_index)
+            if r + 1 == NT:
+                next_banks = product_tile(u_codes, u_scales, u_codes, u_scales, 0)
+                next_acc = gram_row_sums(0)
+            entropy_sums(r, banks, logits, e_win)
+            split_by_keep(r)
+            u_pending = x_step(r + 1) if r + 1 < NT else []
 
         z_both = stats.tile([P, 2 * NT], F32)
         s_both = stats.tile([P, 2 * NT], F32)
@@ -318,39 +323,125 @@ def tile_selfattention_pa_kernel(tc, x, q, k, out_0, out_1, out_2, out_3, out_4)
         neg_inv_z = stats.tile([P, NT], F32)
         e_of_zero = stats.tile([P, NT], F32)
         s_of_zero = stats.tile([P, NT], F32)
+        whole, window = slice(0, NT), slice(NT, 2 * NT)
         nc.scalar.activation(out=e_of_zero[:], in_=neg_max_win[:], func=ACT.Exp)
         nc.vector.tensor_reduce(
-            out=z_both[:, 0:NT], in_=z_halves[:].rearrange("p (r h) -> p r h", h=HALVES),
+            out=z_both[:, whole], in_=z_halves[:].rearrange("p (r h) -> p r h", h=HALVES),
             axis=AX.X, op=ALU.add,
         )
+        nc.vector.tensor_reduce(
+            out=s_both[:, whole], in_=s_halves[:].rearrange("p (r h) -> p r h", h=HALVES),
+            axis=AX.X, op=ALU.add,
+        )
+        nc.vector.reciprocal(out=inv_z_both[:, whole], in_=z_both[:, whole])
         nc.vector.scalar_tensor_tensor(
-            out=z_both[:, NT : 2 * NT], in0=e_of_zero[:], scalar=float(T - WIN), in1=z_win[:],
+            out=z_both[:, window], in0=e_of_zero[:], scalar=float(T - WIN), in1=z_win[:],
             op0=ALU.mult, op1=ALU.add,
         )
-        nc.vector.reciprocal(out=inv_z_both[:], in_=z_both[:])
-        nc.vector.tensor_scalar_mul(out=neg_inv_z[:], in0=inv_z_both[:, 0:NT], scalar1=-1.0)
-        nc.vector.tensor_reduce(
-            out=s_both[:, 0:NT], in_=s_halves[:].rearrange("p (r h) -> p r h", h=HALVES),
-            axis=AX.X, op=ALU.add,
-        )
+        nc.vector.tensor_scalar_mul(out=neg_inv_z[:], in0=inv_z_both[:, whole], scalar1=-1.0)
         nc.vector.tensor_mul(out=s_of_zero[:], in0=e_of_zero[:], in1=neg_max_win[:])
+        nc.vector.reciprocal(out=inv_z_both[:, window], in_=z_both[:, window])
         nc.vector.scalar_tensor_tensor(
-            out=s_both[:, NT : 2 * NT], in0=s_of_zero[:], scalar=float(T - WIN), in1=s_win[:],
+            out=s_both[:, window], in0=s_of_zero[:], scalar=float(T - WIN), in1=s_win[:],
             op0=ALU.mult, op1=ALU.add,
         )
 
-        minus_d_sums = stats.tile([P, 2, NT, HALVES], F32)
-        nc.vector.memset(minus_d_sums[:], 0.0)
         gram_sums = stats.tile([P, NT], F32)
         ln_parts = stats.tile([P, NT, 2], F32)
         ln_z_both = stats.tile([P, 2 * NT], F32)
+        att_keep = resident.tile([P, NT, WIN], F32)
         nc.scalar.activation(out=ln_z_both[:], in_=z_both[:], func=ACT.Ln)
+
+        def total_over_tokens(partial):
+            total_ps = psum_t.tile([P, 1], F32, tag="t")
+            nc.tensor.matmul(out=total_ps[:], lhsT=ones[:], rhs=partial, start=True, stop=True)
+            return total_ps
+
+        def entropy_outputs():
+            entropy_both = stats.tile([P, 2 * NT], F32)
+            abs_entropy = stats.tile([P, NT], F32)
+            abs_sum = stats.tile([P, 1], F32)
+            inv_total = stats.tile([P, 1], F32)
+            nc.vector.tensor_mul(out=entropy_both[:], in0=s_both[:], in1=inv_z_both[:])
+            nc.vector.tensor_sub(out=entropy_both[:], in0=ln_z_both[:], in1=entropy_both[:])
+            nc.vector.tensor_scalar_mul(out=entropy_both[:], in0=entropy_both[:], scalar1=1.0 / LN_T)
+            nc.scalar.activation(
+                out=abs_entropy[:], in_=entropy_both[:, whole], func=ACT.Abs, accum_out=abs_sum[:]
+            )
+            nc.vector.tensor_copy(
+                out=vectors[:, COL_ENT_WIN : COL_ENT_WIN + NT], in_=entropy_both[:, window]
+            )
+            total_ps = total_over_tokens(abs_sum[:])
+            nc.vector.tensor_scalar_max(out=inv_total[:], in0=total_ps[:], scalar1=EPS)
+            nc.vector.reciprocal(out=inv_total[:], in_=inv_total[:])
+            nc.vector.tensor_scalar_mul(
+                out=vectors[:, COL_ENT : COL_ENT + NT], in0=entropy_both[:, whole], scalar1=inv_total[:]
+            )
+
+        sums = stats.tile([P, 2, NT], F32)
+        numer = stats.tile([P, NT], F32)
+        denom = stats.tile([P, NT], F32)
+        dep_rows = []
+
+        def dep_factor_of(first, last):
+            tiles = slice(first, last)
+            nc.vector.tensor_reduce(
+                out=sums[:, :, tiles], in_=minus_d_sums[:, :, tiles, :], axis=AX.X, op=ALU.add
+            )
+            nc.vector.scalar_tensor_tensor(
+                out=denom[:, tiles], in0=sums[:, 1, tiles], scalar=float(T), in1=gram_sums[:, tiles],
+                op0=ALU.add, op1=ALU.subtract,
+            )
+            nc.vector.tensor_mul(out=numer[:, tiles], in0=sums[:, 0, tiles], in1=neg_inv_z[:, tiles])
+            nc.vector.reciprocal(out=denom[:, tiles], in_=denom[:, tiles])
+            nc.vector.tensor_mul(
+                out=vectors[:, COL_DEP + first : COL_DEP + last], in0=numer[:, tiles], in1=denom[:, tiles]
+            )
+            for tile_index in range(first, last):
+                h, i = divmod(tile_index, BANK // P)
+                nc.tensor.matmul(
+                    out=dep_rows[h][:, P * i : P * (i + 1)],
+                    lhsT=vectors[:, COL_DEP + tile_index : COL_DEP + tile_index + 1].to_broadcast([P, P]),
+                    rhs=ident_f32[:], start=True, stop=True,
+                )
+
+        def finish_window(r):
+            dep_keep = stage.tile([P, WIN], F32, tag="dep_keep")
+            for h, first, last, w_first, w_last in window_pieces(r):
+                nc.vector.tensor_tensor(
+                    out=dep_keep[:, w_first:w_last], in0=dep_rows[h][:, first:last],
+                    in1=keep[:, r, w_first:w_last], op=ALU.mult,
+                )
+            att_win = stage.tile([P, WIN], F32, tag="att_win")
+            nc.gpsimd.tensor_tensor(out=att_win[:], in0=dep_keep[:], in1=att_keep[:, r, :], op=ALU.add)
+            lo = WIN_STEP * r
+            nc.sync.dma_start(out=out_0[P * r : P * (r + 1), lo : lo + WIN], in_=att_win[:])
+
+        FIRST_BATCH = 6
+        FIRST_WINDOWS = (P * FIRST_BATCH - WIN) // WIN_STEP + 1
 
         for r in range(NT):
             banks, acc = next_banks, next_acc
             if r + 1 < NT:
                 next_banks = product_tile(u_codes, u_scales, u_codes, u_scales, r + 1)
                 next_acc = gram_row_sums(r + 1)
+            logs = junk.tile([P, T], F32, tag="logs", bufs=2)
+            nc.scalar.activation(
+                out=logs[:], in_=e_all[:, r, :], func=ACT.Ln, scale=neg_inv_z[:, r : r + 1], bias=1.0,
+                accum_out=ln_parts[:, r, 0:1],
+            )
+            win_logs = junk.tile([P, WIN], F32, tag="win_logs")
+            nc.scalar.activation(
+                out=win_logs[:], in_=e_keep[:, r, :], func=ACT.Ln, scale=neg_inv_z[:, r : r + 1], bias=1.0,
+                accum_out=ln_parts[:, r, 1:2],
+            )
+            nc.scalar.activation(
+                out=att_keep[:, r, :], in_=e_keep[:, r, :], func=ACT.Copy, scale=inv_z_both[:, r : r + 1]
+            )
+            acc_copy = junk.tile([P, P], F32, tag="acc_copy")
+            nc.scalar.activation(
+                out=acc_copy[:], in_=acc[:], func=ACT.Copy, accum_out=gram_sums[:, r : r + 1]
+            )
             for h in range(HALVES):
                 products = junk.tile([P, BANK], F32, tag="products")
                 nc.vector.scalar_tensor_tensor(
@@ -365,93 +456,29 @@ def tile_selfattention_pa_kernel(tc, x, q, k, out_0, out_1, out_2, out_3, out_4)
                     in1=keep[:, r, w_first:w_last], op0=ALU.add, op1=ALU.mult,
                     accum_out=minus_d_sums[:, 1, r, i : i + 1],
                 )
-            logs = junk.tile([P, T], F32, tag="logs", bufs=2)
-            nc.scalar.activation(
-                out=logs[:], in_=e_all[:, r, :], func=ACT.Ln, scale=neg_inv_z[:, r : r + 1], bias=1.0,
-                accum_out=ln_parts[:, r, 0:1],
-            )
-            win_logs = junk.tile([P, WIN], F32, tag="win_logs")
-            nc.scalar.activation(
-                out=win_logs[:], in_=e_keep[:, r, :], func=ACT.Ln, scale=neg_inv_z[:, r : r + 1], bias=1.0,
-                accum_out=ln_parts[:, r, 1:2],
-            )
-            acc_copy = junk.tile([P, P], F32, tag="acc_copy")
-            nc.scalar.activation(
-                out=acc_copy[:], in_=acc[:], func=ACT.Copy, accum_out=gram_sums[:, r : r + 1]
-            )
+            if r == 0:
+                entropy_outputs()
+            if r + 1 == FIRST_BATCH:
+                for h in range(HALVES):
+                    dep_rows.append(psum_t.tile([P, BANK], F32, name="dep_rows%d" % h, tag="t"))
+                dep_factor_of(0, FIRST_BATCH)
+            if r == FIRST_BATCH:
+                for w in range(FIRST_WINDOWS):
+                    finish_window(w)
 
-        vectors = stats.tile([P, P], F32)
-        nc.vector.memset(vectors[:], 0.0)
-
-        sums = stats.tile([P, 2, NT], F32)
-        numer = stats.tile([P, NT], F32)
-        denom = stats.tile([P, NT], F32)
-        nc.vector.tensor_reduce(
-            out=sums[:].rearrange("p a r -> p (a r)"),
-            in_=minus_d_sums[:].rearrange("p a r h -> p (a r) h"), axis=AX.X, op=ALU.add,
-        )
-        nc.vector.tensor_mul(out=numer[:], in0=sums[:, 0, :], in1=neg_inv_z[:])
-        nc.vector.tensor_sub(out=denom[:], in0=sums[:, 1, :], in1=gram_sums[:])
-        nc.vector.tensor_scalar_add(out=denom[:], in0=denom[:], scalar1=float(T))
-        nc.vector.reciprocal(out=denom[:], in_=denom[:])
-        nc.vector.tensor_mul(out=vectors[:, COL_DEP : COL_DEP + NT], in0=numer[:], in1=denom[:])
-
-        dep_rows = []
-        for h in range(HALVES):
-            bank = psum_mm.tile([P, BANK], F32, name="bank%d" % h, tag="bank%d" % h)
-            for i in range(BANK // P):
-                col = COL_DEP + h * (BANK // P) + i
-                nc.tensor.matmul(
-                    out=bank[:, P * i : P * (i + 1)],
-                    lhsT=vectors[:, col : col + 1].to_broadcast([P, P]), rhs=ident_f32[:],
-                    start=True, stop=True,
-                )
-            dep_rows.append(bank)
-
-        entropy_both = stats.tile([P, 2 * NT], F32)
-        entropy = stats.tile([P, NT], F32)
         ln_sums = stats.tile([P, NT], F32)
-        nc.vector.tensor_mul(out=entropy_both[:], in0=s_both[:], in1=inv_z_both[:])
-        nc.vector.tensor_sub(out=entropy_both[:], in0=ln_z_both[:], in1=entropy_both[:])
-        nc.vector.tensor_scalar_mul(out=entropy[:], in0=entropy_both[:, 0:NT], scalar1=1.0 / LN_T)
-        nc.vector.tensor_scalar_mul(
-            out=vectors[:, COL_ENT_WIN : COL_ENT_WIN + NT], in0=entropy_both[:, NT : 2 * NT],
-            scalar1=1.0 / LN_T,
-        )
-        nc.vector.tensor_reduce(out=ln_sums[:], in_=ln_parts[:], axis=AX.X, op=ALU.add)
-
         div_h = stats.tile([P, NT], F32)
-        abs_entropy = stats.tile([P, NT], F32)
-        partial = stats.tile([P, 2], F32)
-        nc.scalar.activation(out=abs_entropy[:], in_=entropy[:], func=ACT.Abs, accum_out=partial[:, 0:1])
-        nc.scalar.activation(out=div_h[:], in_=ln_sums[:], func=ACT.Exp, accum_out=partial[:, 1:2])
-        totals_ps = psum_t.tile([P, 2], F32, tag="t")
-        nc.tensor.matmul(out=totals_ps[:], lhsT=ones[:], rhs=partial[:], start=True, stop=True)
-
-        for r in range(NT):
-            dep_keep = stage.tile([P, WIN], F32, tag="dep_keep")
-            for h, first, last, w_first, w_last in window_pieces(r):
-                nc.vector.tensor_tensor(
-                    out=dep_keep[:, w_first:w_last], in0=dep_rows[h][:, first:last],
-                    in1=keep[:, r, w_first:w_last], op=ALU.mult,
-                )
-            att_win = stage.tile([P, WIN], F32, tag="att_win")
-            nc.vector.scalar_tensor_tensor(
-                out=att_win[:], in0=e_keep[:, r, :], scalar=inv_z_both[:, r : r + 1], in1=dep_keep[:],
-                op0=ALU.mult, op1=ALU.add,
-            )
-            lo = WIN_STEP * r
-            nc.sync.dma_start(out=out_0[P * r : P * (r + 1), lo : lo + WIN], in_=att_win[:])
-
-        totals = stats.tile([P, 2], F32)
-        nc.vector.tensor_scalar_max(out=totals[:, 0:1], in0=totals_ps[:, 0:1], scalar1=EPS)
-        nc.vector.tensor_copy(out=totals[:, 1:2], in_=totals_ps[:, 1:2])
-        nc.vector.reciprocal(out=totals[:], in_=totals[:])
+        div_sum = stats.tile([P, 1], F32)
+        inv_div_total = stats.tile([P, 1], F32)
+        nc.vector.tensor_reduce(out=ln_sums[:], in_=ln_parts[:], axis=AX.X, op=ALU.add)
+        nc.scalar.activation(out=div_h[:], in_=ln_sums[:], func=ACT.Exp, accum_out=div_sum[:])
+        dep_factor_of(FIRST_BATCH, NT)
+        div_total_ps = total_over_tokens(div_sum[:])
+        for w in range(FIRST_WINDOWS, NT):
+            finish_window(w)
+        nc.vector.reciprocal(out=inv_div_total[:], in_=div_total_ps[:])
         nc.vector.tensor_scalar_mul(
-            out=vectors[:, COL_ENT : COL_ENT + NT], in0=entropy[:], scalar1=totals[:, 0:1]
-        )
-        nc.vector.tensor_scalar_mul(
-            out=vectors[:, COL_DIV : COL_DIV + NT], in0=div_h[:], scalar1=totals[:, 1:2]
+            out=vectors[:, COL_DIV : COL_DIV + NT], in0=div_h[:], scalar1=inv_div_total[:]
         )
 
         vectors_t_ps = psum_t.tile([P, P], F32, tag="t")

@@ -50,7 +50,6 @@ def window_pieces(r):
 def tile_selfattention_pa_kernel(tc, x, q, k, out_0, out_1, out_2, out_3, out_4):
     nc = tc.nc
     with ExitStack() as ctx:
-        ctx.enter_context(tc.manual_schedule())
         const = ctx.enter_context(tc.tile_pool(name="const", bufs=1))
         resident = ctx.enter_context(tc.tile_pool(name="resident", bufs=1))
         stats = ctx.enter_context(tc.tile_pool(name="stats", bufs=1))
@@ -81,7 +80,7 @@ def tile_selfattention_pa_kernel(tc, x, q, k, out_0, out_1, out_2, out_3, out_4)
         nc.vector.memset(ones[:], 1.0)
         zeros = const.tile([P, T - WIN], F32)
         nc.vector.memset(zeros[:], 0.0)
-        minus_half = const.tile([P, NT], F32)
+        minus_half = const.tile([P, 1], F32)
         nc.vector.memset(minus_half[:], -0.5)
         vectors = stats.tile([P, P], F32)
         nc.vector.memset(vectors[:], 0.0)
@@ -158,19 +157,25 @@ def tile_selfattention_pa_kernel(tc, x, q, k, out_0, out_1, out_2, out_3, out_4)
                 out=squares[:], in_=x_sb[:, r, :], func=ACT.Square, accum_out=sum_sq[:, r : r + 1]
             )
 
-        def inverse_norms():
-            nc.gpsimd.tensor_scalar_max(out=inv_norm[:], in0=sum_sq[:], scalar1=EPS * EPS)
-            nc.gpsimd.tensor_tensor(out=inv_norm[:], in0=inv_norm[:], in1=minus_half[:], op=ALU.pow)
+        def inverse_norm(r):
+            col = slice(r, r + 1)
+            nc.gpsimd.tensor_scalar_max(out=inv_norm[:, col], in0=sum_sq[:, col], scalar1=EPS * EPS)
+            nc.gpsimd.tensor_tensor(
+                out=inv_norm[:, col], in0=inv_norm[:, col], in1=minus_half[:], op=ALU.pow
+            )
 
         def scale_x_tile(r):
             nc.vector.tensor_scalar_mul(
                 out=u_sb[:, r, :], in0=x_sb[:, r, :], scalar1=inv_norm[:, r : r + 1]
             )
 
-        def regroup_u_tile(r):
+        def transpose_u_tile(r):
             planes = psum_t.tile([P, 4 * PASSES, P], BF16, tag="t")
             for j in range(4 * PASSES):
                 nc.tensor.transpose(planes[:, j, :], u_sb[:, r, P * j : P * (j + 1)], ident_bf16[:])
+            return planes
+
+        def regroup_u_tile(planes):
             grouped = stage.tile([P, PASSES, K_PASS], BF16, align_bytes=64, tag="grouped", bufs=6)
             nc.scalar.copy(
                 out=grouped[:].rearrange("p g (c t) -> p g c t", t=4),
@@ -279,43 +284,48 @@ def tile_selfattention_pa_kernel(tc, x, q, k, out_0, out_1, out_2, out_3, out_4)
                     )
             return acc
 
-        X_TILES = 2
-        NORM_STEP = NT // X_TILES
+        Q_AHEAD = 3
+        ACC_AHEAD = 2
 
-        def x_step(s):
-            regrouped = []
-            for tile_index in range(X_TILES * (s % NORM_STEP), X_TILES * (s % NORM_STEP + 1)):
-                if s < NORM_STEP:
-                    sum_squares(tile_index)
-                else:
-                    regrouped.append((tile_index, regroup_u_tile(tile_index)))
-            if s == NORM_STEP - 1:
-                inverse_norms()
-            return regrouped
+        def prepare_q_tile(r):
+            return regroup_input_tile(q_sb, r, nc.scalar.copy)
 
-        quantise_tile(regroup_input_tile(q_sb, 0, nc.scalar.copy), q_codes, q_scales, 0)
-        next_banks = product_tile(q_codes, q_scales, k_codes, k_scales, 0)
-        u_pending = x_step(0)
+        def energies(r):
+            return product_tile(q_codes, q_scales, k_codes, k_scales, r)
+
+        for r in range(Q_AHEAD):
+            quantise_tile(prepare_q_tile(r), q_codes, q_scales, r)
+        banks = [energies(0), energies(1)]
+        for r in range(2):
+            sum_squares(r)
+            inverse_norm(r)
+        scale_x_tile(0)
+        u_planes = transpose_u_tile(0)
+        logits = [maxima(0, banks[0])]
+        accs = []
         for r in range(NT):
-            banks = next_banks
+            e_win = exponentials(r, banks[r], logits[r])
             if r + 1 < NT:
-                q_grouped = regroup_input_tile(q_sb, r + 1, nc.scalar.copy)
-            logits = maxima(r, banks)
-            e_win = exponentials(r, banks, logits)
-            if r + 1 < NT:
-                quantise_tile(q_grouped, q_codes, q_scales, r + 1)
-                next_banks = product_tile(q_codes, q_scales, k_codes, k_scales, r + 1)
-            for tile_index, grouped in u_pending:
-                quantise_tile(grouped, u_codes, u_scales, tile_index)
-            if r + 1 == NORM_STEP:
-                for tile_index in range(NT):
-                    scale_x_tile(tile_index)
-            if r + 1 == NT:
-                next_banks = product_tile(u_codes, u_scales, u_codes, u_scales, 0)
-                next_acc = gram_row_sums(0)
-            entropy_sums(r, banks, logits, e_win)
+                logits.append(maxima(r + 1, banks[r + 1]))
+            entropy_sums(r, banks[r], logits[r], e_win)
             split_by_keep(r)
-            u_pending = x_step(r + 1) if r + 1 < NT else []
+            if r + 2 < NT:
+                banks.append(energies(r + 2))
+            if r + Q_AHEAD < NT:
+                q_grouped = prepare_q_tile(r + Q_AHEAD)
+            u_grouped = regroup_u_tile(u_planes)
+            if r + Q_AHEAD < NT:
+                quantise_tile(q_grouped, q_codes, q_scales, r + Q_AHEAD)
+            quantise_tile(u_grouped, u_codes, u_scales, r)
+            if r + 1 < NT:
+                scale_x_tile(r + 1)
+                u_planes = transpose_u_tile(r + 1)
+            if r + 2 < NT:
+                sum_squares(r + 2)
+                inverse_norm(r + 2)
+        next_banks = product_tile(u_codes, u_scales, u_codes, u_scales, 0)
+        for tile_index in range(ACC_AHEAD):
+            accs.append(gram_row_sums(tile_index))
 
         z_both = stats.tile([P, 2 * NT], F32)
         s_both = stats.tile([P, 2 * NT], F32)
@@ -421,10 +431,11 @@ def tile_selfattention_pa_kernel(tc, x, q, k, out_0, out_1, out_2, out_3, out_4)
         FIRST_WINDOWS = (P * FIRST_BATCH - WIN) // WIN_STEP + 1
 
         for r in range(NT):
-            banks, acc = next_banks, next_acc
+            banks = next_banks
             if r + 1 < NT:
                 next_banks = product_tile(u_codes, u_scales, u_codes, u_scales, r + 1)
-                next_acc = gram_row_sums(r + 1)
+            if r + ACC_AHEAD < NT:
+                accs.append(gram_row_sums(r + ACC_AHEAD))
             logs = junk.tile([P, T], F32, tag="logs", bufs=2)
             nc.scalar.activation(
                 out=logs[:], in_=e_all[:, r, :], func=ACT.Ln, scale=neg_inv_z[:, r : r + 1], bias=1.0,
@@ -435,13 +446,10 @@ def tile_selfattention_pa_kernel(tc, x, q, k, out_0, out_1, out_2, out_3, out_4)
                 out=win_logs[:], in_=e_keep[:, r, :], func=ACT.Ln, scale=neg_inv_z[:, r : r + 1], bias=1.0,
                 accum_out=ln_parts[:, r, 1:2],
             )
-            nc.scalar.activation(
-                out=att_keep[:, r, :], in_=e_keep[:, r, :], func=ACT.Copy, scale=inv_z_both[:, r : r + 1]
+            nc.vector.tensor_scalar_mul(
+                out=att_keep[:, r, :], in0=e_keep[:, r, :], scalar1=inv_z_both[:, r : r + 1]
             )
-            acc_copy = junk.tile([P, P], F32, tag="acc_copy")
-            nc.scalar.activation(
-                out=acc_copy[:], in_=acc[:], func=ACT.Copy, accum_out=gram_sums[:, r : r + 1]
-            )
+            nc.vector.tensor_reduce(out=gram_sums[:, r : r + 1], in_=accs[r][:], axis=AX.X, op=ALU.add)
             for h in range(HALVES):
                 products = junk.tile([P, BANK], F32, tag="products")
                 nc.vector.scalar_tensor_tensor(

@@ -28,8 +28,8 @@ WIN_STEP = 2 * BLOCK
 WIN = T - WIN_STEP * (NT - 1)
 WIN_BLOCKS = 4
 ROW_SHIFT = P - WIN_STEP
-
-LOAD_TILES = 2
+LAST_BLOCK = T % BLOCK
+HUGE = 2.0**100
 
 FLOPS = 2 * 2 * T * T * FEAT
 
@@ -57,51 +57,51 @@ def tile_selfattention_pa_kernel(tc, x, q, k, out_0, out_1, out_2, out_3, out_4)
         junk = ctx.enter_context(tc.tile_pool(name="junk", bufs=3))
         psum_t = ctx.enter_context(tc.psum_pool(name="psum_t", bufs=4))
         psum_mm = ctx.enter_context(tc.psum_pool(name="psum_mm", bufs=2))
+        ctx.enter_context(tc.manual_schedule())
 
         k_sb = resident.tile([P, NT, FEAT], BF16)
         q_sb = resident.tile([P, NT, FEAT], BF16)
         x_sb = resident.tile([P, NT, FEAT], BF16)
 
-        def load(dst, src, first):
-            tiles = slice(first, first + LOAD_TILES)
-            nc.sync.dma_start(
-                out=dst[:, tiles, :], in_=src.rearrange("(r p) f -> p r f", p=P)[:, tiles, :]
-            )
+        def load(dst, src, r):
+            nc.sync.dma_start(out=dst[:, r, :], in_=src[P * r : P * (r + 1), :])
 
-        for first in range(0, NT, LOAD_TILES):
-            load(k_sb, k, first)
-        for first in range(0, NT, LOAD_TILES):
-            load(q_sb, q, first)
-            load(x_sb, x, first)
+        X_EARLY = 2
+        for r in range(X_EARLY):
+            load(x_sb, x, r)
+        for r in range(NT):
+            load(k_sb, k, r)
+        for r in range(NT):
+            load(q_sb, q, r)
+            if 1 <= r < NT - 1:
+                load(x_sb, x, r + 1)
 
         ident_f32 = const.tile([P, P], F32)
         make_identity(nc, ident_f32[:])
-        ones = const.tile([P, P], F32)
-        nc.vector.memset(ones[:], 1.0)
-        zeros = const.tile([P, T - WIN], F32)
-        nc.vector.memset(zeros[:], 0.0)
+        outside4 = const.tile([P, NT, WIN_BLOCKS, BLOCK], F32)
+        nc.vector.memset(outside4[:], 0.0)
         minus_half = const.tile([P, 1], F32)
         nc.vector.memset(minus_half[:], -0.5)
-        vectors = stats.tile([P, P], F32)
-        nc.vector.memset(vectors[:], 0.0)
         minus_d_sums = stats.tile([P, 2, NT, HALVES], F32)
         nc.vector.memset(minus_d_sums[:], 0.0)
-
-        keep4 = const.tile([P, NT, WIN_BLOCKS, BLOCK], F32)
-        nc.vector.memset(keep4[:], 1.0)
+        vectors = stats.tile([P, P], F32)
+        nc.vector.memset(vectors[:], 0.0)
+        zeros = const.tile([P, T - WIN], F32)
+        nc.gpsimd.memset(zeros[:], 0.0)
+        ones = const.tile([P, P], F32)
+        nc.gpsimd.memset(ones[:], 1.0)
+        outside_count = const.tile([P, NT], F32)
+        nc.gpsimd.memset(outside_count[:], float(T - BLOCK))
         nc.gpsimd.affine_select(
-            out=keep4[:], in_=keep4[:], compare_op=ALU.is_ge, fill=0.0,
+            out=outside4[:], in_=outside4[:], compare_op=ALU.is_ge, fill=-HUGE,
             base=0, channel_multiplier=1,
             pattern=[[ROW_SHIFT, NT], [-BLOCK, WIN_BLOCKS], [0, BLOCK]],
         )
-        nc.gpsimd.affine_select(
-            out=keep4[:], in_=keep4[:], compare_op=ALU.is_ge, fill=0.0,
-            base=BLOCK - 1, channel_multiplier=-1,
-            pattern=[[-ROW_SHIFT, NT], [BLOCK, WIN_BLOCKS], [0, BLOCK]],
-        )
+        keep4 = const.tile([P, NT, WIN_BLOCKS, BLOCK], F32)
+        zero4 = const.tile([P, NT, WIN_BLOCKS, BLOCK], F32)
+        outside = outside4[:].rearrange("p r b c -> p r (b c)")
         keep = keep4[:].rearrange("p r b c -> p r (b c)")
-        ident_bf16 = const.tile([P, P], BF16)
-        make_identity(nc, ident_bf16[:])
+        zero = zero4[:].rearrange("p r b c -> p r (b c)")
 
         for r in range(NT):
             rows = slice(P * r, P * (r + 1))
@@ -113,8 +113,8 @@ def tile_selfattention_pa_kernel(tc, x, q, k, out_0, out_1, out_2, out_3, out_4)
 
         k_codes = resident.tile([P, PASSES, T], U32, align_bytes=64)
         k_scales = resident.tile([P, PASSES, T], U8, align_bytes=64)
-        q_codes = resident.tile([P, PASSES, T], U32, align_bytes=64)
-        q_scales = resident.tile([P, PASSES, T], U8, align_bytes=64)
+        q_codes = resident.tile([P, NT, PASSES * P], U32, align_bytes=64)
+        q_scales = resident.tile([P, NT, PASSES * P], U8, align_bytes=64)
         u_codes = resident.tile([P, PASSES, T], U32, align_bytes=64)
         u_scales = resident.tile([P, PASSES, T], U8, align_bytes=64)
 
@@ -124,32 +124,37 @@ def tile_selfattention_pa_kernel(tc, x, q, k, out_0, out_1, out_2, out_3, out_4)
                 nc.vector.quantize_mx(
                     out=codes[:, g, cols].bitcast(FP8X4),
                     scales=scales[:, g, cols],
-                    in_=grouped[:, g, :],
+                    in_=grouped[:, K_PASS * g : K_PASS * (g + 1)],
                 )
 
-        def regroup_input_tile(src_sb, r, copy):
-            words = src_sb[:].bitcast(F32)
-            planes = psum_t.tile([P, 2 * PASSES, P], F32, tag="t")
+        def quantise_q_tile(grouped, r):
+            nc.vector.quantize_mx(
+                out=q_codes[:, r, :].bitcast(FP8X4), scales=q_scales[:, r, :], in_=grouped[:]
+            )
+
+        def transpose_words(words):
+            planes = psum_t.tile([P, 2 * PASSES, P], F32, name="planes", tag="t")
             for w in range(2 * PASSES):
-                nc.tensor.transpose(planes[:, w, :], words[:, r, P * w : P * (w + 1)], ident_f32[:])
-            grouped = stage.tile([P, PASSES, K_PASS], BF16, align_bytes=64, tag="grouped", bufs=6)
+                nc.tensor.transpose(planes[:, w, :], words[:, P * w : P * (w + 1)], ident_f32[:])
+            return planes
+
+        def regroup(planes, copy):
+            grouped = stage.tile([P, PASSES * K_PASS], BF16, align_bytes=64, tag="grouped", bufs=6)
             copy(
-                out=grouped[:].bitcast(F32).rearrange("p g (c v) -> p g c v", v=2),
+                out=grouped[:].bitcast(F32).rearrange("p (g c v) -> p g c v", g=PASSES, v=2),
                 in_=planes[:].rearrange("p (g v) c -> p g c v", v=2),
             )
             return grouped
 
-        k_grouped = []
-        for r in range(NT):
-            copy = nc.vector.tensor_copy if r % 2 == 0 else nc.scalar.copy
-            k_grouped.append(regroup_input_tile(k_sb, r, copy))
-            if r >= 1:
-                quantise_tile(k_grouped[r - 1], k_codes, k_scales, r - 1)
-        quantise_tile(k_grouped[NT - 1], k_codes, k_scales, NT - 1)
+        def transpose_q(r):
+            return transpose_words(q_sb[:].bitcast(F32)[:, r, :])
 
+        def transpose_u(u_tile):
+            return transpose_words(u_tile[:].bitcast(F32))
+
+        u_tiles = {}
         sum_sq = stats.tile([P, NT], F32)
         inv_norm = stats.tile([P, NT], F32)
-        u_sb = resident.tile([P, NT, FEAT], BF16)
 
         def sum_squares(r):
             squares = junk.tile([P, FEAT], BF16, tag="squares")
@@ -164,112 +169,45 @@ def tile_selfattention_pa_kernel(tc, x, q, k, out_0, out_1, out_2, out_3, out_4)
                 out=inv_norm[:, col], in0=inv_norm[:, col], in1=minus_half[:], op=ALU.pow
             )
 
-        def scale_x_tile(r):
+        def scale_x(r):
+            u_tiles[r] = stage.tile([P, FEAT], BF16, name="u_tile", tag="u_tile")
             nc.vector.tensor_scalar_mul(
-                out=u_sb[:, r, :], in0=x_sb[:, r, :], scalar1=inv_norm[:, r : r + 1]
+                out=u_tiles[r][:], in0=x_sb[:, r, :], scalar1=inv_norm[:, r : r + 1]
             )
 
-        def transpose_u_tile(r):
-            planes = psum_t.tile([P, 4 * PASSES, P], BF16, tag="t")
-            for j in range(4 * PASSES):
-                nc.tensor.transpose(planes[:, j, :], u_sb[:, r, P * j : P * (j + 1)], ident_bf16[:])
-            return planes
-
-        def regroup_u_tile(planes):
-            grouped = stage.tile([P, PASSES, K_PASS], BF16, align_bytes=64, tag="grouped", bufs=6)
-            nc.scalar.copy(
-                out=grouped[:].rearrange("p g (c t) -> p g c t", t=4),
-                in_=planes[:].rearrange("p (g t) c -> p g c t", t=4),
+        def scale_x_on_gpsimd(r):
+            u_tiles[r] = stage.tile([P, FEAT], BF16, name="u_tile", tag="u_tile")
+            nc.gpsimd.tensor_scalar(
+                out=u_tiles[r][:], in0=x_sb[:, r, :], scalar1=inv_norm[:, r : r + 1], scalar2=0.0,
+                op0=ALU.mult, op1=ALU.add,
             )
-            return grouped
 
-        def product_tile(a_codes, a_scales, b_codes, b_scales, r):
-            rows = slice(P * r, P * (r + 1))
-            banks = []
-            for h in range(HALVES):
-                cols = slice(BANK * h, BANK * (h + 1))
-                bank = psum_mm.tile([P, BANK], F32, name="bank%d" % h, tag="bank%d" % h)
-                for g in range(PASSES):
-                    nc.tensor.matmul_mx(
-                        out=bank[:],
-                        lhsT=a_codes[:, g, rows].bitcast(FP8X4),
-                        lhsT_scale=a_scales[:, g, rows],
-                        rhs=b_codes[:, g, cols].bitcast(FP8X4),
-                        rhs_scale=b_scales[:, g, cols],
-                        start=(g == 0),
-                        stop=(g == PASSES - 1),
-                    )
-                banks.append(bank)
-            return banks
+        banks = {}
 
-        e_all = resident.tile([P, NT, T], F32)
-        e_keep = resident.tile([P, NT, WIN], F32)
-        max_halves = stats.tile([P, NT * HALVES], F32)
-        neg_max = stats.tile([P, NT], F32)
-        z_halves = stats.tile([P, NT * HALVES], F32)
-        s_halves = stats.tile([P, NT * HALVES], F32)
-        neg_max_win = stats.tile([P, NT], F32)
-        z_win = stats.tile([P, NT], F32)
-        s_win = stats.tile([P, NT], F32)
-
-        def maxima(r, banks):
-            for h in range(HALVES):
-                nc.vector.tensor_reduce(
-                    out=max_halves[:, HALVES * r + h : HALVES * r + h + 1], in_=banks[h][:],
-                    axis=AX.X, op=ALU.max,
+        def product(j, h):
+            bank = psum_mm.tile([P, BANK], F32, name="bank%d" % h, tag="bank%d" % h)
+            cols = slice(BANK * h, BANK * (h + 1))
+            for g in range(PASSES):
+                if j < NT:
+                    rows = slice(P * g, P * (g + 1))
+                    lhs, lhs_scale = q_codes[:, j, rows], q_scales[:, j, rows]
+                    rhs, rhs_scale = k_codes[:, g, cols], k_scales[:, g, cols]
+                else:
+                    rows = slice(P * (j - NT), P * (j - NT + 1))
+                    lhs, lhs_scale = u_codes[:, g, rows], u_scales[:, g, rows]
+                    rhs, rhs_scale = u_codes[:, g, cols], u_scales[:, g, cols]
+                nc.tensor.matmul_mx(
+                    out=bank[:], lhsT=lhs.bitcast(FP8X4), lhsT_scale=lhs_scale,
+                    rhs=rhs.bitcast(FP8X4), rhs_scale=rhs_scale,
+                    start=(g == 0), stop=(g == PASSES - 1),
                 )
-            nc.vector.tensor_reduce(
-                out=neg_max[:, r : r + 1], in_=max_halves[:, HALVES * r : HALVES * (r + 1)],
-                axis=AX.X, op=ALU.max, negate=True,
-            )
-            logits = stage.tile([P, WIN], F32, tag="logits")
-            for h, first, last, w_first, w_last in window_pieces(r):
-                nc.vector.tensor_tensor(
-                    out=logits[:, w_first:w_last], in0=banks[h][:, first:last],
-                    in1=keep[:, r, w_first:w_last], op=ALU.mult,
-                )
-            nc.vector.tensor_reduce(
-                out=neg_max_win[:, r : r + 1], in_=logits[:], axis=AX.X, op=ALU.max, negate=True
-            )
-            return logits
+            banks[j, h] = bank
 
-        def exponentials(r, banks, logits):
-            for h in range(HALVES):
-                col = HALVES * r + h
-                nc.scalar.activation(
-                    out=e_all[:, r, BANK * h : BANK * (h + 1)], in_=banks[h][:], func=ACT.Exp,
-                    bias=neg_max[:, r : r + 1], accum_out=z_halves[:, col : col + 1],
-                )
-            e_win = stage.tile([P, WIN], F32, tag="e_win")
-            nc.scalar.activation(
-                out=e_win[:], in_=logits[:], func=ACT.Exp, bias=neg_max_win[:, r : r + 1],
-                accum_out=z_win[:, r : r + 1],
-            )
-            return e_win
-
-        def entropy_sums(r, banks, logits, e_win):
-            for h in range(HALVES):
-                col = HALVES * r + h
-                products = junk.tile([P, BANK], F32, tag="products")
-                nc.vector.scalar_tensor_tensor(
-                    out=products[:], in0=banks[h][:], scalar=neg_max[:, r : r + 1],
-                    in1=e_all[:, r, BANK * h : BANK * (h + 1)],
-                    op0=ALU.add, op1=ALU.mult, accum_out=s_halves[:, col : col + 1],
-                )
-            products = junk.tile([P, WIN], F32, tag="win_products")
-            nc.vector.scalar_tensor_tensor(
-                out=products[:], in0=logits[:], scalar=neg_max_win[:, r : r + 1], in1=e_win[:],
-                op0=ALU.add, op1=ALU.mult, accum_out=s_win[:, r : r + 1],
-            )
-
-        def split_by_keep(r):
-            window = e_all[:, r, WIN_STEP * r : WIN_STEP * r + WIN]
-            nc.gpsimd.tensor_tensor(out=e_keep[:, r, :], in0=window, in1=keep[:, r, 0:WIN], op=ALU.mult)
-            nc.gpsimd.tensor_tensor(out=window, in0=window, in1=e_keep[:, r, :], op=ALU.subtract)
+        accs = {}
 
         def gram_row_sums(r):
             rows = slice(P * r, P * (r + 1))
-            acc = psum_t.tile([P, P], F32, tag="t")
+            acc = psum_t.tile([P, P], F32, name="acc", tag="t")
             for g in range(PASSES):
                 for c in range(NT):
                     cols = slice(P * c, P * (c + 1))
@@ -282,160 +220,237 @@ def tile_selfattention_pa_kernel(tc, x, q, k, out_0, out_1, out_2, out_3, out_4)
                         start=(g == 0 and c == 0),
                         stop=(g == PASSES - 1 and c == NT - 1),
                     )
-            return acc
+            accs[r] = acc
 
-        Q_AHEAD = 3
-        ACC_AHEAD = 2
+        gram_sums = stats.tile([P, NT], F32)
 
-        def prepare_q_tile(r):
-            return regroup_input_tile(q_sb, r, nc.scalar.copy)
+        def finish_row_sums(r):
+            copied = junk.tile([P, P], F32, tag="copied")
+            nc.scalar.activation(
+                out=copied[:], in_=accs[r][:], func=ACT.Copy, accum_out=gram_sums[:, r : r + 1]
+            )
 
-        def energies(r):
-            return product_tile(q_codes, q_scales, k_codes, k_scales, r)
+        e_all = resident.tile([P, NT, T], F32)
+        e_win = resident.tile([P, NT, WIN], F32)
+        max_halves = stats.tile([P, NT * HALVES], F32)
+        neg_max = stats.tile([P, NT], F32)
+        z_halves = stats.tile([P, NT * HALVES], F32)
+        s_halves = stats.tile([P, NT * HALVES], F32)
+        neg_max_win = stats.tile([P, NT], F32)
+        z_win = stats.tile([P, NT], F32)
+        s_win = stats.tile([P, NT], F32)
+        logits = {}
 
-        for r in range(Q_AHEAD):
-            quantise_tile(prepare_q_tile(r), q_codes, q_scales, r)
-        banks = [energies(0), energies(1)]
-        for r in range(2):
+        def half_maximum(r, h):
+            col = HALVES * r + h
+            nc.vector.tensor_reduce(
+                out=max_halves[:, col : col + 1], in_=banks[r, h][:], axis=AX.X, op=ALU.max
+            )
+
+        def row_maximum(r):
+            nc.vector.tensor_reduce(
+                out=neg_max[:, r : r + 1], in_=max_halves[:, HALVES * r : HALVES * (r + 1)],
+                axis=AX.X, op=ALU.max, negate=True,
+            )
+
+        def window_logits(r):
+            logits[r] = resident.tile([P, WIN], F32, name="logits%d" % r)
+            for h, first, last, w_first, w_last in window_pieces(r):
+                nc.vector.tensor_tensor(
+                    out=logits[r][:, w_first:w_last], in0=banks[r, h][:, first:last],
+                    in1=outside[:, r, w_first:w_last], op=ALU.add,
+                )
+
+        def window_maximum(r):
+            nc.vector.tensor_reduce(
+                out=neg_max_win[:, r : r + 1], in_=logits[r][:], axis=AX.X, op=ALU.max, negate=True
+            )
+
+        def exponentials(r):
+            for h in range(HALVES):
+                col = HALVES * r + h
+                nc.scalar.activation(
+                    out=e_all[:, r, BANK * h : BANK * (h + 1)], in_=banks[r, h][:], func=ACT.Exp,
+                    bias=neg_max[:, r : r + 1], accum_out=z_halves[:, col : col + 1],
+                )
+
+        def window_exponentials(r):
+            nc.scalar.activation(
+                out=e_win[:, r, :], in_=logits[r][:], func=ACT.Exp, bias=neg_max_win[:, r : r + 1],
+                accum_out=z_win[:, r : r + 1],
+            )
+
+        def entropy_sum(r, h):
+            col = HALVES * r + h
+            products = junk.tile([P, BANK], F32, tag="products")
+            nc.vector.scalar_tensor_tensor(
+                out=products[:], in0=banks[r, h][:], scalar=neg_max[:, r : r + 1],
+                in1=e_all[:, r, BANK * h : BANK * (h + 1)],
+                op0=ALU.add, op1=ALU.mult, accum_out=s_halves[:, col : col + 1],
+            )
+
+        def window_entropy_sum(r):
+            products = junk.tile([P, WIN], F32, tag="win_products")
+            nc.vector.scalar_tensor_tensor(
+                out=products[:], in0=logits[r][:], scalar=neg_max_win[:, r : r + 1],
+                in1=e_win[:, r, :], op0=ALU.add, op1=ALU.mult, accum_out=s_win[:, r : r + 1],
+            )
+
+        def clear_blocks(r):
+            window = e_all[:, r, WIN_STEP * r : WIN_STEP * r + WIN]
+            nc.gpsimd.tensor_tensor(out=window, in0=window, in1=zero[:, r, 0:WIN], op=ALU.mult)
+
+        k_words = k_sb[:].bitcast(F32)
+        k_grouped, q_planes, u_planes, q_grouped, u_grouped = {}, {}, {}, {}, {}
+        on_scalar, on_vector = nc.scalar.copy, nc.vector.tensor_copy
+
+        for r in range(X_EARLY):
             sum_squares(r)
             inverse_norm(r)
-        scale_x_tile(0)
-        u_planes = transpose_u_tile(0)
-        logits = [maxima(0, banks[0])]
-        accs = []
-        for r in range(NT):
-            e_win = exponentials(r, banks[r], logits[r])
-            if r + 1 < NT:
-                logits.append(maxima(r + 1, banks[r + 1]))
-            entropy_sums(r, banks[r], logits[r], e_win)
-            split_by_keep(r)
-            if r + 2 < NT:
-                banks.append(energies(r + 2))
-            if r + Q_AHEAD < NT:
-                q_grouped = prepare_q_tile(r + Q_AHEAD)
-            u_grouped = regroup_u_tile(u_planes)
-            if r + Q_AHEAD < NT:
-                quantise_tile(q_grouped, q_codes, q_scales, r + Q_AHEAD)
-            quantise_tile(u_grouped, u_codes, u_scales, r)
-            if r + 1 < NT:
-                scale_x_tile(r + 1)
-                u_planes = transpose_u_tile(r + 1)
-            if r + 2 < NT:
-                sum_squares(r + 2)
-                inverse_norm(r + 2)
-        next_banks = product_tile(u_codes, u_scales, u_codes, u_scales, 0)
-        for tile_index in range(ACC_AHEAD):
-            accs.append(gram_row_sums(tile_index))
+        nc.gpsimd.affine_select(
+            out=outside4[:], in_=outside4[:], compare_op=ALU.is_ge, fill=-HUGE,
+            base=BLOCK - 1, channel_multiplier=-1,
+            pattern=[[-ROW_SHIFT, NT], [BLOCK, WIN_BLOCKS], [0, BLOCK]],
+        )
+        nc.gpsimd.affine_select(
+            out=outside_count[:], in_=outside_count[:], compare_op=ALU.is_ge,
+            fill=float(T - LAST_BLOCK), base=T - LAST_BLOCK - 1, channel_multiplier=-1,
+            pattern=[[-P, NT]],
+        )
 
+        for r in range(NT):
+            k_grouped[r] = regroup(
+                transpose_words(k_words[:, r, :]), on_vector if r % 2 == 0 else on_scalar
+            )
+            if r == 0:
+                scale_x(0)
+            if r == 2:
+                scale_x(1)
+                u_planes[0] = transpose_u(u_tiles[0])
+            if r >= 1:
+                quantise_tile(k_grouped[r - 1], k_codes, k_scales, r - 1)
+            if r == 3:
+                u_grouped[0] = regroup(u_planes[0], on_scalar)
+                u_planes[1] = transpose_u(u_tiles[1])
+            if r == 5:
+                u_grouped[1] = regroup(u_planes[1], on_scalar)
+                quantise_tile(u_grouped[0], u_codes, u_scales, 0)
+        q_planes[0] = transpose_q(0)
+        q_planes[1] = transpose_q(1)
+        q_grouped[0] = regroup(q_planes[0], on_scalar)
+        quantise_tile(k_grouped[NT - 1], k_codes, k_scales, NT - 1)
+        q_grouped[1] = regroup(q_planes[1], on_scalar)
+        quantise_tile(u_grouped[1], u_codes, u_scales, 1)
+        quantise_q_tile(q_grouped[0], 0)
+        for h in range(HALVES):
+            product(0, h)
+        sum_squares(2)
+        inverse_norm(2)
+        q_planes[2] = transpose_q(2)
+        quantise_q_tile(q_grouped[1], 1)
+        q_grouped[2] = regroup(q_planes[2], on_scalar)
+        half_maximum(0, 0)
+        for h in range(HALVES):
+            product(1, h)
+        half_maximum(0, 1)
+        window_logits(0)
+        row_maximum(0)
+        scale_x(2)
+        exponentials(0)
+        u_planes[2] = transpose_u(u_tiles[2])
+        q_planes[3] = transpose_q(3)
+        quantise_q_tile(q_grouped[2], 2)
+        window_maximum(0)
+        sum_squares(3)
+        inverse_norm(3)
+        scale_x_on_gpsimd(3)
+        u_grouped[2] = regroup(u_planes[2], on_scalar)
+        u_planes[3] = transpose_u(u_tiles[3])
+        nc.gpsimd.tensor_scalar(
+            out=keep4[:], in0=outside4[:], scalar1=1.0 / HUGE, scalar2=1.0, op0=ALU.mult, op1=ALU.add
+        )
+
+        diffs = stats.tile([P, 3, NT], F32)
+        exps = stats.tile([P, 3, NT], F32)
         z_both = stats.tile([P, 2 * NT], F32)
         s_both = stats.tile([P, 2 * NT], F32)
         inv_z_both = stats.tile([P, 2 * NT], F32)
         neg_inv_z = stats.tile([P, NT], F32)
-        e_of_zero = stats.tile([P, NT], F32)
-        s_of_zero = stats.tile([P, NT], F32)
-        whole, window = slice(0, NT), slice(NT, 2 * NT)
-        nc.scalar.activation(out=e_of_zero[:], in_=neg_max_win[:], func=ACT.Exp)
-        nc.vector.tensor_reduce(
-            out=z_both[:, whole], in_=z_halves[:].rearrange("p (r h) -> p r h", h=HALVES),
-            axis=AX.X, op=ALU.add,
-        )
-        nc.vector.tensor_reduce(
-            out=s_both[:, whole], in_=s_halves[:].rearrange("p (r h) -> p r h", h=HALVES),
-            axis=AX.X, op=ALU.add,
-        )
-        nc.vector.reciprocal(out=inv_z_both[:, whole], in_=z_both[:, whole])
-        nc.vector.scalar_tensor_tensor(
-            out=z_both[:, window], in0=e_of_zero[:], scalar=float(T - WIN), in1=z_win[:],
-            op0=ALU.mult, op1=ALU.add,
-        )
-        nc.vector.tensor_scalar_mul(out=neg_inv_z[:], in0=inv_z_both[:, whole], scalar1=-1.0)
-        nc.vector.tensor_mul(out=s_of_zero[:], in0=e_of_zero[:], in1=neg_max_win[:])
-        nc.vector.reciprocal(out=inv_z_both[:, window], in_=z_both[:, window])
-        nc.vector.scalar_tensor_tensor(
-            out=s_both[:, window], in0=s_of_zero[:], scalar=float(T - WIN), in1=s_win[:],
-            op0=ALU.mult, op1=ALU.add,
-        )
-
-        gram_sums = stats.tile([P, NT], F32)
-        ln_parts = stats.tile([P, NT, 2], F32)
         ln_z_both = stats.tile([P, 2 * NT], F32)
-        att_keep = resident.tile([P, NT, WIN], F32)
-        nc.scalar.activation(out=ln_z_both[:], in_=z_both[:], func=ACT.Ln)
-
-        def total_over_tokens(partial):
-            total_ps = psum_t.tile([P, 1], F32, tag="t")
-            nc.tensor.matmul(out=total_ps[:], lhsT=ones[:], rhs=partial, start=True, stop=True)
-            return total_ps
-
-        def entropy_outputs():
-            entropy_both = stats.tile([P, 2 * NT], F32)
-            abs_entropy = stats.tile([P, NT], F32)
-            abs_sum = stats.tile([P, 1], F32)
-            inv_total = stats.tile([P, 1], F32)
-            nc.vector.tensor_mul(out=entropy_both[:], in0=s_both[:], in1=inv_z_both[:])
-            nc.vector.tensor_sub(out=entropy_both[:], in0=ln_z_both[:], in1=entropy_both[:])
-            nc.vector.tensor_scalar_mul(out=entropy_both[:], in0=entropy_both[:], scalar1=1.0 / LN_T)
-            nc.scalar.activation(
-                out=abs_entropy[:], in_=entropy_both[:, whole], func=ACT.Abs, accum_out=abs_sum[:]
-            )
-            nc.vector.tensor_copy(
-                out=vectors[:, COL_ENT_WIN : COL_ENT_WIN + NT], in_=entropy_both[:, window]
-            )
-            total_ps = total_over_tokens(abs_sum[:])
-            nc.vector.tensor_scalar_max(out=inv_total[:], in0=total_ps[:], scalar1=EPS)
-            nc.vector.reciprocal(out=inv_total[:], in_=inv_total[:])
-            nc.vector.tensor_scalar_mul(
-                out=vectors[:, COL_ENT : COL_ENT + NT], in0=entropy_both[:, whole], scalar1=inv_total[:]
-            )
-
-        sums = stats.tile([P, 2, NT], F32)
-        numer = stats.tile([P, NT], F32)
-        denom = stats.tile([P, NT], F32)
-        dep_rows = []
-
-        def dep_factor_of(first, last):
-            tiles = slice(first, last)
-            nc.vector.tensor_reduce(
-                out=sums[:, :, tiles], in_=minus_d_sums[:, :, tiles, :], axis=AX.X, op=ALU.add
-            )
-            nc.vector.scalar_tensor_tensor(
-                out=denom[:, tiles], in0=sums[:, 1, tiles], scalar=float(T), in1=gram_sums[:, tiles],
-                op0=ALU.add, op1=ALU.subtract,
-            )
-            nc.vector.tensor_mul(out=numer[:, tiles], in0=sums[:, 0, tiles], in1=neg_inv_z[:, tiles])
-            nc.vector.reciprocal(out=denom[:, tiles], in_=denom[:, tiles])
-            nc.vector.tensor_mul(
-                out=vectors[:, COL_DEP + first : COL_DEP + last], in0=numer[:, tiles], in1=denom[:, tiles]
-            )
-            for tile_index in range(first, last):
-                h, i = divmod(tile_index, BANK // P)
-                nc.tensor.matmul(
-                    out=dep_rows[h][:, P * i : P * (i + 1)],
-                    lhsT=vectors[:, COL_DEP + tile_index : COL_DEP + tile_index + 1].to_broadcast([P, P]),
-                    rhs=ident_f32[:], start=True, stop=True,
-                )
-
-        def finish_window(r):
-            dep_keep = stage.tile([P, WIN], F32, tag="dep_keep")
-            for h, first, last, w_first, w_last in window_pieces(r):
-                nc.vector.tensor_tensor(
-                    out=dep_keep[:, w_first:w_last], in0=dep_rows[h][:, first:last],
-                    in1=keep[:, r, w_first:w_last], op=ALU.mult,
-                )
-            att_win = stage.tile([P, WIN], F32, tag="att_win")
-            nc.gpsimd.tensor_tensor(out=att_win[:], in0=dep_keep[:], in1=att_keep[:, r, :], op=ALU.add)
-            lo = WIN_STEP * r
-            nc.sync.dma_start(out=out_0[P * r : P * (r + 1), lo : lo + WIN], in_=att_win[:])
-
-        FIRST_BATCH = 6
-        FIRST_WINDOWS = (P * FIRST_BATCH - WIN) // WIN_STEP + 1
+        win_factor = stats.tile([P, NT], F32)
+        neg_win_factor = stats.tile([P, NT], F32)
+        rest = stats.tile([P, NT], F32)
+        whole, window = slice(0, NT), slice(NT, 2 * NT)
+        z_pairs = z_halves[:].rearrange("p (r h) -> p r h", h=HALVES)
+        s_pairs = s_halves[:].rearrange("p (r h) -> p r h", h=HALVES)
 
         for r in range(NT):
-            banks = next_banks
+            if r + 4 < NT:
+                sum_squares(r + 4)
+                inverse_norm(r + 4)
+                scale_x_on_gpsimd(r + 4)
+            if r + 3 < NT:
+                q_grouped[r + 3] = regroup(q_planes[r + 3], on_scalar)
+                u_grouped[r + 3] = regroup(u_planes[r + 3], on_scalar)
+            if r == 1:
+                nc.gpsimd.tensor_scalar(
+                    out=zero4[:], in0=outside4[:], scalar1=-1.0 / HUGE, scalar2=0.0,
+                    op0=ALU.mult, op1=ALU.add,
+                )
+            for h in range(HALVES):
+                if r + 1 < NT:
+                    half_maximum(r + 1, h)
+                    if h == 1:
+                        window_logits(r + 1)
+                        row_maximum(r + 1)
+                if (r, h) == (0, 0):
+                    quantise_tile(u_grouped[2], u_codes, u_scales, 2)
+                if r >= NT - 3:
+                    gram_row_sums(2 * (r - NT + 3) + h)
+                entropy_sum(r, h)
+                product(r + 2, h)
             if r + 1 < NT:
-                next_banks = product_tile(u_codes, u_scales, u_codes, u_scales, r + 1)
-            if r + ACC_AHEAD < NT:
-                accs.append(gram_row_sums(r + ACC_AHEAD))
+                exponentials(r + 1)
+            else:
+                nc.vector.tensor_add(
+                    out=z_both[:, whole], in0=z_pairs[:, :, 0], in1=z_pairs[:, :, 1]
+                )
+            if r + 3 < NT:
+                quantise_q_tile(q_grouped[r + 3], r + 3)
+            if r + 1 < NT:
+                window_maximum(r + 1)
+            if r >= NT // 2:
+                for i in range(2):
+                    window_exponentials(2 * r - NT + i)
+            if r + 4 < NT:
+                q_planes[r + 4] = transpose_q(r + 4)
+                u_planes[r + 4] = transpose_u(u_tiles[r + 4])
+            if r + 3 < NT:
+                quantise_tile(u_grouped[r + 3], u_codes, u_scales, r + 3)
+            if r >= NT - 3:
+                clear_blocks(r - NT + 3)
+                if r < NT - 1:
+                    for i in range(2):
+                        finish_row_sums(2 * (r - NT + 3) + i)
+
+        nc.vector.reciprocal(out=inv_z_both[:, whole], in_=z_both[:, whole])
+        nc.gpsimd.tensor_sub(out=diffs[:, 0, :], in0=neg_max[:], in1=neg_max_win[:])
+        nc.gpsimd.tensor_scalar_min(out=diffs[:, 2, :], in0=neg_max_win[:], scalar1=0.0)
+        nc.gpsimd.tensor_sub(out=diffs[:, 1, :], in0=diffs[:, 2, :], in1=neg_max_win[:])
+        nc.scalar.activation(out=exps[:], in_=diffs[:], func=ACT.Exp)
+        for i in range(4, 6):
+            finish_row_sums(i)
+        nc.gpsimd.tensor_mul(out=win_factor[:], in0=exps[:, 0, :], in1=inv_z_both[:, whole])
+        nc.gpsimd.tensor_scalar_mul(out=neg_win_factor[:], in0=win_factor[:], scalar1=-1.0)
+        nc.gpsimd.tensor_mul(out=rest[:], in0=exps[:, 2, :], in1=outside_count[:])
+        nc.gpsimd.tensor_mul(out=z_both[:, window], in0=z_win[:], in1=exps[:, 1, :])
+        nc.gpsimd.tensor_mul(out=s_both[:, window], in0=z_both[:, window], in1=diffs[:, 1, :])
+        nc.gpsimd.tensor_add(out=z_both[:, window], in0=z_both[:, window], in1=rest[:])
+
+        ln_parts = stats.tile([P, NT, 2], F32)
+        att_keep = resident.tile([P, NT, WIN], F32)
+
+        def logs_of_rest(r):
             logs = junk.tile([P, T], F32, tag="logs", bufs=2)
             nc.scalar.activation(
                 out=logs[:], in_=e_all[:, r, :], func=ACT.Ln, scale=neg_inv_z[:, r : r + 1], bias=1.0,
@@ -443,51 +458,219 @@ def tile_selfattention_pa_kernel(tc, x, q, k, out_0, out_1, out_2, out_3, out_4)
             )
             win_logs = junk.tile([P, WIN], F32, tag="win_logs")
             nc.scalar.activation(
-                out=win_logs[:], in_=e_keep[:, r, :], func=ACT.Ln, scale=neg_inv_z[:, r : r + 1], bias=1.0,
-                accum_out=ln_parts[:, r, 1:2],
+                out=win_logs[:], in_=e_win[:, r, :], func=ACT.Ln, scale=neg_win_factor[:, r : r + 1],
+                bias=1.0, accum_out=ln_parts[:, r, 1:2],
             )
-            nc.vector.tensor_scalar_mul(
-                out=att_keep[:, r, :], in0=e_keep[:, r, :], scalar1=inv_z_both[:, r : r + 1]
+
+        def attention_in_blocks(r):
+            nc.gpsimd.tensor_scalar(
+                out=att_keep[:, r, :], in0=e_win[:, r, :], scalar1=win_factor[:, r : r + 1],
+                scalar2=0.0, op0=ALU.mult, op1=ALU.add,
             )
-            nc.vector.tensor_reduce(out=gram_sums[:, r : r + 1], in_=accs[r][:], axis=AX.X, op=ALU.add)
-            for h in range(HALVES):
-                products = junk.tile([P, BANK], F32, tag="products")
-                nc.vector.scalar_tensor_tensor(
-                    out=products[:], in0=banks[h][:], scalar=-1.0,
-                    in1=e_all[:, r, BANK * h : BANK * (h + 1)],
-                    op0=ALU.add, op1=ALU.mult, accum_out=minus_d_sums[:, 0, r, h : h + 1],
-                )
+
+        def window_diversity(r):
             for i, (h, first, last, w_first, w_last) in enumerate(window_pieces(r)):
                 products = junk.tile([P, WIN], F32, tag="win_products")
                 nc.vector.scalar_tensor_tensor(
-                    out=products[:, w_first:w_last], in0=banks[h][:, first:last], scalar=-1.0,
+                    out=products[:, w_first:w_last], in0=banks[NT + r, h][:, first:last], scalar=-1.0,
                     in1=keep[:, r, w_first:w_last], op0=ALU.add, op1=ALU.mult,
                     accum_out=minus_d_sums[:, 1, r, i : i + 1],
                 )
-            if r == 0:
-                entropy_outputs()
-            if r + 1 == FIRST_BATCH:
-                for h in range(HALVES):
-                    dep_rows.append(psum_t.tile([P, BANK], F32, name="dep_rows%d" % h, tag="t"))
-                dep_factor_of(0, FIRST_BATCH)
-            if r == FIRST_BATCH:
-                for w in range(FIRST_WINDOWS):
-                    finish_window(w)
+
+        def weighted_diversity(r, h):
+            products = junk.tile([P, BANK], F32, tag="products")
+            nc.vector.scalar_tensor_tensor(
+                out=products[:], in0=banks[NT + r, h][:], scalar=-1.0,
+                in1=e_all[:, r, BANK * h : BANK * (h + 1)],
+                op0=ALU.add, op1=ALU.mult, accum_out=minus_d_sums[:, 0, r, h : h + 1],
+            )
+
+        def total_over_tokens(partial, columns):
+            total_ps = psum_t.tile([P, NT], F32, name="total_ps", tag="t")
+            nc.tensor.matmul(
+                out=total_ps[:, 0:columns], lhsT=ones[:], rhs=partial, start=True, stop=True
+            )
+            return total_ps
+
+        entropy_both = stats.tile([P, 2 * NT], F32)
+        abs_entropy = stats.tile([P, NT], F32)
+        abs_sum = stats.tile([P, 1], F32)
+        inv_total = stats.tile([P, 1], F32)
+
+        def window_entropy_parts():
+            nc.gpsimd.tensor_mul(out=s_win[:], in0=s_win[:], in1=exps[:, 1, :])
+            nc.gpsimd.tensor_mul(out=rest[:], in0=rest[:], in1=diffs[:, 2, :])
+            nc.gpsimd.tensor_add(out=s_win[:], in0=s_win[:], in1=rest[:])
+            nc.gpsimd.tensor_add(out=s_both[:, window], in0=s_both[:, window], in1=s_win[:])
+
+        def entropies():
+            nc.gpsimd.tensor_mul(out=entropy_both[:], in0=s_both[:], in1=inv_z_both[:])
+            nc.gpsimd.tensor_sub(out=entropy_both[:], in0=ln_z_both[:], in1=entropy_both[:])
+            nc.gpsimd.tensor_scalar_mul(out=entropy_both[:], in0=entropy_both[:], scalar1=1.0 / LN_T)
+            nc.gpsimd.tensor_copy(
+                out=vectors[:, COL_ENT_WIN : COL_ENT_WIN + NT], in_=entropy_both[:, window]
+            )
+            nc.scalar.activation(
+                out=abs_entropy[:], in_=entropy_both[:, whole], func=ACT.Abs, accum_out=abs_sum[:]
+            )
+
+        win_sums = stats.tile([P, NT], F32)
+        denom = stats.tile([P, NT], F32)
+        numer = stats.tile([P, NT], F32)
+        dep_coef = stats.tile([P, NT], F32)
+        segments = [slice(0, 4), slice(4, 7), slice(7, 8)]
+        dep_rows = {}
+
+        def window_sums(tiles):
+            nc.vector.tensor_add(
+                out=win_sums[:, tiles], in0=minus_d_sums[:, 1, tiles, 0], in1=minus_d_sums[:, 1, tiles, 1]
+            )
+
+        def denominators(tiles):
+            nc.vector.scalar_tensor_tensor(
+                out=denom[:, tiles], in0=win_sums[:, tiles], scalar=float(T), in1=gram_sums[:, tiles],
+                op0=ALU.add, op1=ALU.subtract,
+            )
+
+        def inverse_denominators(tiles):
+            nc.vector.reciprocal(out=denom[:, tiles], in_=denom[:, tiles])
+
+        def dep_coefficients(tiles):
+            nc.vector.tensor_mul(
+                out=dep_coef[:, tiles], in0=denom[:, tiles], in1=neg_inv_z[:, tiles]
+            )
+
+        def numerators(tiles):
+            nc.vector.tensor_add(
+                out=numer[:, tiles], in0=minus_d_sums[:, 0, tiles, 0], in1=minus_d_sums[:, 0, tiles, 1]
+            )
+
+        def dep_factors(tiles):
+            cols = slice(COL_DEP + tiles.start, COL_DEP + tiles.stop)
+            nc.vector.tensor_mul(out=vectors[:, cols], in0=numer[:, tiles], in1=dep_coef[:, tiles])
+
+        def dep_factor_of_last_tile():
+            last = slice(NT - 1, NT)
+            nc.vector.tensor_scalar(
+                out=vectors[:, COL_DEP + NT - 1 : COL_DEP + NT], in0=minus_d_sums[:, 0, NT - 1, 0:1],
+                scalar1=minus_d_sums[:, 0, NT - 1, 1:2], scalar2=dep_coef[:, last],
+                op0=ALU.add, op1=ALU.mult,
+            )
+
+        def spread_dep_factor(s):
+            tiles = segments[s]
+            dep_rows[s] = psum_t.tile([P, BANK], F32, name="dep_rows", tag="t")
+            for j in range(tiles.start, tiles.stop):
+                i = j - tiles.start
+                nc.tensor.matmul(
+                    out=dep_rows[s][:, P * i : P * (i + 1)],
+                    lhsT=vectors[:, COL_DEP + j : COL_DEP + j + 1].to_broadcast([P, P]),
+                    rhs=ident_f32[:], start=True, stop=True,
+                )
+
+        dep_keeps = {}
+
+        def window_dep_factor(r, s):
+            lo = WIN_STEP * r
+            seg_first, seg_last = P * segments[s].start, P * segments[s].stop
+            first, last = max(lo, seg_first), min(lo + WIN, seg_last)
+            if r not in dep_keeps:
+                dep_keeps[r] = stage.tile([P, WIN], F32, name="dep_keep", tag="dep_keep", bufs=NT)
+            nc.vector.tensor_tensor(
+                out=dep_keeps[r][:, first - lo : last - lo],
+                in0=dep_rows[s][:, first - seg_first : last - seg_first],
+                in1=keep[:, r, first - lo : last - lo], op=ALU.mult,
+            )
+
+        def finish_window(r, add):
+            att_win = stage.tile([P, WIN], F32, tag="att_win", bufs=6)
+            add(out=att_win[:], in0=dep_keeps[r][:], in1=att_keep[:, r, :], op=ALU.add)
+            lo = WIN_STEP * r
+            nc.sync.dma_start(out=out_0[P * r : P * (r + 1), lo : lo + WIN], in_=att_win[:])
 
         ln_sums = stats.tile([P, NT], F32)
         div_h = stats.tile([P, NT], F32)
         div_sum = stats.tile([P, 1], F32)
         inv_div_total = stats.tile([P, 1], F32)
-        nc.vector.tensor_reduce(out=ln_sums[:], in_=ln_parts[:], axis=AX.X, op=ALU.add)
-        nc.scalar.activation(out=div_h[:], in_=ln_sums[:], func=ACT.Exp, accum_out=div_sum[:])
-        dep_factor_of(FIRST_BATCH, NT)
-        div_total_ps = total_over_tokens(div_sum[:])
-        for w in range(FIRST_WINDOWS, NT):
-            finish_window(w)
-        nc.vector.reciprocal(out=inv_div_total[:], in_=div_total_ps[:])
+
+        window_diversity(0)
+        nc.vector.tensor_scalar_mul(out=neg_inv_z[:], in0=inv_z_both[:, whole], scalar1=-1.0)
+        for r in range(NT):
+            logs_of_rest(r)
+            attention_in_blocks(r)
+            if r + 3 < NT:
+                clear_blocks(r + 3)
+            if r == 5:
+                dep_coefficients(segments[0])
+            weighted_diversity(r, 0)
+            if r + 2 < NT:
+                product(NT + r + 2, 0)
+            if r + 1 < NT:
+                window_diversity(r + 1)
+            if r < NT // 2:
+                window_entropy_sum(2 * r)
+                window_entropy_sum(2 * r + 1)
+            if r == 1:
+                nc.vector.reciprocal(out=inv_z_both[:, window], in_=z_both[:, window])
+            if r == 2:
+                nc.vector.tensor_add(
+                    out=s_both[:, whole], in0=s_pairs[:, :, 0], in1=s_pairs[:, :, 1]
+                )
+                nc.scalar.activation(out=ln_z_both[:], in_=z_both[:], func=ACT.Ln)
+            if r == 4:
+                window_sums(segments[0])
+                window_entropy_parts()
+                entropies()
+                total_ps = total_over_tokens(abs_sum[:], 1)
+            if r == 5:
+                dep_factors(segments[0])
+                spread_dep_factor(0)
+            if r == 7:
+                inverse_denominators(slice(4, 8))
+                numerators(segments[1])
+                nc.vector.tensor_reduce(out=ln_sums[:], in_=ln_parts[:], axis=AX.X, op=ALU.add)
+                nc.scalar.activation(out=div_h[:], in_=ln_sums[:], func=ACT.Exp, accum_out=div_sum[:])
+                dep_coefficients(slice(4, 8))
+                dep_factors(segments[1])
+                spread_dep_factor(1)
+            weighted_diversity(r, 1)
+            if r + 2 < NT:
+                product(NT + r + 2, 1)
+            if r < 2:
+                gram_row_sums(r + 6)
+                finish_row_sums(r + 6)
+            if r == 4:
+                denominators(segments[0])
+                numerators(segments[0])
+                inverse_denominators(segments[0])
+            if r == 6:
+                window_sums(slice(4, 8))
+                nc.vector.tensor_scalar_max(out=inv_total[:], in0=total_ps[:, 0:1], scalar1=EPS)
+                for w in range(3):
+                    window_dep_factor(w, 0)
+                    finish_window(w, nc.gpsimd.tensor_tensor)
+                denominators(slice(4, 8))
+                nc.vector.reciprocal(out=inv_total[:], in_=inv_total[:])
+                nc.gpsimd.tensor_scalar_mul(
+                    out=vectors[:, COL_ENT : COL_ENT + NT], in0=entropy_both[:, whole], scalar1=inv_total[:]
+                )
+        window_dep_factor(3, 0)
+        div_total_ps = total_over_tokens(div_sum[:], 1)
+        dep_factor_of_last_tile()
+        spread_dep_factor(2)
+        window_dep_factor(4, 0)
+        for w in range(3, NT):
+            window_dep_factor(w, 1)
+            if w < 6:
+                finish_window(w, nc.gpsimd.tensor_tensor)
+        nc.vector.reciprocal(out=inv_div_total[:], in_=div_total_ps[:, 0:1])
+        for w in range(6, NT):
+            window_dep_factor(w, 2)
         nc.vector.tensor_scalar_mul(
             out=vectors[:, COL_DIV : COL_DIV + NT], in0=div_h[:], scalar1=inv_div_total[:]
         )
+        for w in range(6, NT):
+            finish_window(w, nc.vector.tensor_tensor)
 
         vectors_t_ps = psum_t.tile([P, P], F32, tag="t")
         nc.tensor.transpose(vectors_t_ps[:], vectors[:], ident_f32[:])

@@ -78,8 +78,22 @@ def tile_selfattention_pa_kernel(tc, x, q, k, out_0, out_1, out_2, out_3, out_4)
 
         ident_f32 = const.tile([P, P], F32)
         make_identity(nc, ident_f32[:])
+        inside = const.tile([P, NT, WIN_BLOCKS], F32)
+        nc.gpsimd.memset(inside[:], 0.0)
+        nc.gpsimd.affine_select(
+            out=inside[:], in_=inside[:], compare_op=ALU.is_ge, fill=-HUGE,
+            base=0, channel_multiplier=1, pattern=[[ROW_SHIFT, NT], [-BLOCK, WIN_BLOCKS]],
+        )
+        nc.gpsimd.affine_select(
+            out=inside[:], in_=inside[:], compare_op=ALU.is_ge, fill=-HUGE,
+            base=BLOCK - 1, channel_multiplier=-1, pattern=[[-ROW_SHIFT, NT], [BLOCK, WIN_BLOCKS]],
+        )
         outside4 = const.tile([P, NT, WIN_BLOCKS, BLOCK], F32)
-        nc.vector.memset(outside4[:], 0.0)
+        nc.scalar.copy(
+            out=outside4[:], in_=inside[:].unsqueeze(3).to_broadcast([P, NT, WIN_BLOCKS, BLOCK])
+        )
+        outside = outside4[:].rearrange("p r b c -> p r (b c)")
+        keep = const.tile([P, NT, WIN], F32)
         minus_half = const.tile([P, 1], F32)
         nc.vector.memset(minus_half[:], -0.5)
         minus_d_sums = stats.tile([P, 2, NT, HALVES], F32)
@@ -87,21 +101,16 @@ def tile_selfattention_pa_kernel(tc, x, q, k, out_0, out_1, out_2, out_3, out_4)
         vectors = stats.tile([P, P], F32)
         nc.vector.memset(vectors[:], 0.0)
         zeros = const.tile([P, T - WIN], F32)
-        nc.gpsimd.memset(zeros[:], 0.0)
+        nc.vector.memset(zeros[:], 0.0)
         ones = const.tile([P, P], F32)
-        nc.gpsimd.memset(ones[:], 1.0)
+        nc.vector.memset(ones[:], 1.0)
         outside_count = const.tile([P, NT], F32)
         nc.gpsimd.memset(outside_count[:], float(T - BLOCK))
         nc.gpsimd.affine_select(
-            out=outside4[:], in_=outside4[:], compare_op=ALU.is_ge, fill=-HUGE,
-            base=0, channel_multiplier=1,
-            pattern=[[ROW_SHIFT, NT], [-BLOCK, WIN_BLOCKS], [0, BLOCK]],
+            out=outside_count[:], in_=outside_count[:], compare_op=ALU.is_ge,
+            fill=float(T - LAST_BLOCK), base=T - LAST_BLOCK - 1, channel_multiplier=-1,
+            pattern=[[-P, NT]],
         )
-        keep4 = const.tile([P, NT, WIN_BLOCKS, BLOCK], F32)
-        zero4 = const.tile([P, NT, WIN_BLOCKS, BLOCK], F32)
-        outside = outside4[:].rearrange("p r b c -> p r (b c)")
-        keep = keep4[:].rearrange("p r b c -> p r (b c)")
-        zero = zero4[:].rearrange("p r b c -> p r (b c)")
 
         for r in range(NT):
             rows = slice(P * r, P * (r + 1))
@@ -173,13 +182,6 @@ def tile_selfattention_pa_kernel(tc, x, q, k, out_0, out_1, out_2, out_3, out_4)
             u_tiles[r] = stage.tile([P, FEAT], BF16, name="u_tile", tag="u_tile")
             nc.vector.tensor_scalar_mul(
                 out=u_tiles[r][:], in0=x_sb[:, r, :], scalar1=inv_norm[:, r : r + 1]
-            )
-
-        def scale_x_on_gpsimd(r):
-            u_tiles[r] = stage.tile([P, FEAT], BF16, name="u_tile", tag="u_tile")
-            nc.gpsimd.tensor_scalar(
-                out=u_tiles[r][:], in0=x_sb[:, r, :], scalar1=inv_norm[:, r : r + 1], scalar2=0.0,
-                op0=ALU.mult, op1=ALU.add,
             )
 
         banks = {}
@@ -298,7 +300,9 @@ def tile_selfattention_pa_kernel(tc, x, q, k, out_0, out_1, out_2, out_3, out_4)
 
         def clear_blocks(r):
             window = e_all[:, r, WIN_STEP * r : WIN_STEP * r + WIN]
-            nc.gpsimd.tensor_tensor(out=window, in0=window, in1=zero[:, r, 0:WIN], op=ALU.mult)
+            nc.vector.scalar_tensor_tensor(
+                out=window, in0=outside[:, r, 0:WIN], scalar=0.0, in1=window, op0=ALU.is_lt, op1=ALU.mult
+            )
 
         k_words = k_sb[:].bitcast(F32)
         k_grouped, q_planes, u_planes, q_grouped, u_grouped = {}, {}, {}, {}, {}
@@ -307,16 +311,6 @@ def tile_selfattention_pa_kernel(tc, x, q, k, out_0, out_1, out_2, out_3, out_4)
         for r in range(X_EARLY):
             sum_squares(r)
             inverse_norm(r)
-        nc.gpsimd.affine_select(
-            out=outside4[:], in_=outside4[:], compare_op=ALU.is_ge, fill=-HUGE,
-            base=BLOCK - 1, channel_multiplier=-1,
-            pattern=[[-ROW_SHIFT, NT], [BLOCK, WIN_BLOCKS], [0, BLOCK]],
-        )
-        nc.gpsimd.affine_select(
-            out=outside_count[:], in_=outside_count[:], compare_op=ALU.is_ge,
-            fill=float(T - LAST_BLOCK), base=T - LAST_BLOCK - 1, channel_multiplier=-1,
-            pattern=[[-P, NT]],
-        )
 
         for r in range(NT):
             k_grouped[r] = regroup(
@@ -363,12 +357,7 @@ def tile_selfattention_pa_kernel(tc, x, q, k, out_0, out_1, out_2, out_3, out_4)
         window_maximum(0)
         sum_squares(3)
         inverse_norm(3)
-        scale_x_on_gpsimd(3)
         u_grouped[2] = regroup(u_planes[2], on_scalar)
-        u_planes[3] = transpose_u(u_tiles[3])
-        nc.gpsimd.tensor_scalar(
-            out=keep4[:], in0=outside4[:], scalar1=1.0 / HUGE, scalar2=1.0, op0=ALU.mult, op1=ALU.add
-        )
 
         diffs = stats.tile([P, 3, NT], F32)
         exps = stats.tile([P, 3, NT], F32)
@@ -388,14 +377,13 @@ def tile_selfattention_pa_kernel(tc, x, q, k, out_0, out_1, out_2, out_3, out_4)
             if r + 4 < NT:
                 sum_squares(r + 4)
                 inverse_norm(r + 4)
-                scale_x_on_gpsimd(r + 4)
             if r + 3 < NT:
                 q_grouped[r + 3] = regroup(q_planes[r + 3], on_scalar)
+            if 1 <= r < NT - 3:
                 u_grouped[r + 3] = regroup(u_planes[r + 3], on_scalar)
-            if r == 1:
-                nc.gpsimd.tensor_scalar(
-                    out=zero4[:], in0=outside4[:], scalar1=-1.0 / HUGE, scalar2=0.0,
-                    op0=ALU.mult, op1=ALU.add,
+            if r == NT - 3:
+                nc.scalar.activation(
+                    out=keep[:], in_=outside[:, :, 0:WIN], func=ACT.Copy, scale=1.0 / HUGE, bias=1.0
                 )
             for h in range(HALVES):
                 if r + 1 < NT:
@@ -405,6 +393,9 @@ def tile_selfattention_pa_kernel(tc, x, q, k, out_0, out_1, out_2, out_3, out_4)
                         row_maximum(r + 1)
                 if (r, h) == (0, 0):
                     quantise_tile(u_grouped[2], u_codes, u_scales, 2)
+                    scale_x(3)
+                    u_planes[3] = transpose_u(u_tiles[3])
+                    u_grouped[3] = regroup(u_planes[3], on_scalar)
                 if r >= NT - 3:
                     gram_row_sums(2 * (r - NT + 3) + h)
                 entropy_sum(r, h)
@@ -424,14 +415,15 @@ def tile_selfattention_pa_kernel(tc, x, q, k, out_0, out_1, out_2, out_3, out_4)
                     window_exponentials(2 * r - NT + i)
             if r + 4 < NT:
                 q_planes[r + 4] = transpose_q(r + 4)
+                scale_x(r + 4)
                 u_planes[r + 4] = transpose_u(u_tiles[r + 4])
             if r + 3 < NT:
                 quantise_tile(u_grouped[r + 3], u_codes, u_scales, r + 3)
-            if r >= NT - 3:
-                clear_blocks(r - NT + 3)
-                if r < NT - 1:
-                    for i in range(2):
-                        finish_row_sums(2 * (r - NT + 3) + i)
+            if NT - 3 <= r < NT - 1:
+                for i in range(2):
+                    finish_row_sums(2 * (r - NT + 3) + i)
+            if r == NT - 1:
+                clear_blocks(0)
 
         nc.vector.reciprocal(out=inv_z_both[:, whole], in_=z_both[:, whole])
         nc.gpsimd.tensor_sub(out=diffs[:, 0, :], in0=neg_max[:], in1=neg_max_win[:])
@@ -448,7 +440,6 @@ def tile_selfattention_pa_kernel(tc, x, q, k, out_0, out_1, out_2, out_3, out_4)
         nc.gpsimd.tensor_add(out=z_both[:, window], in0=z_both[:, window], in1=rest[:])
 
         ln_parts = stats.tile([P, NT, 2], F32)
-        att_keep = resident.tile([P, NT, WIN], F32)
 
         def logs_of_rest(r):
             logs = junk.tile([P, T], F32, tag="logs", bufs=2)
@@ -460,12 +451,6 @@ def tile_selfattention_pa_kernel(tc, x, q, k, out_0, out_1, out_2, out_3, out_4)
             nc.scalar.activation(
                 out=win_logs[:], in_=e_win[:, r, :], func=ACT.Ln, scale=neg_win_factor[:, r : r + 1],
                 bias=1.0, accum_out=ln_parts[:, r, 1:2],
-            )
-
-        def attention_in_blocks(r):
-            nc.gpsimd.tensor_scalar(
-                out=att_keep[:, r, :], in0=e_win[:, r, :], scalar1=win_factor[:, r : r + 1],
-                scalar2=0.0, op0=ALU.mult, op1=ALU.add,
             )
 
         def window_diversity(r):
@@ -582,9 +567,12 @@ def tile_selfattention_pa_kernel(tc, x, q, k, out_0, out_1, out_2, out_3, out_4)
                 in1=keep[:, r, first - lo : last - lo], op=ALU.mult,
             )
 
-        def finish_window(r, add):
-            att_win = stage.tile([P, WIN], F32, tag="att_win", bufs=6)
-            add(out=att_win[:], in0=dep_keeps[r][:], in1=att_keep[:, r, :], op=ALU.add)
+        def finish_window(r):
+            att_win = stage.tile([P, WIN], F32, tag="att_win", bufs=NT)
+            nc.vector.scalar_tensor_tensor(
+                out=att_win[:], in0=e_win[:, r, :], scalar=win_factor[:, r : r + 1],
+                in1=dep_keeps[r][:], op0=ALU.mult, op1=ALU.add,
+            )
             lo = WIN_STEP * r
             nc.sync.dma_start(out=out_0[P * r : P * (r + 1), lo : lo + WIN], in_=att_win[:])
 
@@ -597,11 +585,8 @@ def tile_selfattention_pa_kernel(tc, x, q, k, out_0, out_1, out_2, out_3, out_4)
         nc.vector.tensor_scalar_mul(out=neg_inv_z[:], in0=inv_z_both[:, whole], scalar1=-1.0)
         for r in range(NT):
             logs_of_rest(r)
-            attention_in_blocks(r)
-            if r + 3 < NT:
-                clear_blocks(r + 3)
-            if r == 5:
-                dep_coefficients(segments[0])
+            if r + 1 < NT:
+                clear_blocks(r + 1)
             weighted_diversity(r, 0)
             if r + 2 < NT:
                 product(NT + r + 2, 0)
@@ -623,8 +608,7 @@ def tile_selfattention_pa_kernel(tc, x, q, k, out_0, out_1, out_2, out_3, out_4)
                 entropies()
                 total_ps = total_over_tokens(abs_sum[:], 1)
             if r == 5:
-                dep_factors(segments[0])
-                spread_dep_factor(0)
+                dep_coefficients(segments[0])
             if r == 7:
                 inverse_denominators(slice(4, 8))
                 numerators(segments[1])
@@ -643,13 +627,17 @@ def tile_selfattention_pa_kernel(tc, x, q, k, out_0, out_1, out_2, out_3, out_4)
                 denominators(segments[0])
                 numerators(segments[0])
                 inverse_denominators(segments[0])
+            if r == 5:
+                dep_factors(segments[0])
+                spread_dep_factor(0)
             if r == 6:
                 window_sums(slice(4, 8))
                 nc.vector.tensor_scalar_max(out=inv_total[:], in0=total_ps[:, 0:1], scalar1=EPS)
                 for w in range(3):
                     window_dep_factor(w, 0)
-                    finish_window(w, nc.gpsimd.tensor_tensor)
                 denominators(slice(4, 8))
+                for w in range(3):
+                    finish_window(w)
                 nc.vector.reciprocal(out=inv_total[:], in_=inv_total[:])
                 nc.gpsimd.tensor_scalar_mul(
                     out=vectors[:, COL_ENT : COL_ENT + NT], in0=entropy_both[:, whole], scalar1=inv_total[:]
@@ -661,16 +649,14 @@ def tile_selfattention_pa_kernel(tc, x, q, k, out_0, out_1, out_2, out_3, out_4)
         window_dep_factor(4, 0)
         for w in range(3, NT):
             window_dep_factor(w, 1)
-            if w < 6:
-                finish_window(w, nc.gpsimd.tensor_tensor)
         nc.vector.reciprocal(out=inv_div_total[:], in_=div_total_ps[:, 0:1])
         for w in range(6, NT):
             window_dep_factor(w, 2)
         nc.vector.tensor_scalar_mul(
             out=vectors[:, COL_DIV : COL_DIV + NT], in0=div_h[:], scalar1=inv_div_total[:]
         )
-        for w in range(6, NT):
-            finish_window(w, nc.vector.tensor_tensor)
+        for w in range(NT - 1, 2, -1):
+            finish_window(w)
 
         vectors_t_ps = psum_t.tile([P, P], F32, tag="t")
         nc.tensor.transpose(vectors_t_ps[:], vectors[:], ident_f32[:])

@@ -28,12 +28,14 @@ WIN_STEP = 2 * BLOCK
 WIN = T - WIN_STEP * (NT - 1)
 WIN_BLOCKS = 4
 ROW_SHIFT = P - WIN_STEP
+WARM_UPS = 8
 LAST_BLOCK = T % BLOCK
 HUGE = 2.0**100
 
 FLOPS = 2 * 2 * T * T * FEAT
 
 COL_ENT_WIN, COL_DIV, COL_ENT, COL_DEP = 0, NT, 2 * NT, 3 * NT
+COL_DEP_LAST = 4 * NT
 
 
 def window_pieces(r):
@@ -94,6 +96,7 @@ def tile_selfattention_pa_kernel(tc, x, q, k, out_0, out_1, out_2, out_3, out_4)
         )
         outside = outside4[:].rearrange("p r b c -> p r (b c)")
         keep = const.tile([P, NT, WIN], F32)
+        not_keep = const.tile([P, NT, WIN], F32)
         minus_half = const.tile([P, 1], F32)
         nc.vector.memset(minus_half[:], -0.5)
         minus_d_sums = stats.tile([P, 2, NT, HALVES], F32)
@@ -300,11 +303,13 @@ def tile_selfattention_pa_kernel(tc, x, q, k, out_0, out_1, out_2, out_3, out_4)
 
         def clear_blocks(r):
             window = e_all[:, r, WIN_STEP * r : WIN_STEP * r + WIN]
-            nc.vector.scalar_tensor_tensor(
-                out=window, in0=outside[:, r, 0:WIN], scalar=0.0, in1=window, op0=ALU.is_lt, op1=ALU.mult
-            )
+            nc.gpsimd.tensor_mul(out=window, in0=window, in1=not_keep[:, r, :])
 
         k_words = k_sb[:].bitcast(F32)
+        warm = psum_t.tile([P, P], F32, tag="t")
+        for i in range(WARM_UPS):
+            nc.tensor.matmul(out=warm[:], lhsT=ident_f32[:], rhs=ident_f32[:], start=True, stop=True)
+
         k_grouped, q_planes, u_planes, q_grouped, u_grouped = {}, {}, {}, {}, {}
         on_scalar, on_vector = nc.scalar.copy, nc.vector.tensor_copy
 
@@ -383,6 +388,10 @@ def tile_selfattention_pa_kernel(tc, x, q, k, out_0, out_1, out_2, out_3, out_4)
                 u_grouped[r + 3] = regroup(u_planes[r + 3], on_scalar)
             if r == NT - 3:
                 nc.scalar.activation(
+                    out=not_keep[:], in_=outside[:, :, 0:WIN], func=ACT.Copy, scale=-1.0 / HUGE
+                )
+            if r == NT - 2:
+                nc.scalar.activation(
                     out=keep[:], in_=outside[:, :, 0:WIN], func=ACT.Copy, scale=1.0 / HUGE, bias=1.0
                 )
             for h in range(HALVES):
@@ -391,15 +400,15 @@ def tile_selfattention_pa_kernel(tc, x, q, k, out_0, out_1, out_2, out_3, out_4)
                     if h == 1:
                         window_logits(r + 1)
                         row_maximum(r + 1)
+                if r >= NT - 3:
+                    gram_row_sums(2 * (r - NT + 3) + h)
+                entropy_sum(r, h)
+                product(r + 2, h)
                 if (r, h) == (0, 0):
                     quantise_tile(u_grouped[2], u_codes, u_scales, 2)
                     scale_x(3)
                     u_planes[3] = transpose_u(u_tiles[3])
                     u_grouped[3] = regroup(u_planes[3], on_scalar)
-                if r >= NT - 3:
-                    gram_row_sums(2 * (r - NT + 3) + h)
-                entropy_sum(r, h)
-                product(r + 2, h)
             if r + 1 < NT:
                 exponentials(r + 1)
             else:
@@ -410,6 +419,9 @@ def tile_selfattention_pa_kernel(tc, x, q, k, out_0, out_1, out_2, out_3, out_4)
                 quantise_q_tile(q_grouped[r + 3], r + 3)
             if r + 1 < NT:
                 window_maximum(r + 1)
+            if r > NT // 2:
+                for i in range(2):
+                    window_entropy_sum(2 * r - NT - 2 + i)
             if r >= NT // 2:
                 for i in range(2):
                     window_exponentials(2 * r - NT + i)
@@ -424,14 +436,13 @@ def tile_selfattention_pa_kernel(tc, x, q, k, out_0, out_1, out_2, out_3, out_4)
                     finish_row_sums(2 * (r - NT + 3) + i)
             if r == NT - 1:
                 clear_blocks(0)
+                clear_blocks(1)
 
         nc.vector.reciprocal(out=inv_z_both[:, whole], in_=z_both[:, whole])
         nc.gpsimd.tensor_sub(out=diffs[:, 0, :], in0=neg_max[:], in1=neg_max_win[:])
         nc.gpsimd.tensor_scalar_min(out=diffs[:, 2, :], in0=neg_max_win[:], scalar1=0.0)
         nc.gpsimd.tensor_sub(out=diffs[:, 1, :], in0=diffs[:, 2, :], in1=neg_max_win[:])
         nc.scalar.activation(out=exps[:], in_=diffs[:], func=ACT.Exp)
-        for i in range(4, 6):
-            finish_row_sums(i)
         nc.gpsimd.tensor_mul(out=win_factor[:], in0=exps[:, 0, :], in1=inv_z_both[:, whole])
         nc.gpsimd.tensor_scalar_mul(out=neg_win_factor[:], in0=win_factor[:], scalar1=-1.0)
         nc.gpsimd.tensor_mul(out=rest[:], in0=exps[:, 2, :], in1=outside_count[:])
@@ -507,37 +518,35 @@ def tile_selfattention_pa_kernel(tc, x, q, k, out_0, out_1, out_2, out_3, out_4)
         dep_rows = {}
 
         def window_sums(tiles):
-            nc.vector.tensor_add(
+            nc.gpsimd.tensor_add(
                 out=win_sums[:, tiles], in0=minus_d_sums[:, 1, tiles, 0], in1=minus_d_sums[:, 1, tiles, 1]
             )
 
         def denominators(tiles):
-            nc.vector.scalar_tensor_tensor(
-                out=denom[:, tiles], in0=win_sums[:, tiles], scalar=float(T), in1=gram_sums[:, tiles],
-                op0=ALU.add, op1=ALU.subtract,
-            )
+            nc.gpsimd.tensor_sub(out=denom[:, tiles], in0=win_sums[:, tiles], in1=gram_sums[:, tiles])
+            nc.gpsimd.tensor_scalar_add(out=denom[:, tiles], in0=denom[:, tiles], scalar1=float(T))
 
         def inverse_denominators(tiles):
             nc.vector.reciprocal(out=denom[:, tiles], in_=denom[:, tiles])
 
         def dep_coefficients(tiles):
-            nc.vector.tensor_mul(
+            nc.gpsimd.tensor_mul(
                 out=dep_coef[:, tiles], in0=denom[:, tiles], in1=neg_inv_z[:, tiles]
             )
 
         def numerators(tiles):
-            nc.vector.tensor_add(
+            nc.gpsimd.tensor_add(
                 out=numer[:, tiles], in0=minus_d_sums[:, 0, tiles, 0], in1=minus_d_sums[:, 0, tiles, 1]
             )
 
         def dep_factors(tiles):
             cols = slice(COL_DEP + tiles.start, COL_DEP + tiles.stop)
-            nc.vector.tensor_mul(out=vectors[:, cols], in0=numer[:, tiles], in1=dep_coef[:, tiles])
+            nc.gpsimd.tensor_mul(out=vectors[:, cols], in0=numer[:, tiles], in1=dep_coef[:, tiles])
 
         def dep_factor_of_last_tile():
             last = slice(NT - 1, NT)
             nc.vector.tensor_scalar(
-                out=vectors[:, COL_DEP + NT - 1 : COL_DEP + NT], in0=minus_d_sums[:, 0, NT - 1, 0:1],
+                out=vectors[:, COL_DEP_LAST : COL_DEP_LAST + 1], in0=minus_d_sums[:, 0, NT - 1, 0:1],
                 scalar1=minus_d_sums[:, 0, NT - 1, 1:2], scalar2=dep_coef[:, last],
                 op0=ALU.add, op1=ALU.mult,
             )
@@ -547,34 +556,31 @@ def tile_selfattention_pa_kernel(tc, x, q, k, out_0, out_1, out_2, out_3, out_4)
             dep_rows[s] = psum_t.tile([P, BANK], F32, name="dep_rows", tag="t")
             for j in range(tiles.start, tiles.stop):
                 i = j - tiles.start
-                nc.tensor.matmul(
-                    out=dep_rows[s][:, P * i : P * (i + 1)],
-                    lhsT=vectors[:, COL_DEP + j : COL_DEP + j + 1].to_broadcast([P, P]),
-                    rhs=ident_f32[:], start=True, stop=True,
+                col = COL_DEP_LAST if j == NT - 1 else COL_DEP + j
+                nc.tensor.transpose(
+                    dep_rows[s][:, P * i : P * (i + 1)],
+                    vectors[:, col : col + 1].to_broadcast([P, P]), ident_f32[:],
                 )
 
-        dep_keeps = {}
+        att_wins = {}
 
-        def window_dep_factor(r, s):
+        def add_dep_factor(r, s):
             lo = WIN_STEP * r
             seg_first, seg_last = P * segments[s].start, P * segments[s].stop
             first, last = max(lo, seg_first), min(lo + WIN, seg_last)
-            if r not in dep_keeps:
-                dep_keeps[r] = stage.tile([P, WIN], F32, name="dep_keep", tag="dep_keep", bufs=NT)
-            nc.vector.tensor_tensor(
-                out=dep_keeps[r][:, first - lo : last - lo],
-                in0=dep_rows[s][:, first - seg_first : last - seg_first],
-                in1=keep[:, r, first - lo : last - lo], op=ALU.mult,
+            if r not in att_wins:
+                att_wins[r] = stage.tile([P, WIN], F32, name="att_win", tag="att_win", bufs=NT)
+            nc.vector.scalar_tensor_tensor(
+                out=att_wins[r][:, first - lo : last - lo],
+                in0=e_win[:, r, first - lo : last - lo], scalar=win_factor[:, r : r + 1],
+                in1=dep_rows[s][:, first - seg_first : last - seg_first],
+                op0=ALU.mult, op1=ALU.add,
             )
 
-        def finish_window(r):
-            att_win = stage.tile([P, WIN], F32, tag="att_win", bufs=NT)
-            nc.vector.scalar_tensor_tensor(
-                out=att_win[:], in0=e_win[:, r, :], scalar=win_factor[:, r : r + 1],
-                in1=dep_keeps[r][:], op0=ALU.mult, op1=ALU.add,
-            )
+        def finish_window(r, engine):
+            engine.tensor_mul(out=att_wins[r][:], in0=att_wins[r][:], in1=keep[:, r, :])
             lo = WIN_STEP * r
-            nc.sync.dma_start(out=out_0[P * r : P * (r + 1), lo : lo + WIN], in_=att_win[:])
+            nc.sync.dma_start(out=out_0[P * r : P * (r + 1), lo : lo + WIN], in_=att_wins[r][:])
 
         ln_sums = stats.tile([P, NT], F32)
         div_h = stats.tile([P, NT], F32)
@@ -582,87 +588,94 @@ def tile_selfattention_pa_kernel(tc, x, q, k, out_0, out_1, out_2, out_3, out_4)
         inv_div_total = stats.tile([P, 1], F32)
 
         window_diversity(0)
+        for r in range(NT - 2, NT):
+            window_entropy_sum(r)
         nc.vector.tensor_scalar_mul(out=neg_inv_z[:], in0=inv_z_both[:, whole], scalar1=-1.0)
         for r in range(NT):
             logs_of_rest(r)
-            if r + 1 < NT:
-                clear_blocks(r + 1)
+            if r + 2 < NT:
+                clear_blocks(r + 2)
+            if r == 5:
+                inverse_denominators(segments[0])
+                dep_coefficients(segments[0])
+                dep_factors(segments[0])
             weighted_diversity(r, 0)
             if r + 2 < NT:
                 product(NT + r + 2, 0)
-            if r + 1 < NT:
-                window_diversity(r + 1)
-            if r < NT // 2:
-                window_entropy_sum(2 * r)
-                window_entropy_sum(2 * r + 1)
-            if r == 1:
-                nc.vector.reciprocal(out=inv_z_both[:, window], in_=z_both[:, window])
-            if r == 2:
-                nc.vector.tensor_add(
-                    out=s_both[:, whole], in0=s_pairs[:, :, 0], in1=s_pairs[:, :, 1]
-                )
-                nc.scalar.activation(out=ln_z_both[:], in_=z_both[:], func=ACT.Ln)
-            if r == 4:
-                window_sums(segments[0])
-                window_entropy_parts()
-                entropies()
-                total_ps = total_over_tokens(abs_sum[:], 1)
             if r == 5:
-                dep_coefficients(segments[0])
+                spread_dep_factor(0)
             if r == 7:
                 inverse_denominators(slice(4, 8))
-                numerators(segments[1])
-                nc.vector.tensor_reduce(out=ln_sums[:], in_=ln_parts[:], axis=AX.X, op=ALU.add)
-                nc.scalar.activation(out=div_h[:], in_=ln_sums[:], func=ACT.Exp, accum_out=div_sum[:])
                 dep_coefficients(slice(4, 8))
                 dep_factors(segments[1])
                 spread_dep_factor(1)
+                for w in range(1, 3):
+                    finish_window(w, nc.gpsimd)
             weighted_diversity(r, 1)
             if r + 2 < NT:
                 product(NT + r + 2, 1)
             if r < 2:
                 gram_row_sums(r + 6)
-                finish_row_sums(r + 6)
-            if r == 4:
+            if r < 4:
+                finish_row_sums(r + 4)
+            if r + 1 < NT:
+                window_diversity(r + 1)
+            if r == 1:
+                nc.vector.reciprocal(out=inv_z_both[:, window], in_=z_both[:, window])
+                nc.gpsimd.tensor_add(
+                    out=s_both[:, whole], in0=s_pairs[:, :, 0], in1=s_pairs[:, :, 1]
+                )
+            if r == 2:
+                nc.scalar.activation(out=ln_z_both[:], in_=z_both[:], func=ACT.Ln)
+                window_entropy_parts()
+            if r == 3:
+                window_sums(segments[0])
                 denominators(segments[0])
                 numerators(segments[0])
-                inverse_denominators(segments[0])
+            if r == 4:
+                entropies()
             if r == 5:
-                dep_factors(segments[0])
-                spread_dep_factor(0)
+                total_ps = total_over_tokens(abs_sum[:], 1)
             if r == 6:
                 window_sums(slice(4, 8))
-                nc.vector.tensor_scalar_max(out=inv_total[:], in0=total_ps[:, 0:1], scalar1=EPS)
-                for w in range(3):
-                    window_dep_factor(w, 0)
                 denominators(slice(4, 8))
+                numerators(segments[1])
                 for w in range(3):
-                    finish_window(w)
-                nc.vector.reciprocal(out=inv_total[:], in_=inv_total[:])
-                nc.gpsimd.tensor_scalar_mul(
-                    out=vectors[:, COL_ENT : COL_ENT + NT], in0=entropy_both[:, whole], scalar1=inv_total[:]
-                )
-        window_dep_factor(3, 0)
-        div_total_ps = total_over_tokens(div_sum[:], 1)
+                    add_dep_factor(w, 0)
+                finish_window(0, nc.gpsimd)
+                nc.vector.tensor_scalar_max(out=inv_total[:], in0=total_ps[:, 0:1], scalar1=EPS)
+        nc.vector.reciprocal(out=inv_total[:], in_=inv_total[:])
+        nc.gpsimd.tensor_scalar_mul(
+            out=vectors[:, COL_ENT : COL_ENT + NT], in0=entropy_both[:, whole], scalar1=inv_total[:]
+        )
+        add_dep_factor(3, 0)
+        add_dep_factor(4, 0)
         dep_factor_of_last_tile()
         spread_dep_factor(2)
-        window_dep_factor(4, 0)
+        nc.vector.tensor_reduce(out=ln_sums[:], in_=ln_parts[:], axis=AX.X, op=ALU.add)
+        nc.scalar.activation(out=div_h[:], in_=ln_sums[:], func=ACT.Exp, accum_out=div_sum[:])
+        div_total_ps = total_over_tokens(div_sum[:], 1)
         for w in range(3, NT):
-            window_dep_factor(w, 1)
+            add_dep_factor(w, 1)
+            if w < 6:
+                finish_window(w, nc.gpsimd)
+        for w in range(6, NT):
+            add_dep_factor(w, 2)
         nc.vector.reciprocal(out=inv_div_total[:], in_=div_total_ps[:, 0:1])
         for w in range(6, NT):
-            window_dep_factor(w, 2)
+            finish_window(w, nc.vector)
         nc.vector.tensor_scalar_mul(
             out=vectors[:, COL_DIV : COL_DIV + NT], in0=div_h[:], scalar1=inv_div_total[:]
         )
-        for w in range(NT - 1, 2, -1):
-            finish_window(w)
 
         vectors_t_ps = psum_t.tile([P, P], F32, tag="t")
         nc.tensor.transpose(vectors_t_ps[:], vectors[:], ident_f32[:])
         vectors_t = stats.tile([P, P], F32)
         nc.scalar.copy(out=vectors_t[:], in_=vectors_t_ps[:])
-        for out_vec, col in ((out_1, COL_ENT_WIN), (out_2, COL_DIV), (out_3, COL_ENT), (out_4, COL_DEP)):
+        for out_vec, col in ((out_1, COL_ENT_WIN), (out_2, COL_DIV), (out_3, COL_ENT)):
             nc.sync.dma_start(
                 out=out_vec.rearrange("(r p) -> r p", p=P), in_=vectors_t[col : col + NT, :]
             )
+        dep_out = out_4.rearrange("(r p) -> r p", p=P)
+        nc.sync.dma_start(out=dep_out[0 : NT - 1, :], in_=vectors_t[COL_DEP : COL_DEP + NT - 1, :])
+        nc.sync.dma_start(out=dep_out[NT - 1 : NT, :], in_=vectors_t[COL_DEP_LAST : COL_DEP_LAST + 1, :])

@@ -68,15 +68,30 @@ def tile_selfattention_pa_kernel(tc, x, q, k, out_0, out_1, out_2, out_3, out_4)
         def load(dst, src, r):
             nc.sync.dma_start(out=dst[:, r, :], in_=src[P * r : P * (r + 1), :])
 
-        X_EARLY = 2
-        for r in range(X_EARLY):
-            load(x_sb, x, r)
-        for r in range(NT):
-            load(k_sb, k, r)
-        for r in range(NT):
-            load(q_sb, q, r)
-            if 1 <= r < NT - 1:
-                load(x_sb, x, r + 1)
+        load(k_sb, k, 0)
+        load(k_sb, k, 1)
+        load(x_sb, x, 0)
+        load(k_sb, k, 2)
+        load(k_sb, k, 3)
+        load(q_sb, q, 0)
+        load(k_sb, k, 4)
+        load(k_sb, k, 5)
+        load(q_sb, q, 1)
+        load(k_sb, k, 6)
+        load(k_sb, k, 7)
+        load(x_sb, x, 1)
+        load(x_sb, x, 2)
+        load(q_sb, q, 2)
+        load(x_sb, x, 3)
+        load(q_sb, q, 3)
+        load(x_sb, x, 4)
+        load(q_sb, q, 4)
+        load(x_sb, x, 5)
+        load(q_sb, q, 5)
+        load(x_sb, x, 6)
+        load(q_sb, q, 6)
+        load(x_sb, x, 7)
+        load(q_sb, q, 7)
 
         ident_f32 = const.tile([P, P], F32)
         make_identity(nc, ident_f32[:])
@@ -95,18 +110,29 @@ def tile_selfattention_pa_kernel(tc, x, q, k, out_0, out_1, out_2, out_3, out_4)
             out=outside4[:], in_=inside[:].unsqueeze(3).to_broadcast([P, NT, WIN_BLOCKS, BLOCK])
         )
         outside = outside4[:].rearrange("p r b c -> p r (b c)")
-        keep = const.tile([P, NT, WIN], F32)
-        not_keep = const.tile([P, NT, WIN], F32)
+        keep4 = const.tile([P, NT, WIN_BLOCKS, BLOCK], F32)
+        not_keep4 = const.tile([P, NT, WIN_BLOCKS, BLOCK], F32)
+        keep = keep4[:].rearrange("p r b c -> p r (b c)")
+        not_keep = not_keep4[:].rearrange("p r b c -> p r (b c)")
+        inside_by_column = inside[:].unsqueeze(3).to_broadcast([P, NT, WIN_BLOCKS, BLOCK])
+        nc.gpsimd.tensor_scalar(
+            out=keep4[:], in0=inside_by_column, scalar1=1.0 / HUGE, scalar2=1.0,
+            op0=ALU.mult, op1=ALU.add,
+        )
+        nc.gpsimd.tensor_scalar(
+            out=not_keep4[:], in0=inside_by_column, scalar1=-1.0 / HUGE, scalar2=0.0,
+            op0=ALU.mult, op1=ALU.add,
+        )
         minus_half = const.tile([P, 1], F32)
-        nc.vector.memset(minus_half[:], -0.5)
+        nc.gpsimd.memset(minus_half[:], -0.5)
         minus_d_sums = stats.tile([P, 2, NT, HALVES], F32)
-        nc.vector.memset(minus_d_sums[:], 0.0)
+        nc.gpsimd.memset(minus_d_sums[:], 0.0)
         vectors = stats.tile([P, P], F32)
-        nc.vector.memset(vectors[:], 0.0)
+        nc.gpsimd.memset(vectors[:], 0.0)
         zeros = const.tile([P, T - WIN], F32)
-        nc.vector.memset(zeros[:], 0.0)
+        nc.gpsimd.memset(zeros[:], 0.0)
         ones = const.tile([P, P], F32)
-        nc.vector.memset(ones[:], 1.0)
+        nc.gpsimd.memset(ones[:], 1.0)
         outside_count = const.tile([P, NT], F32)
         nc.gpsimd.memset(outside_count[:], float(T - BLOCK))
         nc.gpsimd.affine_select(
@@ -208,76 +234,70 @@ def tile_selfattention_pa_kernel(tc, x, q, k, out_0, out_1, out_2, out_3, out_4)
                 )
             banks[j, h] = bank
 
+        gram_parts = stats.tile([P, 2, NT], F32)
         accs = {}
 
-        def gram_row_sums(r):
+        def gram_row_sums(r, part, blocks=NT // 2):
             rows = slice(P * r, P * (r + 1))
             acc = psum_t.tile([P, P], F32, name="acc", tag="t")
-            for g in range(PASSES):
-                for c in range(NT):
-                    cols = slice(P * c, P * (c + 1))
-                    nc.tensor.matmul_mx(
-                        out=acc[:],
-                        lhsT=u_codes[:, g, rows].bitcast(FP8X4),
-                        lhsT_scale=u_scales[:, g, rows],
-                        rhs=u_codes[:, g, cols].bitcast(FP8X4),
-                        rhs_scale=u_scales[:, g, cols],
-                        start=(g == 0 and c == 0),
-                        stop=(g == PASSES - 1 and c == NT - 1),
-                    )
-            accs[r] = acc
+            order = [(g, c) for g in range(PASSES) for c in range(part * (NT // 2), part * (NT // 2) + blocks)]
+            for i, (g, c) in enumerate(order):
+                cols = slice(P * c, P * (c + 1))
+                nc.tensor.matmul_mx(
+                    out=acc[:],
+                    lhsT=u_codes[:, g, rows].bitcast(FP8X4),
+                    lhsT_scale=u_scales[:, g, rows],
+                    rhs=u_codes[:, g, cols].bitcast(FP8X4),
+                    rhs_scale=u_scales[:, g, cols],
+                    start=(i == 0), stop=(i == len(order) - 1),
+                )
+            accs[r, part] = acc
 
-        gram_sums = stats.tile([P, NT], F32)
-
-        def finish_row_sums(r):
+        def finish_row_sums(r, part):
             copied = junk.tile([P, P], F32, tag="copied")
             nc.scalar.activation(
-                out=copied[:], in_=accs[r][:], func=ACT.Copy, accum_out=gram_sums[:, r : r + 1]
+                out=copied[:], in_=accs[r, part][:], func=ACT.Copy,
+                accum_out=gram_parts[:, part, r : r + 1],
             )
 
         e_all = resident.tile([P, NT, T], F32)
         e_win = resident.tile([P, NT, WIN], F32)
-        max_halves = stats.tile([P, NT * HALVES], F32)
-        neg_max = stats.tile([P, NT], F32)
-        z_halves = stats.tile([P, NT * HALVES], F32)
-        s_halves = stats.tile([P, NT * HALVES], F32)
+        neg_max_halves = stats.tile([P, HALVES * NT], F32)
+        z_halves = stats.tile([P, HALVES * NT], F32)
+        s_halves = stats.tile([P, HALVES * NT], F32)
         neg_max_win = stats.tile([P, NT], F32)
         z_win = stats.tile([P, NT], F32)
         s_win = stats.tile([P, NT], F32)
         logits = {}
 
         def half_maximum(r, h):
-            col = HALVES * r + h
+            col = NT * h + r
             nc.vector.tensor_reduce(
-                out=max_halves[:, col : col + 1], in_=banks[r, h][:], axis=AX.X, op=ALU.max
+                out=neg_max_halves[:, col : col + 1], in_=banks[r, h][:], axis=AX.X, op=ALU.max,
+                negate=True,
             )
 
-        def row_maximum(r):
-            nc.vector.tensor_reduce(
-                out=neg_max[:, r : r + 1], in_=max_halves[:, HALVES * r : HALVES * (r + 1)],
-                axis=AX.X, op=ALU.max, negate=True,
-            )
-
-        def window_logits(r):
-            logits[r] = resident.tile([P, WIN], F32, name="logits%d" % r)
-            for h, first, last, w_first, w_last in window_pieces(r):
-                nc.vector.tensor_tensor(
-                    out=logits[r][:, w_first:w_last], in0=banks[r, h][:, first:last],
-                    in1=outside[:, r, w_first:w_last], op=ALU.add,
-                )
+        def window_logits(r, h):
+            for piece_h, first, last, w_first, w_last in window_pieces(r):
+                if piece_h == h:
+                    if r not in logits:
+                        logits[r] = resident.tile([P, WIN], F32, name="logits%d" % r)
+                    nc.vector.tensor_tensor(
+                        out=logits[r][:, w_first:w_last], in0=banks[r, h][:, first:last],
+                        in1=outside[:, r, w_first:w_last], op=ALU.add,
+                    )
 
         def window_maximum(r):
             nc.vector.tensor_reduce(
                 out=neg_max_win[:, r : r + 1], in_=logits[r][:], axis=AX.X, op=ALU.max, negate=True
             )
 
-        def exponentials(r):
-            for h in range(HALVES):
-                col = HALVES * r + h
-                nc.scalar.activation(
-                    out=e_all[:, r, BANK * h : BANK * (h + 1)], in_=banks[r, h][:], func=ACT.Exp,
-                    bias=neg_max[:, r : r + 1], accum_out=z_halves[:, col : col + 1],
-                )
+        def exponentials(r, h):
+            col = NT * h + r
+            nc.scalar.activation(
+                out=e_all[:, r, BANK * h : BANK * (h + 1)], in_=banks[r, h][:], func=ACT.Exp,
+                bias=neg_max_halves[:, col : col + 1], accum_out=z_halves[:, col : col + 1],
+            )
 
         def window_exponentials(r):
             nc.scalar.activation(
@@ -286,10 +306,10 @@ def tile_selfattention_pa_kernel(tc, x, q, k, out_0, out_1, out_2, out_3, out_4)
             )
 
         def entropy_sum(r, h):
-            col = HALVES * r + h
+            col = NT * h + r
             products = junk.tile([P, BANK], F32, tag="products")
             nc.vector.scalar_tensor_tensor(
-                out=products[:], in0=banks[r, h][:], scalar=neg_max[:, r : r + 1],
+                out=products[:], in0=banks[r, h][:], scalar=neg_max_halves[:, col : col + 1],
                 in1=e_all[:, r, BANK * h : BANK * (h + 1)],
                 op0=ALU.add, op1=ALU.mult, accum_out=s_halves[:, col : col + 1],
             )
@@ -303,7 +323,7 @@ def tile_selfattention_pa_kernel(tc, x, q, k, out_0, out_1, out_2, out_3, out_4)
 
         def clear_blocks(r):
             window = e_all[:, r, WIN_STEP * r : WIN_STEP * r + WIN]
-            nc.gpsimd.tensor_mul(out=window, in0=window, in1=not_keep[:, r, :])
+            nc.gpsimd.tensor_mul(out=window, in0=window, in1=not_keep[:, r, 0:WIN])
 
         k_words = k_sb[:].bitcast(F32)
         warm = psum_t.tile([P, P], F32, tag="t")
@@ -313,155 +333,194 @@ def tile_selfattention_pa_kernel(tc, x, q, k, out_0, out_1, out_2, out_3, out_4)
         k_grouped, q_planes, u_planes, q_grouped, u_grouped = {}, {}, {}, {}, {}
         on_scalar, on_vector = nc.scalar.copy, nc.vector.tensor_copy
 
-        for r in range(X_EARLY):
-            sum_squares(r)
-            inverse_norm(r)
+        def bring_k(r, copy):
+            k_grouped[r] = regroup(transpose_words(k_words[:, r, :]), copy)
 
-        for r in range(NT):
-            k_grouped[r] = regroup(
-                transpose_words(k_words[:, r, :]), on_vector if r % 2 == 0 else on_scalar
-            )
-            if r == 0:
-                scale_x(0)
-            if r == 2:
-                scale_x(1)
-                u_planes[0] = transpose_u(u_tiles[0])
-            if r >= 1:
-                quantise_tile(k_grouped[r - 1], k_codes, k_scales, r - 1)
-            if r == 3:
-                u_grouped[0] = regroup(u_planes[0], on_scalar)
-                u_planes[1] = transpose_u(u_tiles[1])
-            if r == 5:
-                u_grouped[1] = regroup(u_planes[1], on_scalar)
-                quantise_tile(u_grouped[0], u_codes, u_scales, 0)
+        def quantise_k(r):
+            quantise_tile(k_grouped[r], k_codes, k_scales, r)
+
+        def bring_q(r, copy):
+            q_planes[r] = transpose_q(r)
+            q_grouped[r] = regroup(q_planes[r], copy)
+
+        k_planes = {}
+        k_planes[0] = transpose_words(k_words[:, 0, :])
+        k_planes[1] = transpose_words(k_words[:, 1, :])
+        k_grouped[0] = regroup(k_planes[0], on_vector)
+        k_grouped[1] = regroup(k_planes[1], on_scalar)
+        sum_squares(0)
+        k_planes[2] = transpose_words(k_words[:, 2, :])
+        quantise_k(0)
+        quantise_k(1)
+        k_grouped[2] = regroup(k_planes[2], on_vector)
+        k_planes[3] = transpose_words(k_words[:, 3, :])
+        k_grouped[3] = regroup(k_planes[3], on_scalar)
         q_planes[0] = transpose_q(0)
-        q_planes[1] = transpose_q(1)
         q_grouped[0] = regroup(q_planes[0], on_scalar)
-        quantise_tile(k_grouped[NT - 1], k_codes, k_scales, NT - 1)
-        q_grouped[1] = regroup(q_planes[1], on_scalar)
-        quantise_tile(u_grouped[1], u_codes, u_scales, 1)
+        inverse_norm(0)
+        quantise_k(2)
+        quantise_k(3)
+        k_planes[4] = transpose_words(k_words[:, 4, :])
         quantise_q_tile(q_grouped[0], 0)
-        for h in range(HALVES):
-            product(0, h)
-        sum_squares(2)
-        inverse_norm(2)
-        q_planes[2] = transpose_q(2)
+        k_grouped[4] = regroup(k_planes[4], on_vector)
+        k_planes[5] = transpose_words(k_words[:, 5, :])
+        k_grouped[5] = regroup(k_planes[5], on_scalar)
+        q_planes[1] = transpose_q(1)
+        q_grouped[1] = regroup(q_planes[1], on_scalar)
+        scale_x(0)
+        k_planes[6] = transpose_words(k_words[:, 6, :])
+        product(0, 0)
+        quantise_k(4)
         quantise_q_tile(q_grouped[1], 1)
-        q_grouped[2] = regroup(q_planes[2], on_scalar)
+        quantise_k(5)
+        k_grouped[6] = regroup(k_planes[6], on_scalar)
+        k_planes[7] = transpose_words(k_words[:, 7, :])
+        sum_squares(1)
+        k_grouped[7] = regroup(k_planes[7], on_scalar)
+        u_planes[0] = transpose_u(u_tiles[0])
+        u_grouped[0] = regroup(u_planes[0], on_scalar)
         half_maximum(0, 0)
-        for h in range(HALVES):
-            product(1, h)
-        half_maximum(0, 1)
-        window_logits(0)
-        row_maximum(0)
-        scale_x(2)
-        exponentials(0)
-        u_planes[2] = transpose_u(u_tiles[2])
-        q_planes[3] = transpose_q(3)
+        window_logits(0, 0)
+        product(1, 0)
+        exponentials(0, 0)
+        inverse_norm(1)
+        quantise_k(6)
+        quantise_k(7)
+        q_planes[2] = transpose_q(2)
+        q_grouped[2] = regroup(q_planes[2], on_scalar)
+        product(0, 1)
+        half_maximum(1, 0)
+        window_logits(1, 0)
+        exponentials(1, 0)
+        sum_squares(2)
+        product(1, 1)
+        entropy_sum(0, 0)
+        quantise_tile(u_grouped[0], u_codes, u_scales, 0)
         quantise_q_tile(q_grouped[2], 2)
+        inverse_norm(2)
+        product(2, 0)
+        half_maximum(0, 1)
+        window_logits(0, 1)
+        exponentials(0, 1)
         window_maximum(0)
-        sum_squares(3)
-        inverse_norm(3)
-        u_grouped[2] = regroup(u_planes[2], on_scalar)
+        scale_x(1)
+        u_planes[1] = transpose_u(u_tiles[1])
+        q_planes[3] = transpose_q(3)
 
-        diffs = stats.tile([P, 3, NT], F32)
-        exps = stats.tile([P, 3, NT], F32)
+        diffs = stats.tile([P, 3 + HALVES, NT], F32)
+        exps = stats.tile([P, 3 + HALVES, NT], F32)
+        neg_max = stats.tile([P, NT], F32)
         z_both = stats.tile([P, 2 * NT], F32)
         s_both = stats.tile([P, 2 * NT], F32)
         inv_z_both = stats.tile([P, 2 * NT], F32)
         neg_inv_z = stats.tile([P, NT], F32)
         ln_z_both = stats.tile([P, 2 * NT], F32)
+        half_factor = stats.tile([P, HALVES, NT], F32)
         win_factor = stats.tile([P, NT], F32)
         neg_win_factor = stats.tile([P, NT], F32)
         rest = stats.tile([P, NT], F32)
+        scaled = stats.tile([P, HALVES, NT], F32)
         whole, window = slice(0, NT), slice(NT, 2 * NT)
-        z_pairs = z_halves[:].rearrange("p (r h) -> p r h", h=HALVES)
-        s_pairs = s_halves[:].rearrange("p (r h) -> p r h", h=HALVES)
+        z_by_half = z_halves[:].rearrange("p (h r) -> p h r", h=HALVES)
+        s_by_half = s_halves[:].rearrange("p (h r) -> p h r", h=HALVES)
+        m_by_half = neg_max_halves[:].rearrange("p (h r) -> p h r", h=HALVES)
+
+        def maximum_differences():
+            nc.vector.tensor_tensor(
+                out=neg_max[:], in0=m_by_half[:, 0, :], in1=m_by_half[:, 1, :], op=ALU.min
+            )
+            nc.gpsimd.tensor_scalar_min(out=diffs[:, 2, :], in0=neg_max_win[:], scalar1=0.0)
+            nc.gpsimd.tensor_sub(out=diffs[:, 1, :], in0=diffs[:, 2, :], in1=neg_max_win[:])
+            nc.gpsimd.tensor_sub(out=diffs[:, 0, :], in0=neg_max[:], in1=neg_max_win[:])
+            for h in range(HALVES):
+                nc.gpsimd.tensor_sub(out=diffs[:, 3 + h, :], in0=neg_max[:], in1=m_by_half[:, h, :])
+            nc.scalar.activation(out=exps[:], in_=diffs[:], func=ACT.Exp)
+
+        WINDOW_STEPS = {4: (0, 1, 2), 5: (3, 4), 6: (5, 6, 7)}
+
+        EARLY_SUMS = {3: (0, 1), 4: (2, 3), 5: (4, 5), 6: (6,), 7: (7,)}
 
         for r in range(NT):
-            if r + 4 < NT:
-                sum_squares(r + 4)
-                inverse_norm(r + 4)
             if r + 3 < NT:
                 q_grouped[r + 3] = regroup(q_planes[r + 3], on_scalar)
-            if 1 <= r < NT - 3:
-                u_grouped[r + 3] = regroup(u_planes[r + 3], on_scalar)
-            if r == NT - 3:
-                nc.scalar.activation(
-                    out=not_keep[:], in_=outside[:, :, 0:WIN], func=ACT.Copy, scale=-1.0 / HUGE
-                )
-            if r == NT - 2:
-                nc.scalar.activation(
-                    out=keep[:], in_=outside[:, :, 0:WIN], func=ACT.Copy, scale=1.0 / HUGE, bias=1.0
-                )
-            for h in range(HALVES):
-                if r + 1 < NT:
-                    half_maximum(r + 1, h)
-                    if h == 1:
-                        window_logits(r + 1)
-                        row_maximum(r + 1)
-                if r >= NT - 3:
-                    gram_row_sums(2 * (r - NT + 3) + h)
-                entropy_sum(r, h)
-                product(r + 2, h)
-                if (r, h) == (0, 0):
-                    quantise_tile(u_grouped[2], u_codes, u_scales, 2)
-                    scale_x(3)
-                    u_planes[3] = transpose_u(u_tiles[3])
-                    u_grouped[3] = regroup(u_planes[3], on_scalar)
             if r + 1 < NT:
-                exponentials(r + 1)
-            else:
-                nc.vector.tensor_add(
-                    out=z_both[:, whole], in0=z_pairs[:, :, 0], in1=z_pairs[:, :, 1]
-                )
+                u_grouped[r + 1] = regroup(u_planes[r + 1], on_scalar)
+            for h in range(HALVES):
+                if r + 1 < NT and (r, h) != (0, 0):
+                    half_maximum(r + 1, h)
+                    window_logits(r + 1, h)
+                    exponentials(r + 1, h)
+                if (r, h) != (0, 0):
+                    entropy_sum(r, h)
+                    if r + 2 < NT:
+                        product(r + 2, h)
             if r + 3 < NT:
+                sum_squares(r + 3)
+                inverse_norm(r + 3)
                 quantise_q_tile(q_grouped[r + 3], r + 3)
             if r + 1 < NT:
                 window_maximum(r + 1)
-            if r > NT // 2:
+                quantise_tile(u_grouped[r + 1], u_codes, u_scales, r + 1)
+            if r + 2 >= NT:
+                for h in range(HALVES):
+                    product(r + 2, h)
+            for i in EARLY_SUMS.get(r, ()):
+                gram_row_sums(i, 0)
+            if r == NT - 1:
                 for i in range(2):
-                    window_entropy_sum(2 * r - NT - 2 + i)
-            if r >= NT // 2:
-                for i in range(2):
-                    window_exponentials(2 * r - NT + i)
+                    gram_row_sums(i, 1)
+            for i in WINDOW_STEPS.get(r, ()):
+                window_exponentials(i)
+            for i in WINDOW_STEPS.get(r - 1, ()):
+                window_entropy_sum(i)
+            for i in EARLY_SUMS.get(r, ()):
+                finish_row_sums(i, 0)
             if r + 4 < NT:
                 q_planes[r + 4] = transpose_q(r + 4)
-                scale_x(r + 4)
-                u_planes[r + 4] = transpose_u(u_tiles[r + 4])
-            if r + 3 < NT:
-                quantise_tile(u_grouped[r + 3], u_codes, u_scales, r + 3)
-            if NT - 3 <= r < NT - 1:
-                for i in range(2):
-                    finish_row_sums(2 * (r - NT + 3) + i)
-            if r == NT - 1:
+            if r + 2 < NT:
+                scale_x(r + 2)
+                u_planes[r + 2] = transpose_u(u_tiles[r + 2])
+            if r == NT - 2:
                 clear_blocks(0)
+                maximum_differences()
+            if r == NT - 1:
                 clear_blocks(1)
+                for i in range(2):
+                    finish_row_sums(i, 1)
 
-        nc.vector.reciprocal(out=inv_z_both[:, whole], in_=z_both[:, whole])
-        nc.gpsimd.tensor_sub(out=diffs[:, 0, :], in0=neg_max[:], in1=neg_max_win[:])
-        nc.gpsimd.tensor_scalar_min(out=diffs[:, 2, :], in0=neg_max_win[:], scalar1=0.0)
-        nc.gpsimd.tensor_sub(out=diffs[:, 1, :], in0=diffs[:, 2, :], in1=neg_max_win[:])
-        nc.scalar.activation(out=exps[:], in_=diffs[:], func=ACT.Exp)
-        nc.gpsimd.tensor_mul(out=win_factor[:], in0=exps[:, 0, :], in1=inv_z_both[:, whole])
-        nc.gpsimd.tensor_scalar_mul(out=neg_win_factor[:], in0=win_factor[:], scalar1=-1.0)
-        nc.gpsimd.tensor_mul(out=rest[:], in0=exps[:, 2, :], in1=outside_count[:])
-        nc.gpsimd.tensor_mul(out=z_both[:, window], in0=z_win[:], in1=exps[:, 1, :])
-        nc.gpsimd.tensor_mul(out=s_both[:, window], in0=z_both[:, window], in1=diffs[:, 1, :])
-        nc.gpsimd.tensor_add(out=z_both[:, window], in0=z_both[:, window], in1=rest[:])
+        nc.gpsimd.tensor_mul(out=scaled[:], in0=z_by_half, in1=exps[:, 3 : 3 + HALVES, :])
+        nc.gpsimd.tensor_add(out=z_both[:, whole], in0=scaled[:, 0, :], in1=scaled[:, 1, :])
 
-        ln_parts = stats.tile([P, NT, 2], F32)
+        def attention_factors():
+            nc.vector.tensor_scalar_mul(out=neg_inv_z[:], in0=inv_z_both[:, whole], scalar1=-1.0)
+            for h in range(HALVES):
+                nc.gpsimd.tensor_mul(
+                    out=half_factor[:, h, :], in0=exps[:, 3 + h, :], in1=neg_inv_z[:]
+                )
+            nc.gpsimd.tensor_mul(out=neg_win_factor[:], in0=exps[:, 0, :], in1=neg_inv_z[:])
+            nc.gpsimd.tensor_scalar_mul(out=win_factor[:], in0=neg_win_factor[:], scalar1=-1.0)
+
+        def window_normaliser():
+            nc.gpsimd.tensor_mul(out=rest[:], in0=exps[:, 2, :], in1=outside_count[:])
+            nc.gpsimd.tensor_mul(out=z_both[:, window], in0=z_win[:], in1=exps[:, 1, :])
+            nc.gpsimd.tensor_mul(out=s_both[:, window], in0=z_both[:, window], in1=diffs[:, 1, :])
+            nc.gpsimd.tensor_add(out=z_both[:, window], in0=z_both[:, window], in1=rest[:])
+
+        LATE_SUMS = {0: (2, 3), 1: (4, 5), 2: (6, 7)}
+
+        ln_parts = stats.tile([P, NT, HALVES + 1], F32)
 
         def logs_of_rest(r):
-            logs = junk.tile([P, T], F32, tag="logs", bufs=2)
-            nc.scalar.activation(
-                out=logs[:], in_=e_all[:, r, :], func=ACT.Ln, scale=neg_inv_z[:, r : r + 1], bias=1.0,
-                accum_out=ln_parts[:, r, 0:1],
-            )
+            for h in range(HALVES):
+                logs = junk.tile([P, BANK], F32, tag="logs")
+                nc.scalar.activation(
+                    out=logs[:], in_=e_all[:, r, BANK * h : BANK * (h + 1)], func=ACT.Ln,
+                    scale=half_factor[:, h, r : r + 1], bias=1.0, accum_out=ln_parts[:, r, h : h + 1],
+                )
             win_logs = junk.tile([P, WIN], F32, tag="win_logs")
             nc.scalar.activation(
                 out=win_logs[:], in_=e_win[:, r, :], func=ACT.Ln, scale=neg_win_factor[:, r : r + 1],
-                bias=1.0, accum_out=ln_parts[:, r, 1:2],
+                bias=1.0, accum_out=ln_parts[:, r, HALVES : HALVES + 1],
             )
 
         def window_diversity(r):
@@ -512,43 +571,56 @@ def tile_selfattention_pa_kernel(tc, x, q, k, out_0, out_1, out_2, out_3, out_4)
 
         win_sums = stats.tile([P, NT], F32)
         denom = stats.tile([P, NT], F32)
-        numer = stats.tile([P, NT], F32)
-        dep_coef = stats.tile([P, NT], F32)
+        numer = stats.tile([P, HALVES, NT], F32)
         segments = [slice(0, 4), slice(4, 7), slice(7, 8)]
         dep_rows = {}
 
-        def window_sums(tiles):
+        def denominators(tiles):
             nc.gpsimd.tensor_add(
                 out=win_sums[:, tiles], in0=minus_d_sums[:, 1, tiles, 0], in1=minus_d_sums[:, 1, tiles, 1]
             )
-
-        def denominators(tiles):
-            nc.gpsimd.tensor_sub(out=denom[:, tiles], in0=win_sums[:, tiles], in1=gram_sums[:, tiles])
-            nc.gpsimd.tensor_scalar_add(out=denom[:, tiles], in0=denom[:, tiles], scalar1=float(T))
+            for part in range(2):
+                nc.gpsimd.tensor_sub(
+                    out=win_sums[:, tiles], in0=win_sums[:, tiles], in1=gram_parts[:, part, tiles]
+                )
+            nc.gpsimd.tensor_scalar_add(out=denom[:, tiles], in0=win_sums[:, tiles], scalar1=float(T))
 
         def inverse_denominators(tiles):
             nc.vector.reciprocal(out=denom[:, tiles], in_=denom[:, tiles])
 
-        def dep_coefficients(tiles):
-            nc.gpsimd.tensor_mul(
-                out=dep_coef[:, tiles], in0=denom[:, tiles], in1=neg_inv_z[:, tiles]
-            )
-
         def numerators(tiles):
+            for h in range(HALVES):
+                nc.gpsimd.tensor_mul(
+                    out=numer[:, h, tiles], in0=minus_d_sums[:, 0, tiles, h],
+                    in1=half_factor[:, h, tiles],
+                )
             nc.gpsimd.tensor_add(
-                out=numer[:, tiles], in0=minus_d_sums[:, 0, tiles, 0], in1=minus_d_sums[:, 0, tiles, 1]
+                out=numer[:, 0, tiles], in0=numer[:, 0, tiles], in1=numer[:, 1, tiles]
             )
 
         def dep_factors(tiles):
             cols = slice(COL_DEP + tiles.start, COL_DEP + tiles.stop)
-            nc.gpsimd.tensor_mul(out=vectors[:, cols], in0=numer[:, tiles], in1=dep_coef[:, tiles])
+            nc.gpsimd.tensor_mul(out=vectors[:, cols], in0=numer[:, 0, tiles], in1=denom[:, tiles])
+
+        last_factor = stats.tile([P, HALVES], F32)
+        last_part = stats.tile([P, 1], F32)
+
+        def last_factors():
+            for h in range(HALVES):
+                nc.gpsimd.tensor_mul(
+                    out=last_factor[:, h : h + 1], in0=half_factor[:, h, NT - 1 : NT],
+                    in1=denom[:, NT - 1 : NT],
+                )
+
+        def first_part_of_last_tile():
+            nc.vector.tensor_scalar_mul(
+                out=last_part[:], in0=minus_d_sums[:, 0, NT - 1, 0:1], scalar1=last_factor[:, 0:1]
+            )
 
         def dep_factor_of_last_tile():
-            last = slice(NT - 1, NT)
             nc.vector.tensor_scalar(
-                out=vectors[:, COL_DEP_LAST : COL_DEP_LAST + 1], in0=minus_d_sums[:, 0, NT - 1, 0:1],
-                scalar1=minus_d_sums[:, 0, NT - 1, 1:2], scalar2=dep_coef[:, last],
-                op0=ALU.add, op1=ALU.mult,
+                out=vectors[:, COL_DEP_LAST : COL_DEP_LAST + 1], in0=minus_d_sums[:, 0, NT - 1, 1:2],
+                scalar1=last_factor[:, 1:2], scalar2=last_part[:], op0=ALU.mult, op1=ALU.add,
             )
 
         def spread_dep_factor(s):
@@ -578,7 +650,7 @@ def tile_selfattention_pa_kernel(tc, x, q, k, out_0, out_1, out_2, out_3, out_4)
             )
 
         def finish_window(r, engine):
-            engine.tensor_mul(out=att_wins[r][:], in0=att_wins[r][:], in1=keep[:, r, :])
+            engine.tensor_mul(out=att_wins[r][:], in0=att_wins[r][:], in1=keep[:, r, 0:WIN])
             lo = WIN_STEP * r
             nc.sync.dma_start(out=out_0[P * r : P * (r + 1), lo : lo + WIN], in_=att_wins[r][:])
 
@@ -588,66 +660,67 @@ def tile_selfattention_pa_kernel(tc, x, q, k, out_0, out_1, out_2, out_3, out_4)
         inv_div_total = stats.tile([P, 1], F32)
 
         window_diversity(0)
-        for r in range(NT - 2, NT):
-            window_entropy_sum(r)
-        nc.vector.tensor_scalar_mul(out=neg_inv_z[:], in0=inv_z_both[:, whole], scalar1=-1.0)
         for r in range(NT):
-            logs_of_rest(r)
-            if r + 2 < NT:
-                clear_blocks(r + 2)
-            if r == 5:
-                inverse_denominators(segments[0])
-                dep_coefficients(segments[0])
-                dep_factors(segments[0])
             weighted_diversity(r, 0)
+            if r == 4:
+                inverse_denominators(segments[0])
+                dep_factors(segments[0])
+            if r == 0:
+                nc.vector.reciprocal(out=inv_z_both[:, whole], in_=z_both[:, whole])
             if r + 2 < NT:
                 product(NT + r + 2, 0)
-            if r == 5:
-                spread_dep_factor(0)
             if r == 7:
                 inverse_denominators(slice(4, 8))
-                dep_coefficients(slice(4, 8))
                 dep_factors(segments[1])
+                last_factors()
                 spread_dep_factor(1)
-                for w in range(1, 3):
+                for w in range(3):
                     finish_window(w, nc.gpsimd)
             weighted_diversity(r, 1)
+            if r == 0:
+                attention_factors()
             if r + 2 < NT:
                 product(NT + r + 2, 1)
-            if r < 2:
-                gram_row_sums(r + 6)
-            if r < 4:
-                finish_row_sums(r + 4)
+                clear_blocks(r + 2)
+            logs_of_rest(r)
+            for i in LATE_SUMS.get(r, ()):
+                gram_row_sums(i, 1)
+            for i in LATE_SUMS.get(r - 1, ()):
+                finish_row_sums(i, 1)
+            if r == 5:
+                spread_dep_factor(0)
             if r + 1 < NT:
                 window_diversity(r + 1)
-            if r == 1:
+            if r == 6:
+                denominators(slice(4, 8))
+            if r == 0:
+                window_normaliser()
+            if r == 2:
                 nc.vector.reciprocal(out=inv_z_both[:, window], in_=z_both[:, window])
+            if r == 1:
+                nc.gpsimd.tensor_mul(out=scaled[:], in0=scaled[:], in1=diffs[:, 3 : 3 + HALVES, :])
+                nc.gpsimd.tensor_mul(out=s_by_half, in0=s_by_half, in1=exps[:, 3 : 3 + HALVES, :])
+                nc.gpsimd.tensor_add(out=scaled[:], in0=scaled[:], in1=s_by_half)
                 nc.gpsimd.tensor_add(
-                    out=s_both[:, whole], in0=s_pairs[:, :, 0], in1=s_pairs[:, :, 1]
+                    out=s_both[:, whole], in0=scaled[:, 0, :], in1=scaled[:, 1, :]
                 )
             if r == 2:
                 nc.scalar.activation(out=ln_z_both[:], in_=z_both[:], func=ACT.Ln)
-                window_entropy_parts()
-            if r == 3:
-                window_sums(segments[0])
                 denominators(segments[0])
+            if r == 3:
                 numerators(segments[0])
             if r == 4:
-                entropies()
+                window_entropy_parts()
             if r == 5:
+                entropies()
+            if r == 6:
                 total_ps = total_over_tokens(abs_sum[:], 1)
             if r == 6:
-                window_sums(slice(4, 8))
-                denominators(slice(4, 8))
                 numerators(segments[1])
                 for w in range(3):
                     add_dep_factor(w, 0)
-                finish_window(0, nc.gpsimd)
-                nc.vector.tensor_scalar_max(out=inv_total[:], in0=total_ps[:, 0:1], scalar1=EPS)
-        nc.vector.reciprocal(out=inv_total[:], in_=inv_total[:])
-        nc.gpsimd.tensor_scalar_mul(
-            out=vectors[:, COL_ENT : COL_ENT + NT], in0=entropy_both[:, whole], scalar1=inv_total[:]
-        )
+        nc.vector.tensor_scalar_max(out=inv_total[:], in0=total_ps[:, 0:1], scalar1=EPS)
+        first_part_of_last_tile()
         add_dep_factor(3, 0)
         add_dep_factor(4, 0)
         dep_factor_of_last_tile()
@@ -657,13 +730,17 @@ def tile_selfattention_pa_kernel(tc, x, q, k, out_0, out_1, out_2, out_3, out_4)
         div_total_ps = total_over_tokens(div_sum[:], 1)
         for w in range(3, NT):
             add_dep_factor(w, 1)
-            if w < 6:
+            if w < 5:
                 finish_window(w, nc.gpsimd)
         for w in range(6, NT):
             add_dep_factor(w, 2)
-        nc.vector.reciprocal(out=inv_div_total[:], in_=div_total_ps[:, 0:1])
-        for w in range(6, NT):
+        nc.vector.reciprocal(out=inv_total[:], in_=inv_total[:])
+        for w in range(NT - 1, 4, -1):
             finish_window(w, nc.vector)
+        nc.vector.reciprocal(out=inv_div_total[:], in_=div_total_ps[:, 0:1])
+        nc.vector.tensor_scalar_mul(
+            out=vectors[:, COL_ENT : COL_ENT + NT], in0=entropy_both[:, whole], scalar1=inv_total[:]
+        )
         nc.vector.tensor_scalar_mul(
             out=vectors[:, COL_DIV : COL_DIV + NT], in0=div_h[:], scalar1=inv_div_total[:]
         )

@@ -28,14 +28,12 @@ WIN_STEP = 2 * BLOCK
 WIN = T - WIN_STEP * (NT - 1)
 WIN_BLOCKS = 4
 ROW_SHIFT = P - WIN_STEP
-WARM_UPS = 8
 LAST_BLOCK = T % BLOCK
 HUGE = 2.0**100
 
 FLOPS = 2 * 2 * T * T * FEAT
 
 COL_ENT_WIN, COL_DIV, COL_ENT, COL_DEP = 0, NT, 2 * NT, 3 * NT
-COL_DEP_LAST = 4 * NT
 
 
 def window_pieces(r):
@@ -115,18 +113,20 @@ def tile_selfattention_pa_kernel(tc, x, q, k, out_0, out_1, out_2, out_3, out_4)
         keep = keep4[:].rearrange("p r b c -> p r (b c)")
         not_keep = not_keep4[:].rearrange("p r b c -> p r (b c)")
         inside_by_column = inside[:].unsqueeze(3).to_broadcast([P, NT, WIN_BLOCKS, BLOCK])
-        nc.gpsimd.tensor_scalar(
+        nc.vector.tensor_scalar(
             out=keep4[:], in0=inside_by_column, scalar1=1.0 / HUGE, scalar2=1.0,
             op0=ALU.mult, op1=ALU.add,
         )
-        nc.gpsimd.tensor_scalar(
+        nc.vector.tensor_scalar(
             out=not_keep4[:], in0=inside_by_column, scalar1=-1.0 / HUGE, scalar2=0.0,
             op0=ALU.mult, op1=ALU.add,
         )
         minus_half = const.tile([P, 1], F32)
         nc.gpsimd.memset(minus_half[:], -0.5)
-        minus_d_sums = stats.tile([P, 2, NT, HALVES], F32)
-        nc.gpsimd.memset(minus_d_sums[:], 0.0)
+        denom_parts = stats.tile([P, 5, NT], F32)
+        nc.gpsimd.memset(denom_parts[:], 0.0)
+        nc.gpsimd.memset(denom_parts[:, 4, :], float(T))
+        weighted_sums = stats.tile([P, HALVES, NT], F32)
         vectors = stats.tile([P, P], F32)
         nc.gpsimd.memset(vectors[:], 0.0)
         zeros = const.tile([P, T - WIN], F32)
@@ -234,7 +234,6 @@ def tile_selfattention_pa_kernel(tc, x, q, k, out_0, out_1, out_2, out_3, out_4)
                 )
             banks[j, h] = bank
 
-        gram_parts = stats.tile([P, 2, NT], F32)
         accs = {}
 
         def gram_row_sums(r, part, blocks=NT // 2):
@@ -256,8 +255,8 @@ def tile_selfattention_pa_kernel(tc, x, q, k, out_0, out_1, out_2, out_3, out_4)
         def finish_row_sums(r, part):
             copied = junk.tile([P, P], F32, tag="copied")
             nc.scalar.activation(
-                out=copied[:], in_=accs[r, part][:], func=ACT.Copy,
-                accum_out=gram_parts[:, part, r : r + 1],
+                out=copied[:], in_=accs[r, part][:], func=ACT.Copy, scale=-1.0,
+                accum_out=denom_parts[:, 2 + part, r : r + 1],
             )
 
         e_all = resident.tile([P, NT, T], F32)
@@ -326,10 +325,6 @@ def tile_selfattention_pa_kernel(tc, x, q, k, out_0, out_1, out_2, out_3, out_4)
             nc.gpsimd.tensor_mul(out=window, in0=window, in1=not_keep[:, r, 0:WIN])
 
         k_words = k_sb[:].bitcast(F32)
-        warm = psum_t.tile([P, P], F32, tag="t")
-        for i in range(WARM_UPS):
-            nc.tensor.matmul(out=warm[:], lhsT=ident_f32[:], rhs=ident_f32[:], start=True, stop=True)
-
         k_grouped, q_planes, u_planes, q_grouped, u_grouped = {}, {}, {}, {}, {}
         on_scalar, on_vector = nc.scalar.copy, nc.vector.tensor_copy
 
@@ -425,17 +420,24 @@ def tile_selfattention_pa_kernel(tc, x, q, k, out_0, out_1, out_2, out_3, out_4)
         s_by_half = s_halves[:].rearrange("p (h r) -> p h r", h=HALVES)
         m_by_half = neg_max_halves[:].rearrange("p (h r) -> p h r", h=HALVES)
 
-        def maximum_differences():
+        def by_half(column):
+            return column.unsqueeze(1).to_broadcast([P, HALVES, NT])
+
+        def row_maxima():
             nc.vector.tensor_tensor(
                 out=neg_max[:], in0=m_by_half[:, 0, :], in1=m_by_half[:, 1, :], op=ALU.min
             )
-            nc.gpsimd.tensor_scalar_min(out=diffs[:, 2, :], in0=neg_max_win[:], scalar1=0.0)
-            nc.gpsimd.tensor_sub(out=diffs[:, 1, :], in0=diffs[:, 2, :], in1=neg_max_win[:])
-            nc.gpsimd.tensor_sub(out=diffs[:, 0, :], in0=neg_max[:], in1=neg_max_win[:])
-            for h in range(HALVES):
-                nc.gpsimd.tensor_sub(out=diffs[:, 3 + h, :], in0=neg_max[:], in1=m_by_half[:, h, :])
+            nc.vector.tensor_scalar_min(out=diffs[:, 2, :], in0=neg_max_win[:], scalar1=0.0)
+
+        def maximum_differences():
+            nc.vector.tensor_sub(
+                out=diffs[:, 3 : 3 + HALVES, :], in0=by_half(neg_max[:]), in1=m_by_half
+            )
+            nc.vector.tensor_sub(out=diffs[:, 0, :], in0=neg_max[:], in1=neg_max_win[:])
+            nc.vector.tensor_sub(out=diffs[:, 1, :], in0=diffs[:, 2, :], in1=neg_max_win[:])
             nc.scalar.activation(out=exps[:], in_=diffs[:], func=ACT.Exp)
 
+        CLEARED_EARLY = 3
         WINDOW_STEPS = {4: (0, 1, 2), 5: (3, 4), 6: (5, 6, 7)}
 
         EARLY_SUMS = {3: (0, 1), 4: (2, 3), 5: (4, 5), 6: (6,), 7: (7,)}
@@ -454,9 +456,13 @@ def tile_selfattention_pa_kernel(tc, x, q, k, out_0, out_1, out_2, out_3, out_4)
                     entropy_sum(r, h)
                     if r + 2 < NT:
                         product(r + 2, h)
+            if r == NT - 1:
+                maximum_differences()
             if r + 3 < NT:
                 sum_squares(r + 3)
                 inverse_norm(r + 3)
+                if r + 3 >= NT - CLEARED_EARLY:
+                    clear_blocks(r + 3 - NT + CLEARED_EARLY)
                 quantise_q_tile(q_grouped[r + 3], r + 3)
             if r + 1 < NT:
                 window_maximum(r + 1)
@@ -481,24 +487,22 @@ def tile_selfattention_pa_kernel(tc, x, q, k, out_0, out_1, out_2, out_3, out_4)
                 scale_x(r + 2)
                 u_planes[r + 2] = transpose_u(u_tiles[r + 2])
             if r == NT - 2:
-                clear_blocks(0)
-                maximum_differences()
+                row_maxima()
             if r == NT - 1:
-                clear_blocks(1)
                 for i in range(2):
                     finish_row_sums(i, 1)
 
-        nc.gpsimd.tensor_mul(out=scaled[:], in0=z_by_half, in1=exps[:, 3 : 3 + HALVES, :])
-        nc.gpsimd.tensor_add(out=z_both[:, whole], in0=scaled[:, 0, :], in1=scaled[:, 1, :])
+        def whole_normaliser():
+            nc.vector.tensor_mul(out=scaled[:], in0=z_by_half, in1=exps[:, 3 : 3 + HALVES, :])
+
+        def add_halves():
+            nc.vector.tensor_add(out=z_both[:, whole], in0=scaled[:, 0, :], in1=scaled[:, 1, :])
 
         def attention_factors():
-            nc.vector.tensor_scalar_mul(out=neg_inv_z[:], in0=inv_z_both[:, whole], scalar1=-1.0)
-            for h in range(HALVES):
-                nc.gpsimd.tensor_mul(
-                    out=half_factor[:, h, :], in0=exps[:, 3 + h, :], in1=neg_inv_z[:]
-                )
-            nc.gpsimd.tensor_mul(out=neg_win_factor[:], in0=exps[:, 0, :], in1=neg_inv_z[:])
-            nc.gpsimd.tensor_scalar_mul(out=win_factor[:], in0=neg_win_factor[:], scalar1=-1.0)
+            nc.vector.tensor_mul(
+                out=half_factor[:], in0=exps[:, 3 : 3 + HALVES, :], in1=by_half(neg_inv_z[:])
+            )
+            nc.vector.tensor_mul(out=neg_win_factor[:], in0=exps[:, 0, :], in1=neg_inv_z[:])
 
         def window_normaliser():
             nc.gpsimd.tensor_mul(out=rest[:], in0=exps[:, 2, :], in1=outside_count[:])
@@ -529,7 +533,7 @@ def tile_selfattention_pa_kernel(tc, x, q, k, out_0, out_1, out_2, out_3, out_4)
                 nc.vector.scalar_tensor_tensor(
                     out=products[:, w_first:w_last], in0=banks[NT + r, h][:, first:last], scalar=-1.0,
                     in1=keep[:, r, w_first:w_last], op0=ALU.add, op1=ALU.mult,
-                    accum_out=minus_d_sums[:, 1, r, i : i + 1],
+                    accum_out=denom_parts[:, i, r : r + 1],
                 )
 
         def weighted_diversity(r, h):
@@ -537,7 +541,7 @@ def tile_selfattention_pa_kernel(tc, x, q, k, out_0, out_1, out_2, out_3, out_4)
             nc.vector.scalar_tensor_tensor(
                 out=products[:], in0=banks[NT + r, h][:], scalar=-1.0,
                 in1=e_all[:, r, BANK * h : BANK * (h + 1)],
-                op0=ALU.add, op1=ALU.mult, accum_out=minus_d_sums[:, 0, r, h : h + 1],
+                op0=ALU.add, op1=ALU.mult, accum_out=weighted_sums[:, h, r : r + 1],
             )
 
         def total_over_tokens(partial, columns):
@@ -569,58 +573,51 @@ def tile_selfattention_pa_kernel(tc, x, q, k, out_0, out_1, out_2, out_3, out_4)
                 out=abs_entropy[:], in_=entropy_both[:, whole], func=ACT.Abs, accum_out=abs_sum[:]
             )
 
-        win_sums = stats.tile([P, NT], F32)
         denom = stats.tile([P, NT], F32)
-        numer = stats.tile([P, HALVES, NT], F32)
+        dep_coef = stats.tile([P, HALVES, NT], F32)
+        dep_parts = stats.tile([P, HALVES, NT], F32)
         segments = [slice(0, 4), slice(4, 7), slice(7, 8)]
         dep_rows = {}
 
         def denominators(tiles):
-            nc.gpsimd.tensor_add(
-                out=win_sums[:, tiles], in0=minus_d_sums[:, 1, tiles, 0], in1=minus_d_sums[:, 1, tiles, 1]
+            nc.vector.tensor_reduce(
+                out=denom[:, tiles], in_=denom_parts[:, :, tiles].rearrange("p i r -> p r i"),
+                axis=AX.X, op=ALU.add,
             )
-            for part in range(2):
-                nc.gpsimd.tensor_sub(
-                    out=win_sums[:, tiles], in0=win_sums[:, tiles], in1=gram_parts[:, part, tiles]
-                )
-            nc.gpsimd.tensor_scalar_add(out=denom[:, tiles], in0=win_sums[:, tiles], scalar1=float(T))
 
         def inverse_denominators(tiles):
             nc.vector.reciprocal(out=denom[:, tiles], in_=denom[:, tiles])
 
-        def numerators(tiles):
-            for h in range(HALVES):
-                nc.gpsimd.tensor_mul(
-                    out=numer[:, h, tiles], in0=minus_d_sums[:, 0, tiles, h],
-                    in1=half_factor[:, h, tiles],
-                )
-            nc.gpsimd.tensor_add(
-                out=numer[:, 0, tiles], in0=numer[:, 0, tiles], in1=numer[:, 1, tiles]
+        def dep_coefficients(tiles):
+            n = tiles.stop - tiles.start
+            nc.vector.tensor_mul(
+                out=dep_coef[:, :, tiles], in0=half_factor[:, :, tiles],
+                in1=denom[:, tiles].unsqueeze(1).to_broadcast([P, HALVES, n]),
+            )
+
+        def weighted_parts(tiles):
+            nc.vector.tensor_mul(
+                out=dep_parts[:, :, tiles], in0=weighted_sums[:, :, tiles], in1=dep_coef[:, :, tiles]
             )
 
         def dep_factors(tiles):
-            cols = slice(COL_DEP + tiles.start, COL_DEP + tiles.stop)
-            nc.gpsimd.tensor_mul(out=vectors[:, cols], in0=numer[:, 0, tiles], in1=denom[:, tiles])
+            nc.vector.tensor_add(
+                out=vectors[:, COL_DEP + tiles.start : COL_DEP + tiles.stop],
+                in0=dep_parts[:, 0, tiles], in1=dep_parts[:, 1, tiles],
+            )
 
-        last_factor = stats.tile([P, HALVES], F32)
         last_part = stats.tile([P, 1], F32)
-
-        def last_factors():
-            for h in range(HALVES):
-                nc.gpsimd.tensor_mul(
-                    out=last_factor[:, h : h + 1], in0=half_factor[:, h, NT - 1 : NT],
-                    in1=denom[:, NT - 1 : NT],
-                )
 
         def first_part_of_last_tile():
             nc.vector.tensor_scalar_mul(
-                out=last_part[:], in0=minus_d_sums[:, 0, NT - 1, 0:1], scalar1=last_factor[:, 0:1]
+                out=last_part[:], in0=weighted_sums[:, 0, NT - 1 : NT],
+                scalar1=dep_coef[:, 0, NT - 1 : NT],
             )
 
         def dep_factor_of_last_tile():
             nc.vector.tensor_scalar(
-                out=vectors[:, COL_DEP_LAST : COL_DEP_LAST + 1], in0=minus_d_sums[:, 0, NT - 1, 1:2],
-                scalar1=last_factor[:, 1:2], scalar2=last_part[:], op0=ALU.mult, op1=ALU.add,
+                out=vectors[:, COL_DEP + NT - 1 : COL_DEP + NT], in0=weighted_sums[:, 1, NT - 1 : NT],
+                scalar1=dep_coef[:, 1, NT - 1 : NT], scalar2=last_part[:], op0=ALU.mult, op1=ALU.add,
             )
 
         def spread_dep_factor(s):
@@ -628,7 +625,7 @@ def tile_selfattention_pa_kernel(tc, x, q, k, out_0, out_1, out_2, out_3, out_4)
             dep_rows[s] = psum_t.tile([P, BANK], F32, name="dep_rows", tag="t")
             for j in range(tiles.start, tiles.stop):
                 i = j - tiles.start
-                col = COL_DEP_LAST if j == NT - 1 else COL_DEP + j
+                col = COL_DEP + j
                 nc.tensor.transpose(
                     dep_rows[s][:, P * i : P * (i + 1)],
                     vectors[:, col : col + 1].to_broadcast([P, P]), ident_f32[:],
@@ -659,44 +656,57 @@ def tile_selfattention_pa_kernel(tc, x, q, k, out_0, out_1, out_2, out_3, out_4)
         div_sum = stats.tile([P, 1], F32)
         inv_div_total = stats.tile([P, 1], F32)
 
+        whole_normaliser()
         window_diversity(0)
+        add_halves()
         for r in range(NT):
             weighted_diversity(r, 0)
-            if r == 4:
-                inverse_denominators(segments[0])
-                dep_factors(segments[0])
             if r == 0:
                 nc.vector.reciprocal(out=inv_z_both[:, whole], in_=z_both[:, whole])
-            if r + 2 < NT:
-                product(NT + r + 2, 0)
+            if r == 4:
+                inverse_denominators(segments[0])
+            if r == 5:
+                dep_factors(segments[0])
             if r == 7:
-                inverse_denominators(slice(4, 8))
+                nc.vector.tensor_scalar_max(out=inv_total[:], in0=total_ps[:, 0:1], scalar1=EPS)
+                weighted_parts(segments[1])
+                first_part_of_last_tile()
+                add_dep_factor(2, 0)
                 dep_factors(segments[1])
-                last_factors()
                 spread_dep_factor(1)
                 for w in range(3):
                     finish_window(w, nc.gpsimd)
+            if r + 2 < NT:
+                product(NT + r + 2, 0)
+            if r == 0:
+                window_diversity(1)
+                nc.vector.tensor_scalar_mul(out=neg_inv_z[:], in0=inv_z_both[:, whole], scalar1=-1.0)
             weighted_diversity(r, 1)
             if r == 0:
                 attention_factors()
+            if r == 1:
+                nc.vector.tensor_scalar_mul(out=win_factor[:], in0=neg_win_factor[:], scalar1=-1.0)
+            if r == 4:
+                dep_coefficients(segments[0])
             if r + 2 < NT:
                 product(NT + r + 2, 1)
+            if CLEARED_EARLY <= r + 2 < NT:
                 clear_blocks(r + 2)
             logs_of_rest(r)
             for i in LATE_SUMS.get(r, ()):
                 gram_row_sums(i, 1)
             for i in LATE_SUMS.get(r - 1, ()):
                 finish_row_sums(i, 1)
+            if 1 < r + 1 < NT:
+                window_diversity(r + 1)
+            if r == 3:
+                denominators(segments[0])
+            if r == 4:
+                weighted_parts(segments[0])
             if r == 5:
                 spread_dep_factor(0)
-            if r + 1 < NT:
-                window_diversity(r + 1)
-            if r == 6:
-                denominators(slice(4, 8))
             if r == 0:
                 window_normaliser()
-            if r == 2:
-                nc.vector.reciprocal(out=inv_z_both[:, window], in_=z_both[:, window])
             if r == 1:
                 nc.gpsimd.tensor_mul(out=scaled[:], in0=scaled[:], in1=diffs[:, 3 : 3 + HALVES, :])
                 nc.gpsimd.tensor_mul(out=s_by_half, in0=s_by_half, in1=exps[:, 3 : 3 + HALVES, :])
@@ -705,33 +715,32 @@ def tile_selfattention_pa_kernel(tc, x, q, k, out_0, out_1, out_2, out_3, out_4)
                     out=s_both[:, whole], in0=scaled[:, 0, :], in1=scaled[:, 1, :]
                 )
             if r == 2:
+                nc.vector.reciprocal(out=inv_z_both[:, window], in_=z_both[:, window])
                 nc.scalar.activation(out=ln_z_both[:], in_=z_both[:], func=ACT.Ln)
-                denominators(segments[0])
             if r == 3:
-                numerators(segments[0])
-            if r == 4:
                 window_entropy_parts()
-            if r == 5:
+            if r == 4:
                 entropies()
             if r == 6:
                 total_ps = total_over_tokens(abs_sum[:], 1)
-            if r == 6:
-                numerators(segments[1])
-                for w in range(3):
+                denominators(slice(4, 8))
+                for w in range(2):
                     add_dep_factor(w, 0)
-        nc.vector.tensor_scalar_max(out=inv_total[:], in0=total_ps[:, 0:1], scalar1=EPS)
-        first_part_of_last_tile()
-        add_dep_factor(3, 0)
-        add_dep_factor(4, 0)
+                inverse_denominators(slice(4, 8))
+                for w in range(3, 5):
+                    add_dep_factor(w, 0)
+                dep_coefficients(slice(4, 8))
+        for w in range(3, 5):
+            add_dep_factor(w, 1)
         dep_factor_of_last_tile()
         spread_dep_factor(2)
         nc.vector.tensor_reduce(out=ln_sums[:], in_=ln_parts[:], axis=AX.X, op=ALU.add)
         nc.scalar.activation(out=div_h[:], in_=ln_sums[:], func=ACT.Exp, accum_out=div_sum[:])
         div_total_ps = total_over_tokens(div_sum[:], 1)
-        for w in range(3, NT):
+        for w in range(3, 5):
+            finish_window(w, nc.gpsimd)
+        for w in range(5, NT):
             add_dep_factor(w, 1)
-            if w < 5:
-                finish_window(w, nc.gpsimd)
         for w in range(6, NT):
             add_dep_factor(w, 2)
         nc.vector.reciprocal(out=inv_total[:], in_=inv_total[:])
@@ -749,10 +758,7 @@ def tile_selfattention_pa_kernel(tc, x, q, k, out_0, out_1, out_2, out_3, out_4)
         nc.tensor.transpose(vectors_t_ps[:], vectors[:], ident_f32[:])
         vectors_t = stats.tile([P, P], F32)
         nc.scalar.copy(out=vectors_t[:], in_=vectors_t_ps[:])
-        for out_vec, col in ((out_1, COL_ENT_WIN), (out_2, COL_DIV), (out_3, COL_ENT)):
+        for out_vec, col in ((out_1, COL_ENT_WIN), (out_2, COL_DIV), (out_3, COL_ENT), (out_4, COL_DEP)):
             nc.sync.dma_start(
                 out=out_vec.rearrange("(r p) -> r p", p=P), in_=vectors_t[col : col + NT, :]
             )
-        dep_out = out_4.rearrange("(r p) -> r p", p=P)
-        nc.sync.dma_start(out=dep_out[0 : NT - 1, :], in_=vectors_t[COL_DEP : COL_DEP + NT - 1, :])
-        nc.sync.dma_start(out=dep_out[NT - 1 : NT, :], in_=vectors_t[COL_DEP_LAST : COL_DEP_LAST + 1, :])

@@ -170,8 +170,12 @@ def tile_selfattention_pa_kernel(tc, x, q, k, out_0, out_1, out_2, out_3, out_4)
                 out=q_codes[:, r, :].bitcast(FP8X4), scales=q_scales[:, r, :], in_=grouped[:]
             )
 
-        def transpose_words(words):
+        def transpose_words(words, warm_ups=0):
             planes = psum_t.tile([P, 2 * PASSES, P], F32, name="planes", tag="t")
+            for i in range(warm_ups):
+                nc.tensor.matmul(
+                    out=planes[:, 0, :], lhsT=ident_f32[:], rhs=ident_f32[:], start=True, stop=True
+                )
             for w in range(2 * PASSES):
                 nc.tensor.transpose(planes[:, w, :], words[:, P * w : P * (w + 1)], ident_f32[:])
             return planes
@@ -185,7 +189,7 @@ def tile_selfattention_pa_kernel(tc, x, q, k, out_0, out_1, out_2, out_3, out_4)
             return grouped
 
         def transpose_q(r):
-            return transpose_words(q_sb[:].bitcast(F32)[:, r, :])
+            return transpose_words(q_sb[:].bitcast(F32)[:, r, :], 0 if r < 2 else 0)
 
         def transpose_u(u_tile):
             return transpose_words(u_tile[:].bitcast(F32))
@@ -339,37 +343,37 @@ def tile_selfattention_pa_kernel(tc, x, q, k, out_0, out_1, out_2, out_3, out_4)
             q_grouped[r] = regroup(q_planes[r], copy)
 
         k_planes = {}
-        k_planes[0] = transpose_words(k_words[:, 0, :])
-        k_planes[1] = transpose_words(k_words[:, 1, :])
+        k_planes[0] = transpose_words(k_words[:, 0, :], 4)
+        k_planes[1] = transpose_words(k_words[:, 1, :], 1)
         k_grouped[0] = regroup(k_planes[0], on_vector)
         k_grouped[1] = regroup(k_planes[1], on_scalar)
         sum_squares(0)
-        k_planes[2] = transpose_words(k_words[:, 2, :])
+        k_planes[2] = transpose_words(k_words[:, 2, :], 1)
         quantise_k(0)
         quantise_k(1)
         k_grouped[2] = regroup(k_planes[2], on_vector)
-        k_planes[3] = transpose_words(k_words[:, 3, :])
+        k_planes[3] = transpose_words(k_words[:, 3, :], 1)
         k_grouped[3] = regroup(k_planes[3], on_scalar)
         q_planes[0] = transpose_q(0)
         q_grouped[0] = regroup(q_planes[0], on_scalar)
         inverse_norm(0)
         quantise_k(2)
         quantise_k(3)
-        k_planes[4] = transpose_words(k_words[:, 4, :])
+        k_planes[4] = transpose_words(k_words[:, 4, :], 1)
         quantise_q_tile(q_grouped[0], 0)
         k_grouped[4] = regroup(k_planes[4], on_vector)
-        k_planes[5] = transpose_words(k_words[:, 5, :])
+        k_planes[5] = transpose_words(k_words[:, 5, :], 1)
         k_grouped[5] = regroup(k_planes[5], on_scalar)
         q_planes[1] = transpose_q(1)
         q_grouped[1] = regroup(q_planes[1], on_scalar)
         scale_x(0)
-        k_planes[6] = transpose_words(k_words[:, 6, :])
+        k_planes[6] = transpose_words(k_words[:, 6, :], 1)
         product(0, 0)
         quantise_k(4)
         quantise_q_tile(q_grouped[1], 1)
         quantise_k(5)
         k_grouped[6] = regroup(k_planes[6], on_scalar)
-        k_planes[7] = transpose_words(k_words[:, 7, :])
+        k_planes[7] = transpose_words(k_words[:, 7, :], 1)
         sum_squares(1)
         k_grouped[7] = regroup(k_planes[7], on_scalar)
         u_planes[0] = transpose_u(u_tiles[0])
@@ -437,6 +441,24 @@ def tile_selfattention_pa_kernel(tc, x, q, k, out_0, out_1, out_2, out_3, out_4)
             nc.vector.tensor_sub(out=diffs[:, 1, :], in0=diffs[:, 2, :], in1=neg_max_win[:])
             nc.scalar.activation(out=exps[:], in_=diffs[:], func=ACT.Exp)
 
+        def whole_normaliser():
+            nc.vector.tensor_mul(out=scaled[:], in0=z_by_half, in1=exps[:, 3 : 3 + HALVES, :])
+
+        def add_halves():
+            nc.vector.tensor_add(out=z_both[:, whole], in0=scaled[:, 0, :], in1=scaled[:, 1, :])
+
+        def inverse_normaliser():
+            nc.vector.reciprocal(out=inv_z_both[:, whole], in_=z_both[:, whole])
+
+        def attention_factors():
+            nc.vector.tensor_scalar_mul(out=neg_inv_z[:], in0=inv_z_both[:, whole], scalar1=-1.0)
+
+        def half_and_window_factors():
+            nc.vector.tensor_mul(
+                out=half_factor[:], in0=exps[:, 3 : 3 + HALVES, :], in1=by_half(neg_inv_z[:])
+            )
+            nc.vector.tensor_mul(out=neg_win_factor[:], in0=exps[:, 0, :], in1=neg_inv_z[:])
+
         CLEARED_EARLY = 3
         WINDOW_STEPS = {4: (0, 1, 2), 5: (3, 4), 6: (5, 6, 7)}
 
@@ -454,10 +476,10 @@ def tile_selfattention_pa_kernel(tc, x, q, k, out_0, out_1, out_2, out_3, out_4)
                     exponentials(r + 1, h)
                 if (r, h) != (0, 0):
                     entropy_sum(r, h)
+                    if (r, h) == (NT - 1, 0):
+                        whole_normaliser()
                     if r + 2 < NT:
                         product(r + 2, h)
-            if r == NT - 1:
-                maximum_differences()
             if r + 3 < NT:
                 sum_squares(r + 3)
                 inverse_norm(r + 3)
@@ -477,10 +499,17 @@ def tile_selfattention_pa_kernel(tc, x, q, k, out_0, out_1, out_2, out_3, out_4)
                     gram_row_sums(i, 1)
             for i in WINDOW_STEPS.get(r, ()):
                 window_exponentials(i)
+            if r == NT - 1:
+                add_halves()
             for i in WINDOW_STEPS.get(r - 1, ()):
                 window_entropy_sum(i)
-            for i in EARLY_SUMS.get(r, ()):
-                finish_row_sums(i, 0)
+                if i == 5:
+                    inverse_normaliser()
+                if i == 6:
+                    attention_factors()
+            if r < NT - 2:
+                for i in EARLY_SUMS.get(r, ()):
+                    finish_row_sums(i, 0)
             if r + 4 < NT:
                 q_planes[r + 4] = transpose_q(r + 4)
             if r + 2 < NT:
@@ -488,21 +517,7 @@ def tile_selfattention_pa_kernel(tc, x, q, k, out_0, out_1, out_2, out_3, out_4)
                 u_planes[r + 2] = transpose_u(u_tiles[r + 2])
             if r == NT - 2:
                 row_maxima()
-            if r == NT - 1:
-                for i in range(2):
-                    finish_row_sums(i, 1)
-
-        def whole_normaliser():
-            nc.vector.tensor_mul(out=scaled[:], in0=z_by_half, in1=exps[:, 3 : 3 + HALVES, :])
-
-        def add_halves():
-            nc.vector.tensor_add(out=z_both[:, whole], in0=scaled[:, 0, :], in1=scaled[:, 1, :])
-
-        def attention_factors():
-            nc.vector.tensor_mul(
-                out=half_factor[:], in0=exps[:, 3 : 3 + HALVES, :], in1=by_half(neg_inv_z[:])
-            )
-            nc.vector.tensor_mul(out=neg_win_factor[:], in0=exps[:, 0, :], in1=neg_inv_z[:])
+                maximum_differences()
 
         def window_normaliser():
             nc.gpsimd.tensor_mul(out=rest[:], in0=exps[:, 2, :], in1=outside_count[:])
@@ -511,6 +526,10 @@ def tile_selfattention_pa_kernel(tc, x, q, k, out_0, out_1, out_2, out_3, out_4)
             nc.gpsimd.tensor_add(out=z_both[:, window], in0=z_both[:, window], in1=rest[:])
 
         LATE_SUMS = {0: (2, 3), 1: (4, 5), 2: (6, 7)}
+        READ_SUMS = {
+            0: ((6, 0), (7, 0), (0, 1)), 1: ((1, 1), (2, 1), (3, 1)), 2: ((4, 1), (5, 1)),
+            3: ((6, 1), (7, 1)),
+        }
 
         ln_parts = stats.tile([P, NT, HALVES + 1], F32)
 
@@ -656,34 +675,25 @@ def tile_selfattention_pa_kernel(tc, x, q, k, out_0, out_1, out_2, out_3, out_4)
         div_sum = stats.tile([P, 1], F32)
         inv_div_total = stats.tile([P, 1], F32)
 
-        whole_normaliser()
+        half_and_window_factors()
         window_diversity(0)
-        add_halves()
         for r in range(NT):
             weighted_diversity(r, 0)
-            if r == 0:
-                nc.vector.reciprocal(out=inv_z_both[:, whole], in_=z_both[:, whole])
             if r == 4:
                 inverse_denominators(segments[0])
             if r == 5:
                 dep_factors(segments[0])
+            if r == 6:
+                inverse_denominators(segments[1])
             if r == 7:
                 nc.vector.tensor_scalar_max(out=inv_total[:], in0=total_ps[:, 0:1], scalar1=EPS)
-                weighted_parts(segments[1])
                 first_part_of_last_tile()
-                add_dep_factor(2, 0)
-                dep_factors(segments[1])
-                spread_dep_factor(1)
-                for w in range(3):
-                    finish_window(w, nc.gpsimd)
+                nc.vector.reciprocal(out=inv_total[:], in_=inv_total[:])
             if r + 2 < NT:
                 product(NT + r + 2, 0)
             if r == 0:
                 window_diversity(1)
-                nc.vector.tensor_scalar_mul(out=neg_inv_z[:], in0=inv_z_both[:, whole], scalar1=-1.0)
             weighted_diversity(r, 1)
-            if r == 0:
-                attention_factors()
             if r == 1:
                 nc.vector.tensor_scalar_mul(out=win_factor[:], in0=neg_win_factor[:], scalar1=-1.0)
             if r == 4:
@@ -695,8 +705,8 @@ def tile_selfattention_pa_kernel(tc, x, q, k, out_0, out_1, out_2, out_3, out_4)
             logs_of_rest(r)
             for i in LATE_SUMS.get(r, ()):
                 gram_row_sums(i, 1)
-            for i in LATE_SUMS.get(r - 1, ()):
-                finish_row_sums(i, 1)
+            for i, part in READ_SUMS.get(r, ()):
+                finish_row_sums(i, part)
             if 1 < r + 1 < NT:
                 window_diversity(r + 1)
             if r == 3:
@@ -704,6 +714,7 @@ def tile_selfattention_pa_kernel(tc, x, q, k, out_0, out_1, out_2, out_3, out_4)
             if r == 4:
                 weighted_parts(segments[0])
             if r == 5:
+                denominators(segments[1])
                 spread_dep_factor(0)
             if r == 0:
                 window_normaliser()
@@ -723,13 +734,20 @@ def tile_selfattention_pa_kernel(tc, x, q, k, out_0, out_1, out_2, out_3, out_4)
                 entropies()
             if r == 6:
                 total_ps = total_over_tokens(abs_sum[:], 1)
-                denominators(slice(4, 8))
-                for w in range(2):
-                    add_dep_factor(w, 0)
-                inverse_denominators(slice(4, 8))
-                for w in range(3, 5):
-                    add_dep_factor(w, 0)
-                dep_coefficients(slice(4, 8))
+                dep_coefficients(segments[1])
+                add_dep_factor(0, 0)
+                weighted_parts(segments[1])
+                add_dep_factor(1, 0)
+                dep_factors(segments[1])
+                spread_dep_factor(1)
+                add_dep_factor(2, 0)
+                denominators(segments[2])
+                add_dep_factor(3, 0)
+                inverse_denominators(segments[2])
+                add_dep_factor(4, 0)
+                dep_coefficients(segments[2])
+                for w in range(3):
+                    finish_window(w, nc.gpsimd)
         for w in range(3, 5):
             add_dep_factor(w, 1)
         dep_factor_of_last_tile()
@@ -741,18 +759,18 @@ def tile_selfattention_pa_kernel(tc, x, q, k, out_0, out_1, out_2, out_3, out_4)
             finish_window(w, nc.gpsimd)
         for w in range(5, NT):
             add_dep_factor(w, 1)
-        for w in range(6, NT):
-            add_dep_factor(w, 2)
-        nc.vector.reciprocal(out=inv_total[:], in_=inv_total[:])
-        for w in range(NT - 1, 4, -1):
-            finish_window(w, nc.vector)
-        nc.vector.reciprocal(out=inv_div_total[:], in_=div_total_ps[:, 0:1])
         nc.vector.tensor_scalar_mul(
             out=vectors[:, COL_ENT : COL_ENT + NT], in0=entropy_both[:, whole], scalar1=inv_total[:]
         )
+        for w in range(6, NT):
+            add_dep_factor(w, 2)
+        finish_window(5, nc.vector)
+        nc.vector.reciprocal(out=inv_div_total[:], in_=div_total_ps[:, 0:1])
+        finish_window(6, nc.vector)
         nc.vector.tensor_scalar_mul(
             out=vectors[:, COL_DIV : COL_DIV + NT], in0=div_h[:], scalar1=inv_div_total[:]
         )
+        finish_window(7, nc.vector)
 
         vectors_t_ps = psum_t.tile([P, P], F32, tag="t")
         nc.tensor.transpose(vectors_t_ps[:], vectors[:], ident_f32[:])

@@ -27,13 +27,16 @@ LN_T = 10 * 0.6931471805599453
 WIN_STEP = 2 * BLOCK
 WIN = T - WIN_STEP * (NT - 1)
 WIN_BLOCKS = 4
+PAD_LEFT = WIN_STEP
+PAD_RIGHT = 64
 ROW_SHIFT = P - WIN_STEP
 LAST_BLOCK = T % BLOCK
 HUGE = 2.0**100
+GROUPS, BLOCK_GROUP, ZEROS_GROUP = HALVES + 2, HALVES, HALVES + 1
 
 FLOPS = 2 * 2 * T * T * FEAT
 
-COL_ENT_WIN, COL_DIV, COL_ENT, COL_DEP = 0, NT, 2 * NT, 3 * NT
+COL_ENT_WIN, COL_ENT, COL_DEP = 0, NT, 2 * NT
 
 
 def window_pieces(r):
@@ -108,14 +111,16 @@ def tile_selfattention_pa_kernel(tc, x, q, k, out_0, out_1, out_2, out_3, out_4)
             out=outside4[:], in_=inside[:].unsqueeze(3).to_broadcast([P, NT, WIN_BLOCKS, BLOCK])
         )
         outside = outside4[:].rearrange("p r b c -> p r (b c)")
-        keep4 = const.tile([P, NT, WIN_BLOCKS, BLOCK], F32)
+        keep_wide = const.tile([P, NT, PAD_LEFT + WIN_BLOCKS * BLOCK + PAD_RIGHT], F32)
+        nc.gpsimd.memset(keep_wide[:, :, 0:PAD_LEFT], 0.0)
+        nc.gpsimd.memset(keep_wide[:, :, PAD_LEFT + WIN_BLOCKS * BLOCK :], 0.0)
+        keep = keep_wide[:, :, PAD_LEFT : PAD_LEFT + WIN_BLOCKS * BLOCK]
         not_keep4 = const.tile([P, NT, WIN_BLOCKS, BLOCK], F32)
-        keep = keep4[:].rearrange("p r b c -> p r (b c)")
         not_keep = not_keep4[:].rearrange("p r b c -> p r (b c)")
         inside_by_column = inside[:].unsqueeze(3).to_broadcast([P, NT, WIN_BLOCKS, BLOCK])
         nc.vector.tensor_scalar(
-            out=keep4[:], in0=inside_by_column, scalar1=1.0 / HUGE, scalar2=1.0,
-            op0=ALU.mult, op1=ALU.add,
+            out=keep.rearrange("p r (b c) -> p r b c", b=WIN_BLOCKS), in0=inside_by_column,
+            scalar1=1.0 / HUGE, scalar2=1.0, op0=ALU.mult, op1=ALU.add,
         )
         nc.vector.tensor_scalar(
             out=not_keep4[:], in0=inside_by_column, scalar1=-1.0 / HUGE, scalar2=0.0,
@@ -133,10 +138,13 @@ def tile_selfattention_pa_kernel(tc, x, q, k, out_0, out_1, out_2, out_3, out_4)
         nc.gpsimd.memset(zeros[:], 0.0)
         ones = const.tile([P, P], F32)
         nc.gpsimd.memset(ones[:], 1.0)
-        outside_count = const.tile([P, NT], F32)
-        nc.gpsimd.memset(outside_count[:], float(T - BLOCK))
+        neg_max = stats.tile([P, 1 + HALVES, NT], F32)
+        z = stats.tile([P, GROUPS, NT], F32)
+        s = stats.tile([P, GROUPS, NT], F32)
+        nc.gpsimd.memset(s[:, ZEROS_GROUP, :], 0.0)
+        nc.gpsimd.memset(z[:, ZEROS_GROUP, :], float(T - BLOCK))
         nc.gpsimd.affine_select(
-            out=outside_count[:], in_=outside_count[:], compare_op=ALU.is_ge,
+            out=z[:, ZEROS_GROUP, :], in_=z[:, ZEROS_GROUP, :], compare_op=ALU.is_ge,
             fill=float(T - LAST_BLOCK), base=T - LAST_BLOCK - 1, channel_multiplier=-1,
             pattern=[[-P, NT]],
         )
@@ -170,12 +178,8 @@ def tile_selfattention_pa_kernel(tc, x, q, k, out_0, out_1, out_2, out_3, out_4)
                 out=q_codes[:, r, :].bitcast(FP8X4), scales=q_scales[:, r, :], in_=grouped[:]
             )
 
-        def transpose_words(words, warm_ups=0):
+        def transpose_words(words):
             planes = psum_t.tile([P, 2 * PASSES, P], F32, name="planes", tag="t")
-            for i in range(warm_ups):
-                nc.tensor.matmul(
-                    out=planes[:, 0, :], lhsT=ident_f32[:], rhs=ident_f32[:], start=True, stop=True
-                )
             for w in range(2 * PASSES):
                 nc.tensor.transpose(planes[:, w, :], words[:, P * w : P * (w + 1)], ident_f32[:])
             return planes
@@ -189,14 +193,14 @@ def tile_selfattention_pa_kernel(tc, x, q, k, out_0, out_1, out_2, out_3, out_4)
             return grouped
 
         def transpose_q(r):
-            return transpose_words(q_sb[:].bitcast(F32)[:, r, :], 0 if r < 2 else 0)
+            return transpose_words(q_sb[:].bitcast(F32)[:, r, :])
 
         def transpose_u(u_tile):
             return transpose_words(u_tile[:].bitcast(F32))
 
         u_tiles = {}
         sum_sq = stats.tile([P, NT], F32)
-        inv_norm = stats.tile([P, NT], F32)
+        inv_norms = {}
 
         def sum_squares(r):
             squares = junk.tile([P, FEAT], BF16, tag="squares")
@@ -204,17 +208,18 @@ def tile_selfattention_pa_kernel(tc, x, q, k, out_0, out_1, out_2, out_3, out_4)
                 out=squares[:], in_=x_sb[:, r, :], func=ACT.Square, accum_out=sum_sq[:, r : r + 1]
             )
 
-        def inverse_norm(r):
-            col = slice(r, r + 1)
-            nc.gpsimd.tensor_scalar_max(out=inv_norm[:, col], in0=sum_sq[:, col], scalar1=EPS * EPS)
+        def inverse_norm(r, engine):
+            limited = stage.tile([P, 1], F32, name="limited", tag="limited")
+            engine.tensor_scalar_max(out=limited[:], in0=sum_sq[:, r : r + 1], scalar1=EPS * EPS)
+            inv_norms[r] = stage.tile([P, 1], F32, name="inv_norm", tag="inv_norm")
             nc.gpsimd.tensor_tensor(
-                out=inv_norm[:, col], in0=inv_norm[:, col], in1=minus_half[:], op=ALU.pow
+                out=inv_norms[r][:], in0=limited[:], in1=minus_half[:], op=ALU.pow
             )
 
         def scale_x(r):
             u_tiles[r] = stage.tile([P, FEAT], BF16, name="u_tile", tag="u_tile")
             nc.vector.tensor_scalar_mul(
-                out=u_tiles[r][:], in0=x_sb[:, r, :], scalar1=inv_norm[:, r : r + 1]
+                out=u_tiles[r][:], in0=x_sb[:, r, :], scalar1=inv_norms[r][:]
             )
 
         banks = {}
@@ -265,18 +270,11 @@ def tile_selfattention_pa_kernel(tc, x, q, k, out_0, out_1, out_2, out_3, out_4)
 
         e_all = resident.tile([P, NT, T], F32)
         e_win = resident.tile([P, NT, WIN], F32)
-        neg_max_halves = stats.tile([P, HALVES * NT], F32)
-        z_halves = stats.tile([P, HALVES * NT], F32)
-        s_halves = stats.tile([P, HALVES * NT], F32)
-        neg_max_win = stats.tile([P, NT], F32)
-        z_win = stats.tile([P, NT], F32)
-        s_win = stats.tile([P, NT], F32)
         logits = {}
 
         def half_maximum(r, h):
-            col = NT * h + r
             nc.vector.tensor_reduce(
-                out=neg_max_halves[:, col : col + 1], in_=banks[r, h][:], axis=AX.X, op=ALU.max,
+                out=neg_max[:, 1 + h, r : r + 1], in_=banks[r, h][:], axis=AX.X, op=ALU.max,
                 negate=True,
             )
 
@@ -292,36 +290,34 @@ def tile_selfattention_pa_kernel(tc, x, q, k, out_0, out_1, out_2, out_3, out_4)
 
         def window_maximum(r):
             nc.vector.tensor_reduce(
-                out=neg_max_win[:, r : r + 1], in_=logits[r][:], axis=AX.X, op=ALU.max, negate=True
+                out=neg_max[:, 0, r : r + 1], in_=logits[r][:], axis=AX.X, op=ALU.max, negate=True
             )
 
         def exponentials(r, h):
-            col = NT * h + r
             nc.scalar.activation(
                 out=e_all[:, r, BANK * h : BANK * (h + 1)], in_=banks[r, h][:], func=ACT.Exp,
-                bias=neg_max_halves[:, col : col + 1], accum_out=z_halves[:, col : col + 1],
+                bias=neg_max[:, 1 + h, r : r + 1], accum_out=z[:, h, r : r + 1],
             )
 
         def window_exponentials(r):
             nc.scalar.activation(
-                out=e_win[:, r, :], in_=logits[r][:], func=ACT.Exp, bias=neg_max_win[:, r : r + 1],
-                accum_out=z_win[:, r : r + 1],
+                out=e_win[:, r, :], in_=logits[r][:], func=ACT.Exp, bias=neg_max[:, 0, r : r + 1],
+                accum_out=z[:, BLOCK_GROUP, r : r + 1],
             )
 
         def entropy_sum(r, h):
-            col = NT * h + r
             products = junk.tile([P, BANK], F32, tag="products")
             nc.vector.scalar_tensor_tensor(
-                out=products[:], in0=banks[r, h][:], scalar=neg_max_halves[:, col : col + 1],
+                out=products[:], in0=banks[r, h][:], scalar=neg_max[:, 1 + h, r : r + 1],
                 in1=e_all[:, r, BANK * h : BANK * (h + 1)],
-                op0=ALU.add, op1=ALU.mult, accum_out=s_halves[:, col : col + 1],
+                op0=ALU.add, op1=ALU.mult, accum_out=s[:, h, r : r + 1],
             )
 
         def window_entropy_sum(r):
             products = junk.tile([P, WIN], F32, tag="win_products")
             nc.vector.scalar_tensor_tensor(
-                out=products[:], in0=logits[r][:], scalar=neg_max_win[:, r : r + 1],
-                in1=e_win[:, r, :], op0=ALU.add, op1=ALU.mult, accum_out=s_win[:, r : r + 1],
+                out=products[:], in0=logits[r][:], scalar=neg_max[:, 0, r : r + 1],
+                in1=e_win[:, r, :], op0=ALU.add, op1=ALU.mult, accum_out=s[:, BLOCK_GROUP, r : r + 1],
             )
 
         def clear_blocks(r):
@@ -343,37 +339,37 @@ def tile_selfattention_pa_kernel(tc, x, q, k, out_0, out_1, out_2, out_3, out_4)
             q_grouped[r] = regroup(q_planes[r], copy)
 
         k_planes = {}
-        k_planes[0] = transpose_words(k_words[:, 0, :], 4)
-        k_planes[1] = transpose_words(k_words[:, 1, :], 1)
+        k_planes[0] = transpose_words(k_words[:, 0, :])
+        k_planes[1] = transpose_words(k_words[:, 1, :])
         k_grouped[0] = regroup(k_planes[0], on_vector)
         k_grouped[1] = regroup(k_planes[1], on_scalar)
         sum_squares(0)
-        k_planes[2] = transpose_words(k_words[:, 2, :], 1)
+        k_planes[2] = transpose_words(k_words[:, 2, :])
         quantise_k(0)
         quantise_k(1)
         k_grouped[2] = regroup(k_planes[2], on_vector)
-        k_planes[3] = transpose_words(k_words[:, 3, :], 1)
+        k_planes[3] = transpose_words(k_words[:, 3, :])
         k_grouped[3] = regroup(k_planes[3], on_scalar)
         q_planes[0] = transpose_q(0)
         q_grouped[0] = regroup(q_planes[0], on_scalar)
-        inverse_norm(0)
+        inverse_norm(0, nc.gpsimd)
         quantise_k(2)
         quantise_k(3)
-        k_planes[4] = transpose_words(k_words[:, 4, :], 1)
+        k_planes[4] = transpose_words(k_words[:, 4, :])
         quantise_q_tile(q_grouped[0], 0)
         k_grouped[4] = regroup(k_planes[4], on_vector)
-        k_planes[5] = transpose_words(k_words[:, 5, :], 1)
+        k_planes[5] = transpose_words(k_words[:, 5, :])
         k_grouped[5] = regroup(k_planes[5], on_scalar)
         q_planes[1] = transpose_q(1)
         q_grouped[1] = regroup(q_planes[1], on_scalar)
         scale_x(0)
-        k_planes[6] = transpose_words(k_words[:, 6, :], 1)
+        k_planes[6] = transpose_words(k_words[:, 6, :])
         product(0, 0)
         quantise_k(4)
         quantise_q_tile(q_grouped[1], 1)
         quantise_k(5)
         k_grouped[6] = regroup(k_planes[6], on_scalar)
-        k_planes[7] = transpose_words(k_words[:, 7, :], 1)
+        k_planes[7] = transpose_words(k_words[:, 7, :])
         sum_squares(1)
         k_grouped[7] = regroup(k_planes[7], on_scalar)
         u_planes[0] = transpose_u(u_tiles[0])
@@ -382,7 +378,7 @@ def tile_selfattention_pa_kernel(tc, x, q, k, out_0, out_1, out_2, out_3, out_4)
         window_logits(0, 0)
         product(1, 0)
         exponentials(0, 0)
-        inverse_norm(1)
+        inverse_norm(1, nc.gpsimd)
         quantise_k(6)
         quantise_k(7)
         q_planes[2] = transpose_q(2)
@@ -396,7 +392,7 @@ def tile_selfattention_pa_kernel(tc, x, q, k, out_0, out_1, out_2, out_3, out_4)
         entropy_sum(0, 0)
         quantise_tile(u_grouped[0], u_codes, u_scales, 0)
         quantise_q_tile(q_grouped[2], 2)
-        inverse_norm(2)
+        inverse_norm(2, nc.gpsimd)
         product(2, 0)
         half_maximum(0, 1)
         window_logits(0, 1)
@@ -406,60 +402,58 @@ def tile_selfattention_pa_kernel(tc, x, q, k, out_0, out_1, out_2, out_3, out_4)
         u_planes[1] = transpose_u(u_tiles[1])
         q_planes[3] = transpose_q(3)
 
-        diffs = stats.tile([P, 3 + HALVES, NT], F32)
-        exps = stats.tile([P, 3 + HALVES, NT], F32)
-        neg_max = stats.tile([P, NT], F32)
-        z_both = stats.tile([P, 2 * NT], F32)
-        s_both = stats.tile([P, 2 * NT], F32)
-        inv_z_both = stats.tile([P, 2 * NT], F32)
-        neg_inv_z = stats.tile([P, NT], F32)
-        ln_z_both = stats.tile([P, 2 * NT], F32)
+        diffs = stats.tile([P, 1 + GROUPS, NT], F32)
+        exps = stats.tile([P, 1 + GROUPS, NT], F32)
+        neg_row_max = stats.tile([P, NT], F32)
+        z_groups = stats.tile([P, GROUPS, NT], F32)
+        z_both = stats.tile([P, 2, NT], F32)
+        inv_z_both = stats.tile([P, 2, NT], F32)
+        s_groups = stats.tile([P, GROUPS, NT], F32)
+        s_both = stats.tile([P, 2, NT], F32)
+        ln_z_both = stats.tile([P, 2, NT], F32)
         half_factor = stats.tile([P, HALVES, NT], F32)
         win_factor = stats.tile([P, NT], F32)
         neg_win_factor = stats.tile([P, NT], F32)
-        rest = stats.tile([P, NT], F32)
-        scaled = stats.tile([P, HALVES, NT], F32)
-        whole, window = slice(0, NT), slice(NT, 2 * NT)
-        z_by_half = z_halves[:].rearrange("p (h r) -> p h r", h=HALVES)
-        s_by_half = s_halves[:].rearrange("p (h r) -> p h r", h=HALVES)
-        m_by_half = neg_max_halves[:].rearrange("p (h r) -> p h r", h=HALVES)
 
-        def by_half(column):
-            return column.unsqueeze(1).to_broadcast([P, HALVES, NT])
+        def spread(column, n):
+            return column.unsqueeze(1).to_broadcast([P, n, NT])
 
         def row_maxima():
             nc.vector.tensor_tensor(
-                out=neg_max[:], in0=m_by_half[:, 0, :], in1=m_by_half[:, 1, :], op=ALU.min
+                out=neg_row_max[:], in0=neg_max[:, 1, :], in1=neg_max[:, 2, :], op=ALU.min
             )
-            nc.vector.tensor_scalar_min(out=diffs[:, 2, :], in0=neg_max_win[:], scalar1=0.0)
+            nc.vector.tensor_scalar_min(out=diffs[:, 4, :], in0=neg_max[:, 0, :], scalar1=0.0)
 
         def maximum_differences():
             nc.vector.tensor_sub(
-                out=diffs[:, 3 : 3 + HALVES, :], in0=by_half(neg_max[:]), in1=m_by_half
+                out=diffs[:, 0:3, :], in0=spread(neg_row_max[:], 3), in1=neg_max[:]
             )
-            nc.vector.tensor_sub(out=diffs[:, 0, :], in0=neg_max[:], in1=neg_max_win[:])
-            nc.vector.tensor_sub(out=diffs[:, 1, :], in0=diffs[:, 2, :], in1=neg_max_win[:])
+            nc.vector.tensor_sub(out=diffs[:, 3, :], in0=diffs[:, 4, :], in1=neg_max[:, 0, :])
             nc.scalar.activation(out=exps[:], in_=diffs[:], func=ACT.Exp)
 
-        def whole_normaliser():
-            nc.vector.tensor_mul(out=scaled[:], in0=z_by_half, in1=exps[:, 3 : 3 + HALVES, :])
+        def by_softmax(groups):
+            return groups.rearrange("p (m i) r -> p m i r", i=2)
 
-        def add_halves():
-            nc.vector.tensor_add(out=z_both[:, whole], in0=scaled[:, 0, :], in1=scaled[:, 1, :])
+        def scale_normalisers():
+            nc.vector.tensor_mul(out=z_groups[:], in0=z[:], in1=exps[:, 1:, :])
 
-        def inverse_normaliser():
-            nc.vector.reciprocal(out=inv_z_both[:, whole], in_=z_both[:, whole])
+        def add_normalisers():
+            parts = by_softmax(z_groups[:])
+            nc.vector.tensor_add(out=z_both[:], in0=parts[:, :, 0, :], in1=parts[:, :, 1, :])
+
+        def inverse_normalisers():
+            nc.vector.reciprocal(out=inv_z_both[:], in_=z_both[:])
 
         def attention_factors():
-            nc.vector.tensor_scalar_mul(out=neg_inv_z[:], in0=inv_z_both[:, whole], scalar1=-1.0)
-
-        def half_and_window_factors():
-            nc.vector.tensor_mul(
-                out=half_factor[:], in0=exps[:, 3 : 3 + HALVES, :], in1=by_half(neg_inv_z[:])
+            nc.vector.scalar_tensor_tensor(
+                out=half_factor[:], in0=exps[:, 1:3, :], scalar=-1.0,
+                in1=spread(inv_z_both[:, 0, :], HALVES), op0=ALU.mult, op1=ALU.mult,
             )
-            nc.vector.tensor_mul(out=neg_win_factor[:], in0=exps[:, 0, :], in1=neg_inv_z[:])
+            nc.vector.scalar_tensor_tensor(
+                out=neg_win_factor[:], in0=exps[:, 0, :], scalar=-1.0,
+                in1=inv_z_both[:, 0, :], op0=ALU.mult, op1=ALU.mult,
+            )
 
-        CLEARED_EARLY = 3
         WINDOW_STEPS = {4: (0, 1, 2), 5: (3, 4), 6: (5, 6, 7)}
 
         EARLY_SUMS = {3: (0, 1), 4: (2, 3), 5: (4, 5), 6: (6,), 7: (7,)}
@@ -477,17 +471,18 @@ def tile_selfattention_pa_kernel(tc, x, q, k, out_0, out_1, out_2, out_3, out_4)
                 if (r, h) != (0, 0):
                     entropy_sum(r, h)
                     if (r, h) == (NT - 1, 0):
-                        whole_normaliser()
+                        scale_normalisers()
                     if r + 2 < NT:
                         product(r + 2, h)
             if r + 3 < NT:
                 sum_squares(r + 3)
-                inverse_norm(r + 3)
-                if r + 3 >= NT - CLEARED_EARLY:
-                    clear_blocks(r + 3 - NT + CLEARED_EARLY)
-                quantise_q_tile(q_grouped[r + 3], r + 3)
+                inverse_norm(r + 3, nc.gpsimd)
+                clear_blocks(r)
             if r + 1 < NT:
                 window_maximum(r + 1)
+            if r + 3 < NT:
+                quantise_q_tile(q_grouped[r + 3], r + 3)
+            if r + 1 < NT:
                 quantise_tile(u_grouped[r + 1], u_codes, u_scales, r + 1)
             if r + 2 >= NT:
                 for h in range(HALVES):
@@ -500,13 +495,10 @@ def tile_selfattention_pa_kernel(tc, x, q, k, out_0, out_1, out_2, out_3, out_4)
             for i in WINDOW_STEPS.get(r, ()):
                 window_exponentials(i)
             if r == NT - 1:
-                add_halves()
-            for i in WINDOW_STEPS.get(r - 1, ()):
-                window_entropy_sum(i)
-                if i == 5:
-                    inverse_normaliser()
-                if i == 6:
-                    attention_factors()
+                add_normalisers()
+                window_entropy_sum(0)
+                inverse_normalisers()
+                window_entropy_sum(1)
             if r < NT - 2:
                 for i in EARLY_SUMS.get(r, ()):
                     finish_row_sums(i, 0)
@@ -518,12 +510,6 @@ def tile_selfattention_pa_kernel(tc, x, q, k, out_0, out_1, out_2, out_3, out_4)
             if r == NT - 2:
                 row_maxima()
                 maximum_differences()
-
-        def window_normaliser():
-            nc.gpsimd.tensor_mul(out=rest[:], in0=exps[:, 2, :], in1=outside_count[:])
-            nc.gpsimd.tensor_mul(out=z_both[:, window], in0=z_win[:], in1=exps[:, 1, :])
-            nc.gpsimd.tensor_mul(out=s_both[:, window], in0=z_both[:, window], in1=diffs[:, 1, :])
-            nc.gpsimd.tensor_add(out=z_both[:, window], in0=z_both[:, window], in1=rest[:])
 
         LATE_SUMS = {0: (2, 3), 1: (4, 5), 2: (6, 7)}
         READ_SUMS = {
@@ -563,40 +549,40 @@ def tile_selfattention_pa_kernel(tc, x, q, k, out_0, out_1, out_2, out_3, out_4)
                 op0=ALU.add, op1=ALU.mult, accum_out=weighted_sums[:, h, r : r + 1],
             )
 
-        def total_over_tokens(partial, columns):
-            total_ps = psum_t.tile([P, NT], F32, name="total_ps", tag="t")
-            nc.tensor.matmul(
-                out=total_ps[:, 0:columns], lhsT=ones[:], rhs=partial, start=True, stop=True
-            )
+        def total_over_tokens(partial, pool, tag):
+            total_ps = pool.tile([P, BANK], F32, name="total_ps", tag=tag)
+            nc.tensor.matmul(out=total_ps[:, 0:1], lhsT=ones[:], rhs=partial, start=True, stop=True)
             return total_ps
 
-        entropy_both = stats.tile([P, 2 * NT], F32)
+        entropy_both = stats.tile([P, 2, NT], F32)
+        entropy = stats.tile([P, NT], F32)
         abs_entropy = stats.tile([P, NT], F32)
         abs_sum = stats.tile([P, 1], F32)
         inv_total = stats.tile([P, 1], F32)
 
-        def window_entropy_parts():
-            nc.gpsimd.tensor_mul(out=s_win[:], in0=s_win[:], in1=exps[:, 1, :])
-            nc.gpsimd.tensor_mul(out=rest[:], in0=rest[:], in1=diffs[:, 2, :])
-            nc.gpsimd.tensor_add(out=s_win[:], in0=s_win[:], in1=rest[:])
-            nc.gpsimd.tensor_add(out=s_both[:, window], in0=s_both[:, window], in1=s_win[:])
+        def shifted_sums():
+            nc.gpsimd.tensor_mul(out=s_groups[:], in0=s[:], in1=exps[:, 1:, :])
+            nc.gpsimd.tensor_mul(out=z_groups[:], in0=z_groups[:], in1=diffs[:, 1:, :])
+            nc.gpsimd.tensor_add(out=s_groups[:], in0=s_groups[:], in1=z_groups[:])
+            parts = by_softmax(s_groups[:])
+            nc.gpsimd.tensor_add(out=s_both[:], in0=parts[:, :, 0, :], in1=parts[:, :, 1, :])
 
         def entropies():
             nc.gpsimd.tensor_mul(out=entropy_both[:], in0=s_both[:], in1=inv_z_both[:])
             nc.gpsimd.tensor_sub(out=entropy_both[:], in0=ln_z_both[:], in1=entropy_both[:])
-            nc.gpsimd.tensor_scalar_mul(out=entropy_both[:], in0=entropy_both[:], scalar1=1.0 / LN_T)
-            nc.gpsimd.tensor_copy(
-                out=vectors[:, COL_ENT_WIN : COL_ENT_WIN + NT], in_=entropy_both[:, window]
-            )
+            for out, plane in ((entropy[:], 0), (vectors[:, COL_ENT_WIN : COL_ENT_WIN + NT], 1)):
+                nc.gpsimd.tensor_scalar(
+                    out=out, in0=entropy_both[:, plane, :], scalar1=1.0 / LN_T, scalar2=0.0,
+                    op0=ALU.mult, op1=ALU.add,
+                )
             nc.scalar.activation(
-                out=abs_entropy[:], in_=entropy_both[:, whole], func=ACT.Abs, accum_out=abs_sum[:]
+                out=abs_entropy[:], in_=entropy[:], func=ACT.Abs, accum_out=abs_sum[:]
             )
 
         denom = stats.tile([P, NT], F32)
         dep_coef = stats.tile([P, HALVES, NT], F32)
         dep_parts = stats.tile([P, HALVES, NT], F32)
         segments = [slice(0, 4), slice(4, 7), slice(7, 8)]
-        dep_rows = {}
 
         def denominators(tiles):
             nc.vector.tensor_reduce(
@@ -639,144 +625,142 @@ def tile_selfattention_pa_kernel(tc, x, q, k, out_0, out_1, out_2, out_3, out_4)
                 scalar1=dep_coef[:, 1, NT - 1 : NT], scalar2=last_part[:], op0=ALU.mult, op1=ALU.add,
             )
 
-        def spread_dep_factor(s):
-            tiles = segments[s]
-            dep_rows[s] = psum_t.tile([P, BANK], F32, name="dep_rows", tag="t")
-            for j in range(tiles.start, tiles.stop):
-                i = j - tiles.start
-                col = COL_DEP + j
-                nc.tensor.transpose(
-                    dep_rows[s][:, P * i : P * (i + 1)],
-                    vectors[:, col : col + 1].to_broadcast([P, P]), ident_f32[:],
-                )
+        diagonals, dep_windows = {}, {}
 
-        att_wins = {}
-
-        def add_dep_factor(r, s):
-            lo = WIN_STEP * r
-            seg_first, seg_last = P * segments[s].start, P * segments[s].stop
-            first, last = max(lo, seg_first), min(lo + WIN, seg_last)
-            if r not in att_wins:
-                att_wins[r] = stage.tile([P, WIN], F32, name="att_win", tag="att_win", bufs=NT)
-            nc.vector.scalar_tensor_tensor(
-                out=att_wins[r][:, first - lo : last - lo],
-                in0=e_win[:, r, first - lo : last - lo], scalar=win_factor[:, r : r + 1],
-                in1=dep_rows[s][:, first - seg_first : last - seg_first],
-                op0=ALU.mult, op1=ALU.add,
+        def diagonal(c, engine):
+            diagonals[c] = stage.tile([P, P], F32, name="diagonal", tag="diagonal", bufs=NT)
+            engine.tensor_scalar(
+                out=diagonals[c][:], in0=ident_f32[:], scalar1=vectors[:, COL_DEP + c : COL_DEP + c + 1],
+                scalar2=0.0, op0=ALU.mult, op1=ALU.add,
             )
 
-        def finish_window(r, engine):
-            engine.tensor_mul(out=att_wins[r][:], in0=att_wins[r][:], in1=keep[:, r, 0:WIN])
+        def spread_dep_factor(r, tiles):
             lo = WIN_STEP * r
-            nc.sync.dma_start(out=out_0[P * r : P * (r + 1), lo : lo + WIN], in_=att_wins[r][:])
+            if r not in dep_windows:
+                dep_windows[r] = psum_t.tile([P, WIN], F32, name="dep_window", tag="t")
+            for c in range(max(r - 1, tiles.start), min(r + 2, tiles.stop)):
+                first, last = max(lo, P * c), min(lo + WIN, P * (c + 1))
+                rows = PAD_LEFT + P * r - WIN_STEP * c
+                if first < last:
+                    nc.tensor.matmul(
+                        out=dep_windows[r][:, first - lo : last - lo],
+                        lhsT=keep_wide[:, c, rows : rows + P],
+                        rhs=diagonals[c][:, first - P * c : last - P * c], start=True, stop=True,
+                    )
+
+        def finish_window(r):
+            lo = WIN_STEP * r
+            att_win = stage.tile([P, WIN], F32, name="att_win", tag="att_win", bufs=NT)
+            nc.vector.scalar_tensor_tensor(
+                out=att_win[:], in0=e_win[:, r, :], scalar=win_factor[:, r : r + 1],
+                in1=dep_windows[r][:], op0=ALU.mult, op1=ALU.add,
+            )
+            nc.sync.dma_start(out=out_0[P * r : P * (r + 1), lo : lo + WIN], in_=att_win[:])
 
         ln_sums = stats.tile([P, NT], F32)
-        div_h = stats.tile([P, NT], F32)
+        div_h = stats.tile([P, P], F32)
+        nc.gpsimd.memset(div_h[:], 0.0)
         div_sum = stats.tile([P, 1], F32)
         inv_div_total = stats.tile([P, 1], F32)
 
-        half_and_window_factors()
+        def by_token(vector):
+            return vector.rearrange("(r p) -> r p", p=P)
+
+        attention_factors()
         window_diversity(0)
+        for r in range(NT - 3, NT):
+            clear_blocks(r)
         for r in range(NT):
             weighted_diversity(r, 0)
             if r == 4:
                 inverse_denominators(segments[0])
             if r == 5:
                 dep_factors(segments[0])
+                for c in range(4):
+                    diagonal(c, nc.gpsimd)
             if r == 6:
                 inverse_denominators(segments[1])
-            if r == 7:
                 nc.vector.tensor_scalar_max(out=inv_total[:], in0=total_ps[:, 0:1], scalar1=EPS)
-                first_part_of_last_tile()
-                nc.vector.reciprocal(out=inv_total[:], in_=inv_total[:])
+            if r == 7:
+                dep_coefficients(segments[2])
+                nc.vector.tensor_scalar_mul(
+                    out=vectors[:, COL_ENT : COL_ENT + NT], in0=entropy[:], scalar1=inv_total[:]
+                )
             if r + 2 < NT:
                 product(NT + r + 2, 0)
             if r == 0:
                 window_diversity(1)
             weighted_diversity(r, 1)
             if r == 1:
-                nc.vector.tensor_scalar_mul(out=win_factor[:], in0=neg_win_factor[:], scalar1=-1.0)
+                nc.vector.tensor_mul(out=win_factor[:], in0=exps[:, 0, :], in1=inv_z_both[:, 0, :])
             if r == 4:
                 dep_coefficients(segments[0])
+            if r < 3:
+                for i in range(2):
+                    window_entropy_sum(2 + 2 * r + i)
             if r + 2 < NT:
                 product(NT + r + 2, 1)
-            if CLEARED_EARLY <= r + 2 < NT:
-                clear_blocks(r + 2)
             logs_of_rest(r)
-            for i in LATE_SUMS.get(r, ()):
-                gram_row_sums(i, 1)
             for i, part in READ_SUMS.get(r, ()):
                 finish_row_sums(i, part)
+            for i in LATE_SUMS.get(r, ()):
+                gram_row_sums(i, 1)
             if 1 < r + 1 < NT:
                 window_diversity(r + 1)
             if r == 3:
                 denominators(segments[0])
+                shifted_sums()
+                nc.scalar.activation(out=ln_z_both[:], in_=z_both[:], func=ACT.Ln)
             if r == 4:
                 weighted_parts(segments[0])
+                entropies()
             if r == 5:
                 denominators(segments[1])
-                spread_dep_factor(0)
-            if r == 0:
-                window_normaliser()
-            if r == 1:
-                nc.gpsimd.tensor_mul(out=scaled[:], in0=scaled[:], in1=diffs[:, 3 : 3 + HALVES, :])
-                nc.gpsimd.tensor_mul(out=s_by_half, in0=s_by_half, in1=exps[:, 3 : 3 + HALVES, :])
-                nc.gpsimd.tensor_add(out=scaled[:], in0=scaled[:], in1=s_by_half)
-                nc.gpsimd.tensor_add(
-                    out=s_both[:, whole], in0=scaled[:, 0, :], in1=scaled[:, 1, :]
-                )
-            if r == 2:
-                nc.vector.reciprocal(out=inv_z_both[:, window], in_=z_both[:, window])
-                nc.scalar.activation(out=ln_z_both[:], in_=z_both[:], func=ACT.Ln)
-            if r == 3:
-                window_entropy_parts()
-            if r == 4:
-                entropies()
-            if r == 6:
-                total_ps = total_over_tokens(abs_sum[:], 1)
-                dep_coefficients(segments[1])
-                add_dep_factor(0, 0)
-                weighted_parts(segments[1])
-                add_dep_factor(1, 0)
-                dep_factors(segments[1])
-                spread_dep_factor(1)
-                add_dep_factor(2, 0)
-                denominators(segments[2])
-                add_dep_factor(3, 0)
-                inverse_denominators(segments[2])
-                add_dep_factor(4, 0)
-                dep_coefficients(segments[2])
+                total_ps = total_over_tokens(abs_sum[:], psum_t, "t")
                 for w in range(3):
-                    finish_window(w, nc.gpsimd)
-        for w in range(3, 5):
-            add_dep_factor(w, 1)
+                    spread_dep_factor(w, segments[0])
+            if r == 6:
+                dep_coefficients(segments[1])
+                finish_window(0)
+                weighted_parts(segments[1])
+                finish_window(1)
+                dep_factors(segments[1])
+                denominators(segments[2])
+                finish_window(2)
+                for c in range(4, 7):
+                    diagonal(c, nc.vector)
+                for w in range(3, 6):
+                    spread_dep_factor(w, slice(0, NT - 1))
+                inverse_denominators(segments[2])
+                nc.vector.reciprocal(out=inv_total[:], in_=inv_total[:])
+            if r == 7:
+                nc.vector.tensor_reduce(out=ln_sums[:], in_=ln_parts[:], axis=AX.X, op=ALU.add)
+        nc.scalar.activation(
+            out=div_h[:, 0:NT], in_=ln_sums[:], func=ACT.Exp, accum_out=div_sum[:]
+        )
+        first_part_of_last_tile()
+        finish_window(3)
         dep_factor_of_last_tile()
-        spread_dep_factor(2)
-        nc.vector.tensor_reduce(out=ln_sums[:], in_=ln_parts[:], axis=AX.X, op=ALU.add)
-        nc.scalar.activation(out=div_h[:], in_=ln_sums[:], func=ACT.Exp, accum_out=div_sum[:])
-        div_total_ps = total_over_tokens(div_sum[:], 1)
-        for w in range(3, 5):
-            finish_window(w, nc.gpsimd)
-        for w in range(5, NT):
-            add_dep_factor(w, 1)
-        nc.vector.tensor_scalar_mul(
-            out=vectors[:, COL_ENT : COL_ENT + NT], in0=entropy_both[:, whole], scalar1=inv_total[:]
-        )
+        finish_window(4)
+        diagonal(7, nc.vector)
         for w in range(6, NT):
-            add_dep_factor(w, 2)
-        finish_window(5, nc.vector)
-        nc.vector.reciprocal(out=inv_div_total[:], in_=div_total_ps[:, 0:1])
-        finish_window(6, nc.vector)
-        nc.vector.tensor_scalar_mul(
-            out=vectors[:, COL_DIV : COL_DIV + NT], in0=div_h[:], scalar1=inv_div_total[:]
-        )
-        finish_window(7, nc.vector)
+            spread_dep_factor(w, slice(0, NT - 1))
+        total_ps = total_over_tokens(div_sum[:], psum_mm, "bank0")
+        div_t_ps = psum_mm.tile([P, BANK], F32, name="div_t_ps", tag="bank1")
+        nc.tensor.transpose(div_t_ps[:, 0:P], div_h[:], ident_f32[:])
+        for w in range(6, NT):
+            spread_dep_factor(w, segments[2])
+        vectors_t_ps = psum_mm.tile([P, BANK], F32, name="vectors_t_ps", tag="bank0")
+        nc.tensor.transpose(vectors_t_ps[:, 0:P], vectors[:], ident_f32[:])
+        finish_window(5)
+        nc.vector.reciprocal(out=inv_div_total[:], in_=total_ps[:, 0:1])
+        finish_window(6)
+        div_t = stats.tile([P, P], F32)
+        nc.vector.tensor_scalar_mul(out=div_t[:], in0=div_t_ps[:, 0:P], scalar1=inv_div_total[:])
+        nc.sync.dma_start(out=by_token(out_2), in_=div_t[0:NT, :])
+        finish_window(7)
 
-        vectors_t_ps = psum_t.tile([P, P], F32, tag="t")
-        nc.tensor.transpose(vectors_t_ps[:], vectors[:], ident_f32[:])
         vectors_t = stats.tile([P, P], F32)
-        nc.scalar.copy(out=vectors_t[:], in_=vectors_t_ps[:])
-        for out_vec, col in ((out_1, COL_ENT_WIN), (out_2, COL_DIV), (out_3, COL_ENT), (out_4, COL_DEP)):
-            nc.sync.dma_start(
-                out=out_vec.rearrange("(r p) -> r p", p=P), in_=vectors_t[col : col + NT, :]
-            )
+        nc.scalar.copy(out=vectors_t[:], in_=vectors_t_ps[:, 0:P])
+        for out_vec, col in ((out_1, COL_ENT_WIN), (out_3, COL_ENT), (out_4, COL_DEP)):
+            nc.sync.dma_start(out=by_token(out_vec), in_=vectors_t[col : col + NT, :])

@@ -112,33 +112,29 @@ def tile_selfattention_pa_kernel(tc, x, q, k, out_0, out_1, out_2, out_3, out_4)
         )
         outside = outside4[:].rearrange("p r b c -> p r (b c)")
         keep_wide = const.tile([P, NT, PAD_LEFT + WIN_BLOCKS * BLOCK + PAD_RIGHT], F32)
-        nc.gpsimd.memset(keep_wide[:, :, 0:PAD_LEFT], 0.0)
-        nc.gpsimd.memset(keep_wide[:, :, PAD_LEFT + WIN_BLOCKS * BLOCK :], 0.0)
+        nc.vector.memset(keep_wide[:, :, 0:PAD_LEFT], 0.0)
+        nc.vector.memset(keep_wide[:, :, PAD_LEFT + WIN_BLOCKS * BLOCK :], 0.0)
         keep = keep_wide[:, :, PAD_LEFT : PAD_LEFT + WIN_BLOCKS * BLOCK]
-        not_keep4 = const.tile([P, NT, WIN_BLOCKS, BLOCK], F32)
-        not_keep = not_keep4[:].rearrange("p r b c -> p r (b c)")
+        minus_half = const.tile([P, 1], F32)
+        nc.vector.memset(minus_half[:], -0.5)
+        denom_parts = stats.tile([P, 5, NT], F32)
+        nc.vector.memset(denom_parts[:], 0.0)
+        nc.vector.memset(denom_parts[:, 4, :], float(T))
+        weighted_sums = stats.tile([P, HALVES, NT], F32)
+        vectors = stats.tile([P, P], F32)
+        nc.vector.memset(vectors[:], 0.0)
+        div_h = stats.tile([P, P], F32)
+        nc.vector.memset(div_h[:], 0.0)
+        zeros = const.tile([P, T - WIN], F32)
+        nc.vector.memset(zeros[:], 0.0)
+        ones = const.tile([P, P], F32)
+        nc.vector.memset(ones[:], 1.0)
+        neg_max = stats.tile([P, 1 + HALVES, NT], F32)
         inside_by_column = inside[:].unsqueeze(3).to_broadcast([P, NT, WIN_BLOCKS, BLOCK])
         nc.vector.tensor_scalar(
             out=keep.rearrange("p r (b c) -> p r b c", b=WIN_BLOCKS), in0=inside_by_column,
             scalar1=1.0 / HUGE, scalar2=1.0, op0=ALU.mult, op1=ALU.add,
         )
-        nc.vector.tensor_scalar(
-            out=not_keep4[:], in0=inside_by_column, scalar1=-1.0 / HUGE, scalar2=0.0,
-            op0=ALU.mult, op1=ALU.add,
-        )
-        minus_half = const.tile([P, 1], F32)
-        nc.gpsimd.memset(minus_half[:], -0.5)
-        denom_parts = stats.tile([P, 5, NT], F32)
-        nc.gpsimd.memset(denom_parts[:], 0.0)
-        nc.gpsimd.memset(denom_parts[:, 4, :], float(T))
-        weighted_sums = stats.tile([P, HALVES, NT], F32)
-        vectors = stats.tile([P, P], F32)
-        nc.gpsimd.memset(vectors[:], 0.0)
-        zeros = const.tile([P, T - WIN], F32)
-        nc.gpsimd.memset(zeros[:], 0.0)
-        ones = const.tile([P, P], F32)
-        nc.gpsimd.memset(ones[:], 1.0)
-        neg_max = stats.tile([P, 1 + HALVES, NT], F32)
         z = stats.tile([P, GROUPS, NT], F32)
         s = stats.tile([P, GROUPS, NT], F32)
         nc.gpsimd.memset(s[:, ZEROS_GROUP, :], 0.0)
@@ -244,11 +240,14 @@ def tile_selfattention_pa_kernel(tc, x, q, k, out_0, out_1, out_2, out_3, out_4)
             banks[j, h] = bank
 
         accs = {}
+        FIRST_BLOCKS = [NT // 2 + r // 2 for r in range(NT)]
 
-        def gram_row_sums(r, part, blocks=NT // 2):
+        def gram_row_sums(r, part):
             rows = slice(P * r, P * (r + 1))
             acc = psum_t.tile([P, P], F32, name="acc", tag="t")
-            order = [(g, c) for g in range(PASSES) for c in range(part * (NT // 2), part * (NT // 2) + blocks)]
+            first_blocks = FIRST_BLOCKS[r]
+            blocks = range(first_blocks, NT) if part else range(first_blocks)
+            order = [(g, c) for g in range(PASSES) for c in blocks]
             for i, (g, c) in enumerate(order):
                 cols = slice(P * c, P * (c + 1))
                 nc.tensor.matmul_mx(
@@ -321,8 +320,14 @@ def tile_selfattention_pa_kernel(tc, x, q, k, out_0, out_1, out_2, out_3, out_4)
             )
 
         def clear_blocks(r):
-            window = e_all[:, r, WIN_STEP * r : WIN_STEP * r + WIN]
-            nc.gpsimd.tensor_mul(out=window, in0=window, in1=not_keep[:, r, 0:WIN])
+            zero_first = 0 if r >= NT // 2 else T - BLOCK
+            for block in range(P * r // BLOCK, (P * (r + 1) - 1) // BLOCK + 1):
+                first, last = BLOCK * block, min(BLOCK * (block + 1), T)
+                row_first, row_last = max(first, P * r), min(last, P * (r + 1))
+                nc.sync.dma_start(
+                    out=e_all[row_first - P * r : row_last - P * r, r, first:last],
+                    in_=out_0[row_first:row_last, zero_first : zero_first + last - first],
+                )
 
         k_words = k_sb[:].bitcast(F32)
         k_grouped, q_planes, u_planes, q_grouped, u_grouped = {}, {}, {}, {}, {}
@@ -456,7 +461,7 @@ def tile_selfattention_pa_kernel(tc, x, q, k, out_0, out_1, out_2, out_3, out_4)
 
         WINDOW_STEPS = {4: (0, 1, 2), 5: (3, 4), 6: (5, 6, 7)}
 
-        EARLY_SUMS = {3: (0, 1), 4: (2, 3), 5: (4, 5), 6: (6,), 7: (7,)}
+        EARLY_SUMS = {3: (0, 1), 4: (2, 3), 5: (4, 5), 6: (6, 7)}
 
         for r in range(NT):
             if r + 3 < NT:
@@ -470,7 +475,7 @@ def tile_selfattention_pa_kernel(tc, x, q, k, out_0, out_1, out_2, out_3, out_4)
                     exponentials(r + 1, h)
                 if (r, h) != (0, 0):
                     entropy_sum(r, h)
-                    if (r, h) == (NT - 1, 0):
+                    if (r, h) == (NT - 1, 1):
                         scale_normalisers()
                     if r + 2 < NT:
                         product(r + 2, h)
@@ -489,9 +494,6 @@ def tile_selfattention_pa_kernel(tc, x, q, k, out_0, out_1, out_2, out_3, out_4)
                     product(r + 2, h)
             for i in EARLY_SUMS.get(r, ()):
                 gram_row_sums(i, 0)
-            if r == NT - 1:
-                for i in range(2):
-                    gram_row_sums(i, 1)
             for i in WINDOW_STEPS.get(r, ()):
                 window_exponentials(i)
             if r == NT - 1:
@@ -511,11 +513,8 @@ def tile_selfattention_pa_kernel(tc, x, q, k, out_0, out_1, out_2, out_3, out_4)
                 row_maxima()
                 maximum_differences()
 
-        LATE_SUMS = {0: (2, 3), 1: (4, 5), 2: (6, 7)}
-        READ_SUMS = {
-            0: ((6, 0), (7, 0), (0, 1)), 1: ((1, 1), (2, 1), (3, 1)), 2: ((4, 1), (5, 1)),
-            3: ((6, 1), (7, 1)),
-        }
+        LATE_SUMS = {0: (0, 1), 1: (2, 3), 2: (4, 5, 6, 7)}
+        READ_SUMS = {0: ((6, 0), (7, 0)), 1: ((0, 1), (1, 1)), 2: ((2, 1), (3, 1)), 3: ((4, 1), (5, 1), (6, 1), (7, 1))}
 
         ln_parts = stats.tile([P, NT, HALVES + 1], F32)
 
@@ -627,11 +626,17 @@ def tile_selfattention_pa_kernel(tc, x, q, k, out_0, out_1, out_2, out_3, out_4)
 
         diagonals, dep_windows = {}, {}
 
-        def diagonal(c, engine):
+        def diagonal_on_scalar(c):
             diagonals[c] = stage.tile([P, P], F32, name="diagonal", tag="diagonal", bufs=NT)
-            engine.tensor_scalar(
-                out=diagonals[c][:], in0=ident_f32[:], scalar1=vectors[:, COL_DEP + c : COL_DEP + c + 1],
-                scalar2=0.0, op0=ALU.mult, op1=ALU.add,
+            nc.scalar.activation(
+                out=diagonals[c][:], in_=ident_f32[:], func=ACT.Copy,
+                scale=vectors[:, COL_DEP + c : COL_DEP + c + 1],
+            )
+
+        def diagonal_on_vector(c):
+            diagonals[c] = stage.tile([P, P], F32, name="diagonal", tag="diagonal", bufs=NT)
+            nc.vector.tensor_scalar_mul(
+                out=diagonals[c][:], in0=ident_f32[:], scalar1=vectors[:, COL_DEP + c : COL_DEP + c + 1]
             )
 
         def spread_dep_factor(r, tiles):
@@ -658,8 +663,6 @@ def tile_selfattention_pa_kernel(tc, x, q, k, out_0, out_1, out_2, out_3, out_4)
             nc.sync.dma_start(out=out_0[P * r : P * (r + 1), lo : lo + WIN], in_=att_win[:])
 
         ln_sums = stats.tile([P, NT], F32)
-        div_h = stats.tile([P, P], F32)
-        nc.gpsimd.memset(div_h[:], 0.0)
         div_sum = stats.tile([P, 1], F32)
         inv_div_total = stats.tile([P, 1], F32)
 
@@ -676,8 +679,6 @@ def tile_selfattention_pa_kernel(tc, x, q, k, out_0, out_1, out_2, out_3, out_4)
                 inverse_denominators(segments[0])
             if r == 5:
                 dep_factors(segments[0])
-                for c in range(4):
-                    diagonal(c, nc.gpsimd)
             if r == 6:
                 inverse_denominators(segments[1])
                 nc.vector.tensor_scalar_max(out=inv_total[:], in0=total_ps[:, 0:1], scalar1=EPS)
@@ -717,6 +718,8 @@ def tile_selfattention_pa_kernel(tc, x, q, k, out_0, out_1, out_2, out_3, out_4)
             if r == 5:
                 denominators(segments[1])
                 total_ps = total_over_tokens(abs_sum[:], psum_t, "t")
+                for c in range(segments[0].start, segments[0].stop):
+                    diagonal_on_scalar(c)
                 for w in range(3):
                     spread_dep_factor(w, segments[0])
             if r == 6:
@@ -728,7 +731,7 @@ def tile_selfattention_pa_kernel(tc, x, q, k, out_0, out_1, out_2, out_3, out_4)
                 denominators(segments[2])
                 finish_window(2)
                 for c in range(4, 7):
-                    diagonal(c, nc.vector)
+                    diagonal_on_vector(c)
                 for w in range(3, 6):
                     spread_dep_factor(w, slice(0, NT - 1))
                 inverse_denominators(segments[2])
@@ -742,7 +745,7 @@ def tile_selfattention_pa_kernel(tc, x, q, k, out_0, out_1, out_2, out_3, out_4)
         finish_window(3)
         dep_factor_of_last_tile()
         finish_window(4)
-        diagonal(7, nc.vector)
+        diagonal_on_vector(NT - 1)
         for w in range(6, NT):
             spread_dep_factor(w, slice(0, NT - 1))
         total_ps = total_over_tokens(div_sum[:], psum_mm, "bank0")

from contextlib import ExitStack

import concourse.mybir as mybir
from concourse.masks import make_identity

F32 = mybir.dt.float32
BF16 = mybir.dt.bfloat16
U32 = mybir.dt.uint32
U8 = mybir.dt.uint8
FP8X4 = mybir.dt.float8_e4m3fn_x4
ACT = mybir.ActivationFunctionType
ALU = mybir.AluOpType
AX = mybir.AxisListType

P = 128
T = 1024
FEAT = 1024
NT = T // P
K_PASS = 4 * P
PASSES = FEAT // K_PASS
BANK = 512
HALVES = T // BANK
BLOCK = 60
EPS = 1e-12
LN_T = 10 * 0.6931471805599453

WIN_STEP = 2 * BLOCK
WIN = T - WIN_STEP * (NT - 1)
WIN_BLOCKS = 4
PAD_LEFT = WIN_STEP
PAD_RIGHT = 64
ROW_SHIFT = P - WIN_STEP
LAST_BLOCK = T % BLOCK
HUGE = 2.0**100
GROUPS, BLOCK_GROUP, ZEROS_GROUP = HALVES + 2, HALVES, HALVES + 1

FLOPS = 2 * 2 * T * T * FEAT

COL_ENT_WIN, COL_ENT, COL_DEP = 0, NT, 2 * NT


def window_pieces(r):
    lo = WIN_STEP * r
    pieces = []
    for h in range(HALVES):
        first = max(lo, BANK * h)
        last = min(lo + WIN, BANK * (h + 1))
        if first < last:
            pieces.append((h, first - BANK * h, last - BANK * h, first - lo, last - lo))
    return pieces


def tile_selfattention_pa_kernel(tc, x, q, k, out_0, out_1, out_2, out_3, out_4):
    nc = tc.nc
    with ExitStack() as ctx:
        const = ctx.enter_context(tc.tile_pool(name="const", bufs=1))
        resident = ctx.enter_context(tc.tile_pool(name="resident", bufs=1))
        stats = ctx.enter_context(tc.tile_pool(name="stats", bufs=1))
        stage = ctx.enter_context(tc.tile_pool(name="stage", bufs=3))
        junk = ctx.enter_context(tc.tile_pool(name="junk", bufs=3))
        psum_t = ctx.enter_context(tc.psum_pool(name="psum_t", bufs=4))
        psum_mm = ctx.enter_context(tc.psum_pool(name="psum_mm", bufs=2))
        ctx.enter_context(tc.manual_schedule())

        k_sb = resident.tile([P, NT, FEAT], BF16)
        q_sb = resident.tile([P, NT, FEAT], BF16)
        x_sb = resident.tile([P, NT, FEAT], BF16)

        def load(dst, src, r):
            nc.sync.dma_start(out=dst[:, r, :], in_=src[P * r : P * (r + 1), :])

        load(k_sb, k, 0)
        load(k_sb, k, 1)
        load(x_sb, x, 0)
        load(k_sb, k, 2)
        load(k_sb, k, 3)
        load(q_sb, q, 0)
        load(k_sb, k, 4)
        load(k_sb, k, 5)
        load(q_sb, q, 1)
        load(k_sb, k, 6)
        load(k_sb, k, 7)
        load(x_sb, x, 1)
        load(x_sb, x, 2)
        load(q_sb, q, 2)
        load(x_sb, x, 3)
        load(q_sb, q, 3)
        load(x_sb, x, 4)
        load(q_sb, q, 4)
        load(x_sb, x, 5)
        load(q_sb, q, 5)
        load(x_sb, x, 6)
        load(q_sb, q, 6)
        load(x_sb, x, 7)
        load(q_sb, q, 7)

        ident_f32 = const.tile([P, P], F32)
        make_identity(nc, ident_f32[:])
        inside = const.tile([P, NT, WIN_BLOCKS], F32)
        nc.gpsimd.memset(inside[:], 0.0)
        nc.gpsimd.affine_select(
            out=inside[:], in_=inside[:], compare_op=ALU.is_ge, fill=-HUGE,
            base=0, channel_multiplier=1, pattern=[[ROW_SHIFT, NT], [-BLOCK, WIN_BLOCKS]],
        )
        nc.gpsimd.affine_select(
            out=inside[:], in_=inside[:], compare_op=ALU.is_ge, fill=-HUGE,
            base=BLOCK - 1, channel_multiplier=-1, pattern=[[-ROW_SHIFT, NT], [BLOCK, WIN_BLOCKS]],
        )
        outside4 = const.tile([P, NT, WIN_BLOCKS, BLOCK], F32)
        nc.scalar.copy(
            out=outside4[:], in_=inside[:].unsqueeze(3).to_broadcast([P, NT, WIN_BLOCKS, BLOCK])
        )
        outside = outside4[:].rearrange("p r b c -> p r (b c)")
        keep_wide = const.tile([P, NT, PAD_LEFT + WIN_BLOCKS * BLOCK + PAD_RIGHT], F32)
        nc.vector.memset(keep_wide[:, :, 0:PAD_LEFT], 0.0)
        nc.vector.memset(keep_wide[:, :, PAD_LEFT + WIN_BLOCKS * BLOCK :], 0.0)
        keep = keep_wide[:, :, PAD_LEFT : PAD_LEFT + WIN_BLOCKS * BLOCK]
        minus_half = const.tile([P, 1], F32)
        nc.vector.memset(minus_half[:], -0.5)
        denom_parts = stats.tile([P, 5, NT], F32)
        nc.vector.memset(denom_parts[:], 0.0)
        nc.vector.memset(denom_parts[:, 4, :], float(T))
        weighted_sums = stats.tile([P, HALVES, NT], F32)
        vectors = stats.tile([P, P], F32)
        nc.vector.memset(vectors[:], 0.0)
        div_h = stats.tile([P, P], F32)
        nc.vector.memset(div_h[:], 0.0)
        zeros = const.tile([P, T - WIN], F32)
        nc.vector.memset(zeros[:], 0.0)
        ones = const.tile([P, P], F32)
        nc.vector.memset(ones[:], 1.0)
        neg_max = stats.tile([P, 1 + HALVES, NT], F32)
        inside_by_column = inside[:].unsqueeze(3).to_broadcast([P, NT, WIN_BLOCKS, BLOCK])
        nc.vector.tensor_scalar(
            out=keep.rearrange("p r (b c) -> p r b c", b=WIN_BLOCKS), in0=inside_by_column,
            scalar1=1.0 / HUGE, scalar2=1.0, op0=ALU.mult, op1=ALU.add,
        )
        z = stats.tile([P, GROUPS, NT], F32)
        s = stats.tile([P, GROUPS, NT], F32)
        nc.gpsimd.memset(s[:, ZEROS_GROUP, :], 0.0)
        nc.gpsimd.memset(z[:, ZEROS_GROUP, :], float(T - BLOCK))
        nc.gpsimd.affine_select(
            out=z[:, ZEROS_GROUP, :], in_=z[:, ZEROS_GROUP, :], compare_op=ALU.is_ge,
            fill=float(T - LAST_BLOCK), base=T - LAST_BLOCK - 1, channel_multiplier=-1,
            pattern=[[-P, NT]],
        )

        for r in range(NT):
            rows = slice(P * r, P * (r + 1))
            lo = WIN_STEP * r
            if lo > 0:
                nc.sync.dma_start(out=out_0[rows, 0:lo], in_=zeros[:, 0:lo])
            if lo + WIN < T:
                nc.sync.dma_start(out=out_0[rows, lo + WIN : T], in_=zeros[:, 0 : T - WIN - lo])

        k_codes = resident.tile([P, PASSES, T], U32, align_bytes=64)
        k_scales = resident.tile([P, PASSES, T], U8, align_bytes=64)
        q_codes = resident.tile([P, NT, PASSES * P], U32, align_bytes=64)
        q_scales = resident.tile([P, NT, PASSES * P], U8, align_bytes=64)
        u_codes = resident.tile([P, PASSES, T], U32, align_bytes=64)
        u_scales = resident.tile([P, PASSES, T], U8, align_bytes=64)

        def quantise_tile(grouped, codes, scales, r):
            cols = slice(P * r, P * (r + 1))
            for g in range(PASSES):
                nc.vector.quantize_mx(
                    out=codes[:, g, cols].bitcast(FP8X4),
                    scales=scales[:, g, cols],
                    in_=grouped[:, K_PASS * g : K_PASS * (g + 1)],
                )

        def quantise_q_tile(grouped, r):
            nc.vector.quantize_mx(
                out=q_codes[:, r, :].bitcast(FP8X4), scales=q_scales[:, r, :], in_=grouped[:]
            )

        def transpose_words(words):
            planes = psum_t.tile([P, 2 * PASSES, P], F32, name="planes", tag="t")
            for w in range(2 * PASSES):
                nc.tensor.transpose(planes[:, w, :], words[:, P * w : P * (w + 1)], ident_f32[:])
            return planes

        def regroup(planes, copy):
            grouped = stage.tile([P, PASSES * K_PASS], BF16, align_bytes=64, tag="grouped", bufs=6)
            copy(
                out=grouped[:].bitcast(F32).rearrange("p (g c v) -> p g c v", g=PASSES, v=2),
                in_=planes[:].rearrange("p (g v) c -> p g c v", v=2),
            )
            return grouped

        def transpose_q(r):
            return transpose_words(q_sb[:].bitcast(F32)[:, r, :])

        def transpose_u(u_tile):
            return transpose_words(u_tile[:].bitcast(F32))

        u_tiles = {}
        sum_sq = stats.tile([P, NT], F32)
        inv_norms = {}

        def sum_squares(r):
            squares = junk.tile([P, FEAT], BF16, tag="squares")
            nc.scalar.activation(
                out=squares[:], in_=x_sb[:, r, :], func=ACT.Square, accum_out=sum_sq[:, r : r + 1]
            )

        def inverse_norm(r, engine):
            limited = stage.tile([P, 1], F32, name="limited", tag="limited")
            engine.tensor_scalar_max(out=limited[:], in0=sum_sq[:, r : r + 1], scalar1=EPS * EPS)
            inv_norms[r] = stage.tile([P, 1], F32, name="inv_norm", tag="inv_norm")
            nc.gpsimd.tensor_tensor(
                out=inv_norms[r][:], in0=limited[:], in1=minus_half[:], op=ALU.pow
            )

        def scale_x(r):
            u_tiles[r] = stage.tile([P, FEAT], BF16, name="u_tile", tag="u_tile")
            nc.vector.tensor_scalar_mul(
                out=u_tiles[r][:], in0=x_sb[:, r, :], scalar1=inv_norms[r][:]
            )

        banks = {}

        def product(j, h):
            bank = psum_mm.tile([P, BANK], F32, name="bank%d" % h, tag="bank%d" % h)
            cols = slice(BANK * h, BANK * (h + 1))
            for g in range(PASSES):
                if j < NT:
                    rows = slice(P * g, P * (g + 1))
                    lhs, lhs_scale = q_codes[:, j, rows], q_scales[:, j, rows]
                    rhs, rhs_scale = k_codes[:, g, cols], k_scales[:, g, cols]
                else:
                    rows = slice(P * (j - NT), P * (j - NT + 1))
                    lhs, lhs_scale = u_codes[:, g, rows], u_scales[:, g, rows]
                    rhs, rhs_scale = u_codes[:, g, cols], u_scales[:, g, cols]
                nc.tensor.matmul_mx(
                    out=bank[:], lhsT=lhs.bitcast(FP8X4), lhsT_scale=lhs_scale,
                    rhs=rhs.bitcast(FP8X4), rhs_scale=rhs_scale,
                    start=(g == 0), stop=(g == PASSES - 1),
                )
            banks[j, h] = bank

        accs = {}
        FIRST_BLOCKS = [NT // 2 + r // 2 for r in range(NT)]

        def gram_row_sums(r, part):
            rows = slice(P * r, P * (r + 1))
            acc = psum_t.tile([P, P], F32, name="acc", tag="t")
            first_blocks = FIRST_BLOCKS[r]
            blocks = range(first_blocks, NT) if part else range(first_blocks)
            order = [(g, c) for g in range(PASSES) for c in blocks]
            for i, (g, c) in enumerate(order):
                cols = slice(P * c, P * (c + 1))
                nc.tensor.matmul_mx(
                    out=acc[:],
                    lhsT=u_codes[:, g, rows].bitcast(FP8X4),
                    lhsT_scale=u_scales[:, g, rows],
                    rhs=u_codes[:, g, cols].bitcast(FP8X4),
                    rhs_scale=u_scales[:, g, cols],
                    start=(i == 0), stop=(i == len(order) - 1),
                )
            accs[r, part] = acc

        def finish_row_sums(r, part):
            copied = junk.tile([P, P], F32, tag="copied")
            nc.scalar.activation(
                out=copied[:], in_=accs[r, part][:], func=ACT.Copy, scale=-1.0,
                accum_out=denom_parts[:, 2 + part, r : r + 1],
            )

        e_all = resident.tile([P, NT, T], F32)
        e_win = resident.tile([P, NT, WIN], F32)
        logits = {}

        def half_maximum(r, h):
            nc.vector.tensor_reduce(
                out=neg_max[:, 1 + h, r : r + 1], in_=banks[r, h][:], axis=AX.X, op=ALU.max,
                negate=True,
            )

        def window_logits(r, h):
            for piece_h, first, last, w_first, w_last in window_pieces(r):
                if piece_h == h:
                    if r not in logits:
                        logits[r] = resident.tile([P, WIN], F32, name="logits%d" % r)
                    nc.vector.tensor_tensor(
                        out=logits[r][:, w_first:w_last], in0=banks[r, h][:, first:last],
                        in1=outside[:, r, w_first:w_last], op=ALU.add,
                    )

        def window_maximum(r):
            nc.vector.tensor_reduce(
                out=neg_max[:, 0, r : r + 1], in_=logits[r][:], axis=AX.X, op=ALU.max, negate=True
            )

        def exponentials(r, h):
            nc.scalar.activation(
                out=e_all[:, r, BANK * h : BANK * (h + 1)], in_=banks[r, h][:], func=ACT.Exp,
                bias=neg_max[:, 1 + h, r : r + 1], accum_out=z[:, h, r : r + 1],
            )

        def window_exponentials(r):
            nc.scalar.activation(
                out=e_win[:, r, :], in_=logits[r][:], func=ACT.Exp, bias=neg_max[:, 0, r : r + 1],
                accum_out=z[:, BLOCK_GROUP, r : r + 1],
            )

        def entropy_sum(r, h):
            products = junk.tile([P, BANK], F32, tag="products")
            nc.vector.scalar_tensor_tensor(
                out=products[:], in0=banks[r, h][:], scalar=neg_max[:, 1 + h, r : r + 1],
                in1=e_all[:, r, BANK * h : BANK * (h + 1)],
                op0=ALU.add, op1=ALU.mult, accum_out=s[:, h, r : r + 1],
            )

        def window_entropy_sum(r):
            products = junk.tile([P, WIN], F32, tag="win_products")
            nc.vector.scalar_tensor_tensor(
                out=products[:], in0=logits[r][:], scalar=neg_max[:, 0, r : r + 1],
                in1=e_win[:, r, :], op0=ALU.add, op1=ALU.mult, accum_out=s[:, BLOCK_GROUP, r : r + 1],
            )

        def clear_blocks(r):
            zero_first = 0 if r >= NT // 2 else T - BLOCK
            for block in range(P * r // BLOCK, (P * (r + 1) - 1) // BLOCK + 1):
                first, last = BLOCK * block, min(BLOCK * (block + 1), T)
                row_first, row_last = max(first, P * r), min(last, P * (r + 1))
                nc.sync.dma_start(
                    out=e_all[row_first - P * r : row_last - P * r, r, first:last],
                    in_=out_0[row_first:row_last, zero_first : zero_first + last - first],
                )

        k_words = k_sb[:].bitcast(F32)
        k_grouped, q_planes, u_planes, q_grouped, u_grouped = {}, {}, {}, {}, {}
        on_scalar, on_vector = nc.scalar.copy, nc.vector.tensor_copy

        def bring_k(r, copy):
            k_grouped[r] = regroup(transpose_words(k_words[:, r, :]), copy)

        def quantise_k(r):
            quantise_tile(k_grouped[r], k_codes, k_scales, r)

        def bring_q(r, copy):
            q_planes[r] = transpose_q(r)
            q_grouped[r] = regroup(q_planes[r], copy)

        k_planes = {}
        k_planes[0] = transpose_words(k_words[:, 0, :])
        k_planes[1] = transpose_words(k_words[:, 1, :])
        k_grouped[0] = regroup(k_planes[0], on_vector)
        k_grouped[1] = regroup(k_planes[1], on_scalar)
        sum_squares(0)
        k_planes[2] = transpose_words(k_words[:, 2, :])
        quantise_k(0)
        quantise_k(1)
        k_grouped[2] = regroup(k_planes[2], on_vector)
        k_planes[3] = transpose_words(k_words[:, 3, :])
        k_grouped[3] = regroup(k_planes[3], on_scalar)
        q_planes[0] = transpose_q(0)
        q_grouped[0] = regroup(q_planes[0], on_scalar)
        inverse_norm(0, nc.gpsimd)
        quantise_k(2)
        quantise_k(3)
        k_planes[4] = transpose_words(k_words[:, 4, :])
        quantise_q_tile(q_grouped[0], 0)
        k_grouped[4] = regroup(k_planes[4], on_vector)
        k_planes[5] = transpose_words(k_words[:, 5, :])
        k_grouped[5] = regroup(k_planes[5], on_scalar)
        q_planes[1] = transpose_q(1)
        q_grouped[1] = regroup(q_planes[1], on_scalar)
        scale_x(0)
        k_planes[6] = transpose_words(k_words[:, 6, :])
        product(0, 0)
        quantise_k(4)
        quantise_q_tile(q_grouped[1], 1)
        quantise_k(5)
        k_grouped[6] = regroup(k_planes[6], on_scalar)
        k_planes[7] = transpose_words(k_words[:, 7, :])
        sum_squares(1)
        k_grouped[7] = regroup(k_planes[7], on_scalar)
        u_planes[0] = transpose_u(u_tiles[0])
        u_grouped[0] = regroup(u_planes[0], on_scalar)
        half_maximum(0, 0)
        window_logits(0, 0)
        product(1, 0)
        exponentials(0, 0)
        inverse_norm(1, nc.gpsimd)
        quantise_k(6)
        quantise_k(7)
        q_planes[2] = transpose_q(2)
        q_grouped[2] = regroup(q_planes[2], on_scalar)
        product(0, 1)
        half_maximum(1, 0)
        window_logits(1, 0)
        exponentials(1, 0)
        sum_squares(2)
        product(1, 1)
        entropy_sum(0, 0)
        quantise_tile(u_grouped[0], u_codes, u_scales, 0)
        quantise_q_tile(q_grouped[2], 2)
        inverse_norm(2, nc.gpsimd)
        product(2, 0)
        half_maximum(0, 1)
        window_logits(0, 1)
        exponentials(0, 1)
        window_maximum(0)
        scale_x(1)
        u_planes[1] = transpose_u(u_tiles[1])
        q_planes[3] = transpose_q(3)

        diffs = stats.tile([P, 1 + GROUPS, NT], F32)
        exps = stats.tile([P, 1 + GROUPS, NT], F32)
        neg_row_max = stats.tile([P, NT], F32)
        z_groups = stats.tile([P, GROUPS, NT], F32)
        z_both = stats.tile([P, 2, NT], F32)
        inv_z_both = stats.tile([P, 2, NT], F32)
        s_groups = stats.tile([P, GROUPS, NT], F32)
        s_both = stats.tile([P, 2, NT], F32)
        ln_z_both = stats.tile([P, 2, NT], F32)
        half_factor = stats.tile([P, HALVES, NT], F32)
        win_factor = stats.tile([P, NT], F32)
        neg_win_factor = stats.tile([P, NT], F32)

        def spread(column, n):
            return column.unsqueeze(1).to_broadcast([P, n, NT])

        def row_maxima():
            nc.vector.tensor_tensor(
                out=neg_row_max[:], in0=neg_max[:, 1, :], in1=neg_max[:, 2, :], op=ALU.min
            )
            nc.vector.tensor_scalar_min(out=diffs[:, 4, :], in0=neg_max[:, 0, :], scalar1=0.0)

        def maximum_differences():
            nc.vector.tensor_sub(
                out=diffs[:, 0:3, :], in0=spread(neg_row_max[:], 3), in1=neg_max[:]
            )
            nc.vector.tensor_sub(out=diffs[:, 3, :], in0=diffs[:, 4, :], in1=neg_max[:, 0, :])
            nc.scalar.activation(out=exps[:], in_=diffs[:], func=ACT.Exp)

        def by_softmax(groups):
            return groups.rearrange("p (m i) r -> p m i r", i=2)

        def scale_normalisers():
            nc.vector.tensor_mul(out=z_groups[:], in0=z[:], in1=exps[:, 1:, :])

        def add_normalisers():
            parts = by_softmax(z_groups[:])
            nc.vector.tensor_add(out=z_both[:], in0=parts[:, :, 0, :], in1=parts[:, :, 1, :])

        def inverse_normalisers():
            nc.vector.reciprocal(out=inv_z_both[:], in_=z_both[:])

        def attention_factors():
            nc.vector.scalar_tensor_tensor(
                out=half_factor[:], in0=exps[:, 1:3, :], scalar=-1.0,
                in1=spread(inv_z_both[:, 0, :], HALVES), op0=ALU.mult, op1=ALU.mult,
            )
            nc.vector.scalar_tensor_tensor(
                out=neg_win_factor[:], in0=exps[:, 0, :], scalar=-1.0,
                in1=inv_z_both[:, 0, :], op0=ALU.mult, op1=ALU.mult,
            )

        WINDOW_STEPS = {4: (0, 1, 2), 5: (3, 4), 6: (5, 6, 7)}

        EARLY_SUMS = {3: (0, 1), 4: (2, 3), 5: (4, 5), 6: (6, 7)}

        for r in range(NT):
            if r + 3 < NT:
                q_grouped[r + 3] = regroup(q_planes[r + 3], on_scalar)
            if r + 1 < NT:
                u_grouped[r + 1] = regroup(u_planes[r + 1], on_scalar)
            for h in range(HALVES):
                if r + 1 < NT and (r, h) != (0, 0):
                    half_maximum(r + 1, h)
                    window_logits(r + 1, h)
                    exponentials(r + 1, h)
                if (r, h) != (0, 0):
                    entropy_sum(r, h)
                    if (r, h) == (NT - 1, 1):
                        scale_normalisers()
                    if r + 2 < NT:
                        product(r + 2, h)
            if r + 3 < NT:
                sum_squares(r + 3)
                inverse_norm(r + 3, nc.gpsimd)
                clear_blocks(r)
            if r + 1 < NT:
                window_maximum(r + 1)
            if r + 3 < NT:
                quantise_q_tile(q_grouped[r + 3], r + 3)
            if r + 1 < NT:
                quantise_tile(u_grouped[r + 1], u_codes, u_scales, r + 1)
            if r + 2 >= NT:
                for h in range(HALVES):
                    product(r + 2, h)
            for i in EARLY_SUMS.get(r, ()):
                gram_row_sums(i, 0)
            for i in WINDOW_STEPS.get(r, ()):
                window_exponentials(i)
            if r == NT - 1:
                add_normalisers()
                window_entropy_sum(0)
                inverse_normalisers()
                window_entropy_sum(1)
            if r < NT - 2:
                for i in EARLY_SUMS.get(r, ()):
                    finish_row_sums(i, 0)
            if r + 4 < NT:
                q_planes[r + 4] = transpose_q(r + 4)
            if r + 2 < NT:
                scale_x(r + 2)
                u_planes[r + 2] = transpose_u(u_tiles[r + 2])
            if r == NT - 2:
                row_maxima()
                maximum_differences()

        LATE_SUMS = {0: (0, 1), 1: (2, 3), 2: (4, 5, 6, 7)}
        READ_SUMS = {0: ((6, 0), (7, 0)), 1: ((0, 1), (1, 1)), 2: ((2, 1), (3, 1)), 3: ((4, 1), (5, 1), (6, 1), (7, 1))}

        ln_parts = stats.tile([P, NT, HALVES + 1], F32)

        def logs_of_rest(r):
            for h in range(HALVES):
                logs = junk.tile([P, BANK], F32, tag="logs")
                nc.scalar.activation(
                    out=logs[:], in_=e_all[:, r, BANK * h : BANK * (h + 1)], func=ACT.Ln,
                    scale=half_factor[:, h, r : r + 1], bias=1.0, accum_out=ln_parts[:, r, h : h + 1],
                )
            win_logs = junk.tile([P, WIN], F32, tag="win_logs")
            nc.scalar.activation(
                out=win_logs[:], in_=e_win[:, r, :], func=ACT.Ln, scale=neg_win_factor[:, r : r + 1],
                bias=1.0, accum_out=ln_parts[:, r, HALVES : HALVES + 1],
            )

        def window_diversity(r):
            for i, (h, first, last, w_first, w_last) in enumerate(window_pieces(r)):
                products = junk.tile([P, WIN], F32, tag="win_products")
                nc.vector.scalar_tensor_tensor(
                    out=products[:, w_first:w_last], in0=banks[NT + r, h][:, first:last], scalar=-1.0,
                    in1=keep[:, r, w_first:w_last], op0=ALU.add, op1=ALU.mult,
                    accum_out=denom_parts[:, i, r : r + 1],
                )

        def weighted_diversity(r, h):
            products = junk.tile([P, BANK], F32, tag="products")
            nc.vector.scalar_tensor_tensor(
                out=products[:], in0=banks[NT + r, h][:], scalar=-1.0,
                in1=e_all[:, r, BANK * h : BANK * (h + 1)],
                op0=ALU.add, op1=ALU.mult, accum_out=weighted_sums[:, h, r : r + 1],
            )

        def total_over_tokens(partial, pool, tag):
            total_ps = pool.tile([P, BANK], F32, name="total_ps", tag=tag)
            nc.tensor.matmul(out=total_ps[:, 0:1], lhsT=ones[:], rhs=partial, start=True, stop=True)
            return total_ps

        entropy_both = stats.tile([P, 2, NT], F32)
        entropy = stats.tile([P, NT], F32)
        abs_entropy = stats.tile([P, NT], F32)
        abs_sum = stats.tile([P, 1], F32)
        inv_total = stats.tile([P, 1], F32)

        def shifted_sums():
            nc.gpsimd.tensor_mul(out=s_groups[:], in0=s[:], in1=exps[:, 1:, :])
            nc.gpsimd.tensor_mul(out=z_groups[:], in0=z_groups[:], in1=diffs[:, 1:, :])
            nc.gpsimd.tensor_add(out=s_groups[:], in0=s_groups[:], in1=z_groups[:])
            parts = by_softmax(s_groups[:])
            nc.gpsimd.tensor_add(out=s_both[:], in0=parts[:, :, 0, :], in1=parts[:, :, 1, :])

        def entropies():
            nc.gpsimd.tensor_mul(out=entropy_both[:], in0=s_both[:], in1=inv_z_both[:])
            nc.gpsimd.tensor_sub(out=entropy_both[:], in0=ln_z_both[:], in1=entropy_both[:])
            for out, plane in ((entropy[:], 0), (vectors[:, COL_ENT_WIN : COL_ENT_WIN + NT], 1)):
                nc.gpsimd.tensor_scalar(
                    out=out, in0=entropy_both[:, plane, :], scalar1=1.0 / LN_T, scalar2=0.0,
                    op0=ALU.mult, op1=ALU.add,
                )
            nc.scalar.activation(
                out=abs_entropy[:], in_=entropy[:], func=ACT.Abs, accum_out=abs_sum[:]
            )

        denom = stats.tile([P, NT], F32)
        dep_coef = stats.tile([P, HALVES, NT], F32)
        dep_parts = stats.tile([P, HALVES, NT], F32)
        segments = [slice(0, 4), slice(4, 7), slice(7, 8)]

        def denominators(tiles):
            nc.vector.tensor_reduce(
                out=denom[:, tiles], in_=denom_parts[:, :, tiles].rearrange("p i r -> p r i"),
                axis=AX.X, op=ALU.add,
            )

        def inverse_denominators(tiles):
            nc.vector.reciprocal(out=denom[:, tiles], in_=denom[:, tiles])

        def dep_coefficients(tiles):
            n = tiles.stop - tiles.start
            nc.vector.tensor_mul(
                out=dep_coef[:, :, tiles], in0=half_factor[:, :, tiles],
                in1=denom[:, tiles].unsqueeze(1).to_broadcast([P, HALVES, n]),
            )

        def weighted_parts(tiles):
            nc.vector.tensor_mul(
                out=dep_parts[:, :, tiles], in0=weighted_sums[:, :, tiles], in1=dep_coef[:, :, tiles]
            )

        def dep_factors(tiles):
            nc.vector.tensor_add(
                out=vectors[:, COL_DEP + tiles.start : COL_DEP + tiles.stop],
                in0=dep_parts[:, 0, tiles], in1=dep_parts[:, 1, tiles],
            )

        last_part = stats.tile([P, 1], F32)

        def first_part_of_last_tile():
            nc.vector.tensor_scalar_mul(
                out=last_part[:], in0=weighted_sums[:, 0, NT - 1 : NT],
                scalar1=dep_coef[:, 0, NT - 1 : NT],
            )

        def dep_factor_of_last_tile():
            nc.vector.tensor_scalar(
                out=vectors[:, COL_DEP + NT - 1 : COL_DEP + NT], in0=weighted_sums[:, 1, NT - 1 : NT],
                scalar1=dep_coef[:, 1, NT - 1 : NT], scalar2=last_part[:], op0=ALU.mult, op1=ALU.add,
            )

        diagonals, dep_windows = {}, {}

        def diagonal_on_scalar(c):
            diagonals[c] = stage.tile([P, P], F32, name="diagonal", tag="diagonal", bufs=NT)
            nc.scalar.activation(
                out=diagonals[c][:], in_=ident_f32[:], func=ACT.Copy,
                scale=vectors[:, COL_DEP + c : COL_DEP + c + 1],
            )

        def diagonal_on_vector(c):
            diagonals[c] = stage.tile([P, P], F32, name="diagonal", tag="diagonal", bufs=NT)
            nc.vector.tensor_scalar_mul(
                out=diagonals[c][:], in0=ident_f32[:], scalar1=vectors[:, COL_DEP + c : COL_DEP + c + 1]
            )

        def spread_dep_factor(r, tiles):
            lo = WIN_STEP * r
            if r not in dep_windows:
                dep_windows[r] = psum_t.tile([P, WIN], F32, name="dep_window", tag="t")
            for c in range(max(r - 1, tiles.start), min(r + 2, tiles.stop)):
                first, last = max(lo, P * c), min(lo + WIN, P * (c + 1))
                rows = PAD_LEFT + P * r - WIN_STEP * c
                if first < last:
                    nc.tensor.matmul(
                        out=dep_windows[r][:, first - lo : last - lo],
                        lhsT=keep_wide[:, c, rows : rows + P],
                        rhs=diagonals[c][:, first - P * c : last - P * c], start=True, stop=True,
                    )

        def finish_window(r):
            lo = WIN_STEP * r
            att_win = stage.tile([P, WIN], F32, name="att_win", tag="att_win", bufs=NT)
            nc.vector.scalar_tensor_tensor(
                out=att_win[:], in0=e_win[:, r, :], scalar=win_factor[:, r : r + 1],
                in1=dep_windows[r][:], op0=ALU.mult, op1=ALU.add,
            )
            nc.sync.dma_start(out=out_0[P * r : P * (r + 1), lo : lo + WIN], in_=att_win[:])

        ln_sums = stats.tile([P, NT], F32)
        div_sum = stats.tile([P, 1], F32)
        inv_div_total = stats.tile([P, 1], F32)

        def by_token(vector):
            return vector.rearrange("(r p) -> r p", p=P)

        attention_factors()
        window_diversity(0)
        for r in range(NT - 3, NT):
            clear_blocks(r)
        for r in range(NT):
            weighted_diversity(r, 0)
            if r == 4:
                inverse_denominators(segments[0])
            if r == 5:
                dep_factors(segments[0])
            if r == 6:
                inverse_denominators(segments[1])
                nc.vector.tensor_scalar_max(out=inv_total[:], in0=total_ps[:, 0:1], scalar1=EPS)
            if r == 7:
                dep_coefficients(segments[2])
                nc.vector.tensor_scalar_mul(
                    out=vectors[:, COL_ENT : COL_ENT + NT], in0=entropy[:], scalar1=inv_total[:]
                )
            if r + 2 < NT:
                product(NT + r + 2, 0)
            if r == 0:
                window_diversity(1)
            weighted_diversity(r, 1)
            if r == 1:
                nc.vector.tensor_mul(out=win_factor[:], in0=exps[:, 0, :], in1=inv_z_both[:, 0, :])
            if r == 4:
                dep_coefficients(segments[0])
            if r < 3:
                for i in range(2):
                    window_entropy_sum(2 + 2 * r + i)
            if r + 2 < NT:
                product(NT + r + 2, 1)
            logs_of_rest(r)
            for i, part in READ_SUMS.get(r, ()):
                finish_row_sums(i, part)
            for i in LATE_SUMS.get(r, ()):
                gram_row_sums(i, 1)
            if 1 < r + 1 < NT:
                window_diversity(r + 1)
            if r == 3:
                denominators(segments[0])
                shifted_sums()
                nc.scalar.activation(out=ln_z_both[:], in_=z_both[:], func=ACT.Ln)
            if r == 4:
                weighted_parts(segments[0])
                entropies()
            if r == 5:
                denominators(segments[1])
                total_ps = total_over_tokens(abs_sum[:], psum_t, "t")
                for c in range(segments[0].start, segments[0].stop):
                    diagonal_on_scalar(c)
                for w in range(3):
                    spread_dep_factor(w, segments[0])
            if r == 6:
                dep_coefficients(segments[1])
                finish_window(0)
                weighted_parts(segments[1])
                finish_window(1)
                dep_factors(segments[1])
                denominators(segments[2])
                finish_window(2)
                for c in range(4, 7):
                    diagonal_on_vector(c)
                for w in range(3, 6):
                    spread_dep_factor(w, slice(0, NT - 1))
                inverse_denominators(segments[2])
                nc.vector.reciprocal(out=inv_total[:], in_=inv_total[:])
            if r == 7:
                nc.vector.tensor_reduce(out=ln_sums[:], in_=ln_parts[:], axis=AX.X, op=ALU.add)
        nc.scalar.activation(
            out=div_h[:, 0:NT], in_=ln_sums[:], func=ACT.Exp, accum_out=div_sum[:]
        )
        first_part_of_last_tile()
        finish_window(3)
        dep_factor_of_last_tile()
        finish_window(4)
        diagonal_on_vector(NT - 1)
        for w in range(6, NT):
            spread_dep_factor(w, slice(0, NT - 1))
        total_ps = total_over_tokens(div_sum[:], psum_mm, "bank0")
        div_t_ps = psum_mm.tile([P, BANK], F32, name="div_t_ps", tag="bank1")
        nc.tensor.transpose(div_t_ps[:, 0:P], div_h[:], ident_f32[:])
        for w in range(6, NT):
            spread_dep_factor(w, segments[2])
        vectors_t_ps = psum_mm.tile([P, BANK], F32, name="vectors_t_ps", tag="bank0")
        nc.tensor.transpose(vectors_t_ps[:, 0:P], vectors[:], ident_f32[:])
        finish_window(5)
        nc.vector.reciprocal(out=inv_div_total[:], in_=total_ps[:, 0:1])
        finish_window(6)
        div_t = stats.tile([P, P], F32)
        nc.vector.tensor_scalar_mul(out=div_t[:], in0=div_t_ps[:, 0:P], scalar1=inv_div_total[:])
        nc.sync.dma_start(out=by_token(out_2), in_=div_t[0:NT, :])
        finish_window(7)

        vectors_t = stats.tile([P, P], F32)
        nc.scalar.copy(out=vectors_t[:], in_=vectors_t_ps[:, 0:P])
        for out_vec, col in ((out_1, COL_ENT_WIN), (out_3, COL_ENT), (out_4, COL_DEP)):
            nc.sync.dma_start(out=by_token(out_vec), in_=vectors_t[col : col + NT, :])
